import numpy as np
import ml_dtypes


def mxq(x, axis, fmt="e4m3"):
    dtype, down = {"e4m3": (ml_dtypes.float8_e4m3fn, 7), "e5m2": (ml_dtypes.float8_e5m2, 14)}[fmt]
    v = np.moveaxis(np.asarray(x, np.float32).astype(ml_dtypes.bfloat16).astype(np.float64), axis, -1)
    blocks = v.reshape(v.shape[:-1] + (-1, 32))
    amax = np.abs(blocks).max(-1, keepdims=True)
    byte = np.maximum(np.where(amax > 0, np.frexp(amax)[1] - 1 + 127, 0) - down, 1)
    scale = np.exp2(byte - 127.0)
    codes = (blocks / scale).astype(np.float32).astype(dtype).astype(np.float64)
    return np.moveaxis((codes * scale).reshape(v.shape), -1, axis)


WIDE = False


def mx_kscale(k):
    if not WIDE:
        return np.ones(k)
    levels = np.array([10, -10, 5, -5, 0])
    a = np.random.permutation(np.resize(levels, k // 512 * 4)).reshape(k // 512, 4)
    idx = np.arange(k)
    return np.exp2(a[idx // 512, idx % 128 // 32])


BF16 = ml_dtypes.bfloat16


def bf(x):
    return np.asarray(x, np.float32).astype(BF16)


def f64(x):
    return np.asarray(x).astype(np.float64)


B, S, DIM, H, NOPE, ROPE, VHD, KV_RANK = 2, 256, 2048, 16, 128, 64, 128, 512
QKHD = NOPE + ROPE
HALF = ROPE // 2
EPS = 1e-5


def rope(u, cos, sin):
    ur = u.reshape(u.shape[:-1] + (HALF, 2))
    a, b = ur[..., 0], ur[..., 1]
    c = cos[None, :, None, :]
    s = sin[None, :, None, :]
    return np.stack([a * c - b * s, a * s + b * c], axis=-1).reshape(u.shape)


def setup_inputs():
    s = mx_kscale(DIM)
    t = mx_kscale(KV_RANK)
    inv_freq = 1.0 / 10000.0 ** (np.arange(0, ROPE, 2) / ROPE)
    ang = np.arange(S)[:, None] * inv_freq[None, :]
    return {"x": bf(np.random.standard_normal((B, S, DIM)) * s),
            "wkv_a_w": bf(np.random.standard_normal((DIM, KV_RANK + H * ROPE)) / np.sqrt(DIM) / s[:, None]),
            "wkv_a_b": bf(np.random.standard_normal(KV_RANK + H * ROPE) * 0.2),
            "kvn_g": bf((1.0 + 0.1 * np.random.standard_normal(KV_RANK)) * t),
            "kvn_b": bf(0.1 * np.random.standard_normal(KV_RANK) * t),
            "wk_w": bf(np.random.standard_normal((KV_RANK, H * NOPE)) / np.sqrt(KV_RANK) / t[:, None]),
            "wk_b": bf(np.random.standard_normal(H * NOPE) * 0.2),
            "wv_w": bf(np.random.standard_normal((KV_RANK, H * VHD)) / np.sqrt(KV_RANK) / t[:, None]),
            "wv_b": bf(np.random.standard_normal(H * VHD) * 0.2),
            "cos": bf(np.cos(ang)), "sin": bf(np.sin(ang))}


def reference(x, wkv_a_w, wkv_a_b, kvn_g, kvn_b, wk_w, wk_b, wv_w, wv_b, cos, sin):
    kv = (mxq(f64(x), 2, "e4m3") @ mxq(f64(wkv_a_w), 0, "e4m3")) + f64(wkv_a_b)
    k_rope = kv[..., : H * ROPE]
    c = kv[..., H * ROPE:]
    mu = c.mean(-1, keepdims=True)
    var = np.square(c - mu).mean(-1, keepdims=True)
    c = (c - mu) / np.sqrt(var + EPS) * f64(kvn_g) + f64(kvn_b)
    cq = mxq(c, 2, "e4m3")
    k_nope = (cq @ mxq(f64(wk_w), 0, "e4m3")) + f64(wk_b)
    v = (cq @ mxq(f64(wv_w), 0, "e4m3")) + f64(wv_b)
    k = np.concatenate([k_nope, k_rope], axis=-1).reshape(B, S, H, QKHD)
    k = np.concatenate([k[..., :NOPE], rope(k[..., NOPE:], f64(cos), f64(sin))], axis=-1)
    return k, v.reshape(B, S, H, VHD)

@@ -1,0 +1,325 @@
+from contextlib import ExitStack
+
+import concourse.mybir as mybir
+from concourse.masks import make_identity
+
+F32 = mybir.dt.float32
+BF16 = mybir.dt.bfloat16
+U32 = mybir.dt.uint32
+U8 = mybir.dt.uint8
+FP8X4 = mybir.dt.float8_e4m3fn_x4
+ALU = mybir.AluOpType
+ACT = mybir.ActivationFunctionType
+
+P = 128
+PACK = 4
+K_PASS = P * PACK
+BATCH, SEQ, DIM, HEADS, NOPE, ROPE, RANK = 2, 256, 2048, 16, 128, 64, 512
+HEAD = NOPE + ROPE
+TOKENS = BATCH * SEQ
+TOKEN_TILES = TOKENS // P
+SEQ_TILES = SEQ // P
+PASSES = DIM // K_PASS
+UNIT = 512
+ROPE_COLS = HEADS * ROPE
+NOPE_COLS = HEADS * NOPE
+EPS = 1e-5
+FLOPS = 2 * TOKENS * DIM * (ROPE_COLS + RANK) + 2 * 2 * TOKENS * RANK * NOPE_COLS
+
+ROW_LATENT_BIAS, ROW_GAIN, ROW_SHIFT, ROW_ROPE_BIAS, ROW_WK_BIAS, ROW_WV_BIAS, ROWS = 0, 1, 2, 3, 5, 9, 14
+
+
+def copy(nc, on_vector, out, in_):
+    if on_vector:
+        nc.vector.tensor_copy(out=out, in_=in_)
+    else:
+        nc.scalar.copy(out=out, in_=in_)
+
+
+def quantise_piece(nc, stage, on_vector, rows, codes, scales):
+    grouped = stage.tile([P, UNIT * PACK], BF16, align_bytes=64, tag="grouped")
+    copy(
+        nc,
+        on_vector,
+        grouped[:].rearrange("p (c i t) -> p c t i", i=4, t=PACK),
+        rows.rearrange("p t (c i) -> p c t i", i=4),
+    )
+    nc.vector.quantize_mx(out=codes.bitcast(FP8X4), scales=scales, in_=grouped[:])
+
+
+def rotate(nc, eng, scratch, unit_out, first_block, cos_pair, sin_minus, sin_plus):
+    blocks = unit_out.rearrange("p t (k d) -> p t k d", d=ROPE)[:, :, first_block::3, :]
+    n = blocks.shape[2]
+    pairs = blocks.rearrange("p t n (j e) -> p t n j e", e=2)
+    half = [P, TOKEN_TILES, n, ROPE // 2]
+    crossed = scratch.tile([P, 2, TOKEN_TILES, n, ROPE // 2], F32, tag="crossed")
+    eng.tensor_tensor(
+        out=crossed[:, 0], in0=pairs[:, :, :, :, 1], in1=sin_minus.unsqueeze(2).to_broadcast(half), op=ALU.mult
+    )
+    eng.tensor_tensor(
+        out=crossed[:, 1], in0=pairs[:, :, :, :, 0], in1=sin_plus.unsqueeze(2).to_broadcast(half), op=ALU.mult
+    )
+    eng.tensor_tensor(
+        out=blocks, in0=blocks, in1=cos_pair.unsqueeze(2).to_broadcast([P, TOKEN_TILES, n, ROPE]), op=ALU.mult
+    )
+    eng.tensor_tensor(out=pairs, in0=pairs, in1=crossed[:].rearrange("p e t n j -> p t n j e"), op=ALU.add)
+
+
+def tile_mla_pa_kernel(
+    tc, x, wkv_a_w, wkv_a_b, kvn_g, kvn_b, wk_w, wk_b, wv_w, wv_b, cos, sin, out_0, out_1
+):
+    nc = tc.nc
+    x_rows = x.flatten_outer_dims()
+    k_flat = out_0.rearrange("b s h d -> (b s) (h d)")
+    v_flat = out_1.rearrange("b s h d -> (b s) (h d)")
+
+    with ExitStack() as ctx:
+        const = ctx.enter_context(tc.tile_pool(name="const", bufs=1))
+        raw = ctx.enter_context(tc.tile_pool(name="raw", bufs=1))
+        keep = ctx.enter_context(tc.tile_pool(name="keep", bufs=1))
+        x_stage = ctx.enter_context(tc.tile_pool(name="x_stage", bufs=3))
+        stage = ctx.enter_context(tc.tile_pool(name="stage", bufs=4))
+        a_pool = ctx.enter_context(tc.tile_pool(name="a_pool", bufs=2))
+        w_pool = ctx.enter_context(tc.tile_pool(name="w_pool", bufs=3))
+        norm = ctx.enter_context(tc.tile_pool(name="norm", bufs=2))
+        outs = ctx.enter_context(tc.tile_pool(name="outs", bufs=3))
+        scratch = ctx.enter_context(tc.tile_pool(name="scratch", bufs=2))
+        acc_pool = ctx.enter_context(tc.psum_pool(name="acc_pool", bufs=6))
+        turn_pool = ctx.enter_context(tc.psum_pool(name="turn_pool", bufs=2))
+
+        ident_f32 = const.tile([P, P], F32)
+        make_identity(nc, ident_f32[:])
+        ident_bf = const.tile([P, P], BF16)
+        make_identity(nc, ident_bf[:])
+        one = const.tile([P, 1], F32)
+        nc.vector.memset(one[:], 1.0)
+        nc.scalar.sqrt(out=one[:], in_=one[:])
+        vec_rows = const.tile([P, UNIT], BF16)
+        nc.vector.memset(vec_rows[:], 0.0)
+
+        x_sb = raw.tile([P, TOKEN_TILES, DIM], BF16)
+        for tt in range(TOKEN_TILES):
+            nc.sync.dma_start(out=x_sb[:, tt, :], in_=x_rows[tt * P : (tt + 1) * P, :])
+
+        def load_row(row, count, vector):
+            nc.sync.dma_start(out=vec_rows[row : row + count, :], in_=vector.rearrange("(r c) -> r c", c=UNIT))
+
+        def load_first_stage(tile_, col0, width):
+            for g in range(PASSES):
+                for u in range(2):
+                    row0 = g * K_PASS + u * 2 * P
+                    nc.sync.dma_start(
+                        out=tile_[:, g, 2 * u : 2 * u + 2, :],
+                        in_=wkv_a_w[row0 : row0 + 2 * P, col0 : col0 + width].rearrange("(q e) c -> q e c", e=2),
+                    )
+
+        def load_second_stage(tile_, weight):
+            view = weight.rearrange("(t p) n -> p t n", p=P)
+            for half in range(2):
+                cols = slice(half * NOPE_COLS // 2, (half + 1) * NOPE_COLS // 2)
+                nc.sync.dma_start(out=tile_[:, :, cols], in_=view[:, :, cols])
+
+        load_row(ROW_LATENT_BIAS, 1, wkv_a_b[ROPE_COLS:])
+        load_row(ROW_GAIN, 1, kvn_g)
+        load_row(ROW_SHIFT, 1, kvn_b)
+        raw_latent = raw.tile([P, PASSES, PACK, RANK], BF16)
+        load_first_stage(raw_latent, ROPE_COLS, RANK)
+        load_row(ROW_ROPE_BIAS, 2, wkv_a_b[:ROPE_COLS])
+        load_row(ROW_WK_BIAS, 4, wk_b)
+        load_row(ROW_WV_BIAS, 4, wv_b)
+        cos_sin = const.tile([P, 2, SEQ_TILES, ROPE // 2], BF16)
+        nc.sync.dma_start(out=cos_sin[:, 0], in_=cos.rearrange("(a p) j -> p a j", p=P))
+        nc.sync.dma_start(out=cos_sin[:, 1], in_=sin.rearrange("(a p) j -> p a j", p=P))
+        raw_rope = raw.tile([P, PASSES, PACK, ROPE_COLS], BF16)
+        load_first_stage(raw_rope, 0, ROPE_COLS)
+        raw_wk = raw.tile([P, PACK, NOPE_COLS], BF16)
+        load_second_stage(raw_wk, wk_w)
+        raw_wv = raw.tile([P, PACK, NOPE_COLS], BF16)
+        load_second_stage(raw_wv, wv_w)
+
+        x_codes = keep.tile([P, PASSES, TOKENS], U32, align_bytes=64)
+        x_scales = keep.tile([P, PASSES, TOKENS], U8, align_bytes=64)
+        for pair in range(TOKEN_TILES // 2):
+            for g in range(PASSES):
+                turned = turn_pool.tile([P, 2, 2, P], F32, tag="turn")
+                for i in range(2):
+                    words = x_sb[:, 2 * pair + i, :].bitcast(F32)
+                    for u in range(2):
+                        col0 = (2 * g + u) * P
+                        nc.tensor.transpose(turned[:, i, u, :], words[:, col0 : col0 + P], ident_f32[:])
+                x_grouped = x_stage.tile([P, 2 * P * PACK], BF16, align_bytes=64)
+                copy(
+                    nc,
+                    g % 2 == 1,
+                    x_grouped[:].bitcast(F32).rearrange("p (i k u) -> p i k u", i=2, u=2),
+                    turned[:].rearrange("p i u k -> p i k u"),
+                )
+                cols = slice(pair * 2 * P, (pair + 1) * 2 * P)
+                nc.vector.quantize_mx(
+                    out=x_codes[:, g, cols].bitcast(FP8X4), scales=x_scales[:, g, cols], in_=x_grouped[:]
+                )
+
+        spread = const.tile([P, ROWS, UNIT], BF16)
+        for r in range(0, ROWS, 2):
+            picked = turn_pool.tile([P, 2, UNIT], BF16, tag="turn")
+            for i in range(2):
+                nc.tensor.matmul(
+                    out=picked[:, i, :],
+                    lhsT=ident_bf[:, r + i : r + i + 1].to_broadcast([P, P]),
+                    rhs=vec_rows[:],
+                    start=True,
+                    stop=True,
+                )
+            copy(nc, r % 4 == 2, spread[:, r : r + 2, :], picked[:])
+
+        cos_pair = const.tile([P, TOKEN_TILES, ROPE], F32)
+        sin_plus = const.tile([P, TOKEN_TILES, ROPE // 2], F32)
+        sin_minus = const.tile([P, TOKEN_TILES, ROPE // 2], F32)
+        for b in range(BATCH):
+            tiles = slice(b * SEQ_TILES, (b + 1) * SEQ_TILES)
+            nc.vector.tensor_copy(
+                out=cos_pair[:, tiles, :].rearrange("p a (j e) -> p a j e", e=2),
+                in_=cos_sin[:, 0].unsqueeze(3).to_broadcast([P, SEQ_TILES, ROPE // 2, 2]),
+            )
+            nc.vector.tensor_copy(out=sin_plus[:, tiles, :], in_=cos_sin[:, 1])
+            nc.vector.tensor_scalar(
+                out=sin_minus[:, tiles, :], in0=cos_sin[:, 1], scalar1=-1.0, scalar2=None, op0=ALU.mult
+            )
+
+        def first_stage_unit(raw_tile, col0, vector_helps):
+            codes = a_pool.tile([P, PASSES, UNIT], U32, align_bytes=64, tag="a_codes")
+            scales = a_pool.tile([P, PASSES, UNIT], U8, align_bytes=64, tag="a_scales")
+            sums = [acc_pool.tile([P, UNIT], F32, tag="acc", name="sum%d" % tt) for tt in range(TOKEN_TILES)]
+            for g in range(PASSES):
+                quantise_piece(
+                    nc,
+                    stage,
+                    vector_helps and g % 2 == 1,
+                    raw_tile[:, g, :, col0 : col0 + UNIT],
+                    codes[:, g, :],
+                    scales[:, g, :],
+                )
+                for tt in range(TOKEN_TILES):
+                    tokens = slice(tt * P, (tt + 1) * P)
+                    nc.tensor.matmul_mx(
+                        out=sums[tt][:],
+                        lhsT=x_codes[:, g, tokens].bitcast(FP8X4),
+                        lhsT_scale=x_scales[:, g, tokens],
+                        rhs=codes[:, g, :].bitcast(FP8X4),
+                        rhs_scale=scales[:, g, :],
+                        start=(g == 0),
+                        stop=(g == PASSES - 1),
+                    )
+            return sums
+
+        def finish_k_unit(unit_out, flat_unit):
+            rotate(nc, nc.vector, scratch, unit_out[:], (2 - 8 * flat_unit) % 3, cos_pair[:], sin_minus[:], sin_plus[:])
+            cols = slice(flat_unit * UNIT, (flat_unit + 1) * UNIT)
+            nc.sync.dma_start(out=k_flat[:, cols].rearrange("(t p) c -> p t c", p=P), in_=unit_out[:])
+
+        latent_sums = first_stage_unit(raw_latent, 0, True)
+
+        c_all = keep.tile([P, TOKEN_TILES, RANK], F32)
+        c_sum = keep.tile([P, TOKEN_TILES], F32)
+        for tt in range(TOKEN_TILES):
+            nc.vector.scalar_tensor_tensor(
+                out=c_all[:, tt, :],
+                in0=latent_sums[tt][:],
+                scalar=1.0,
+                in1=spread[:, ROW_LATENT_BIAS, :],
+                op0=ALU.mult,
+                op1=ALU.add,
+                accum_out=c_sum[:, tt : tt + 1],
+            )
+        minus_mean = keep.tile([P, TOKEN_TILES], F32)
+        nc.vector.tensor_scalar(out=minus_mean[:], in0=c_sum[:], scalar1=-1.0 / RANK, scalar2=None, op0=ALU.mult)
+        square_sum = keep.tile([P, TOKEN_TILES], F32)
+        for tt in range(TOKEN_TILES):
+            squares = norm.tile([P, RANK], BF16, tag="squares")
+            nc.scalar.activation(
+                out=squares[:],
+                in_=c_all[:, tt, :],
+                func=ACT.Square,
+                bias=minus_mean[:, tt : tt + 1],
+                scale=1.0,
+                accum_out=square_sum[:, tt : tt + 1],
+            )
+        spread_of_c = keep.tile([P, TOKEN_TILES], F32)
+        nc.vector.tensor_scalar(
+            out=spread_of_c[:], in0=square_sum[:], scalar1=1.0 / RANK, scalar2=EPS, op0=ALU.mult, op1=ALU.add
+        )
+        nc.scalar.sqrt(out=spread_of_c[:], in_=spread_of_c[:])
+        inv_std = keep.tile([P, TOKEN_TILES], F32)
+        nc.vector.reciprocal(out=inv_std[:], in_=spread_of_c[:])
+
+        cn_codes = keep.tile([P, TOKENS], U32, align_bytes=64)
+        cn_scales = keep.tile([P, TOKENS], U8, align_bytes=64)
+        cn = keep.tile([P, TOKEN_TILES, RANK], BF16)
+        for tt in range(TOKEN_TILES):
+            gained = norm.tile([P, RANK], F32, tag="gained")
+            nc.vector.scalar_tensor_tensor(
+                out=gained[:],
+                in0=c_all[:, tt, :],
+                scalar=minus_mean[:, tt : tt + 1],
+                in1=spread[:, ROW_GAIN, :],
+                op0=ALU.add,
+                op1=ALU.mult,
+            )
+            nc.vector.scalar_tensor_tensor(
+                out=cn[:, tt, :],
+                in0=gained[:],
+                scalar=inv_std[:, tt : tt + 1],
+                in1=spread[:, ROW_SHIFT, :],
+                op0=ALU.mult,
+                op1=ALU.add,
+            )
+        for tt in range(TOKEN_TILES):
+            cn_turned = turn_pool.tile([P, PACK, P], BF16, tag="turn")
+            for t in range(PACK):
+                nc.tensor.transpose(cn_turned[:, t, :], cn[:, tt, t * P : (t + 1) * P], ident_bf[:])
+            cn_grouped = norm.tile([P, P * PACK], BF16, align_bytes=64, tag="cn_grouped")
+            nc.scalar.copy(
+                out=cn_grouped[:].rearrange("p (k t) -> p k t", t=PACK), in_=cn_turned[:].rearrange("p t k -> p k t")
+            )
+            tokens = slice(tt * P, (tt + 1) * P)
+            nc.vector.quantize_mx(
+                out=cn_codes[:, tokens].bitcast(FP8X4), scales=cn_scales[:, tokens], in_=cn_grouped[:]
+            )
+
+        for i in range(ROPE_COLS // UNIT):
+            rope_sums = first_stage_unit(raw_rope, i * UNIT, False)
+            unit_out = outs.tile([P, TOKEN_TILES, UNIT], F32, tag="unit_out")
+            for tt in range(TOKEN_TILES):
+                nc.vector.tensor_tensor(
+                    out=unit_out[:, tt, :], in0=rope_sums[tt][:], in1=spread[:, ROW_ROPE_BIAS + i, :], op=ALU.add
+                )
+            finish_k_unit(unit_out, NOPE_COLS // UNIT + i)
+
+        def second_stage_unit(raw_tile, i, bias_row):
+            codes = w_pool.tile([P, UNIT], U32, align_bytes=64, tag="w_codes")
+            scales = w_pool.tile([P, UNIT], U8, align_bytes=64, tag="w_scales")
+            quantise_piece(nc, stage, False, raw_tile[:, :, i * UNIT : (i + 1) * UNIT], codes[:], scales[:])
+            unit_out = outs.tile([P, TOKEN_TILES, UNIT], F32, tag="unit_out")
+            for tt in range(TOKEN_TILES):
+                tokens = slice(tt * P, (tt + 1) * P)
+                product = acc_pool.tile([P, UNIT], F32, tag="acc")
+                nc.tensor.matmul_mx(
+                    out=product[:],
+                    lhsT=cn_codes[:, tokens].bitcast(FP8X4),
+                    lhsT_scale=cn_scales[:, tokens],
+                    rhs=codes[:].bitcast(FP8X4),
+                    rhs_scale=scales[:],
+                    start=True,
+                    stop=True,
+                )
+                nc.vector.tensor_tensor(
+                    out=unit_out[:, tt, :], in0=product[:], in1=spread[:, bias_row + i, :], op=ALU.add
+                )
+            return unit_out
+
+        for i in range(NOPE_COLS // UNIT):
+            finish_k_unit(second_stage_unit(raw_wk, i, ROW_WK_BIAS), i)
+        for i in range(NOPE_COLS // UNIT):
+            unit_out = second_stage_unit(raw_wv, i, ROW_WV_BIAS)
+            cols = slice(i * UNIT, (i + 1) * UNIT)
+            nc.sync.dma_start(out=v_flat[:, cols].rearrange("(t p) c -> p t c", p=P), in_=unit_out[:])

@@ -213,7 +213,7 @@ def tile_mla_pa_kernel(
             return sums
 
         def finish_k_unit(unit_out, flat_unit):
-            rotate(nc, nc.vector, scratch, unit_out[:], (2 - 8 * flat_unit) % 3, cos_pair[:], sin_minus[:], sin_plus[:])
+            rotate(nc, nc.gpsimd, scratch, unit_out[:], (2 - 8 * flat_unit) % 3, cos_pair[:], sin_minus[:], sin_plus[:])
             cols = slice(flat_unit * UNIT, (flat_unit + 1) * UNIT)
             nc.sync.dma_start(out=k_flat[:, cols].rearrange("(t p) c -> p t c", p=P), in_=unit_out[:])
 

@@ -28,6 +28,10 @@ FLOPS = 2 * TOKENS * DIM * (ROPE_COLS + RANK) + 2 * 2 * TOKENS * RANK * NOPE_COL
 
 ROW_LATENT_BIAS, ROW_GAIN, ROW_SHIFT, ROW_ROPE_BIAS, ROW_WK_BIAS, ROW_WV_BIAS, ROWS = 0, 1, 2, 3, 5, 9, 14
 
+ADD_LAG = 2
+PIECES_QUANTISED_AHEAD = 2
+PIECES_REGROUPED_AHEAD = 4
+
 
 def copy(nc, on_vector, out, in_):
     if on_vector:
@@ -36,7 +40,7 @@ def copy(nc, on_vector, out, in_):
         nc.scalar.copy(out=out, in_=in_)
 
 
-def quantise_piece(nc, stage, on_vector, rows, codes, scales):
+def regroup(nc, stage, on_vector, rows):
     grouped = stage.tile([P, UNIT * PACK], BF16, align_bytes=64, tag="grouped")
     copy(
         nc,
@@ -44,25 +48,29 @@ def quantise_piece(nc, stage, on_vector, rows, codes, scales):
         grouped[:].rearrange("p (c i t) -> p c t i", i=4, t=PACK),
         rows.rearrange("p t (c i) -> p c t i", i=4),
     )
+    return grouped
+
+
+def quantise(nc, grouped, codes, scales):
     nc.vector.quantize_mx(out=codes.bitcast(FP8X4), scales=scales, in_=grouped[:])
 
 
-def rotate(nc, eng, scratch, unit_out, first_block, cos_pair, sin_minus, sin_plus):
+def rotate_products(nc, scratch, unit_out, first_block, cos_pair, sin_minus, sin_plus):
     blocks = unit_out.rearrange("p t (k d) -> p t k d", d=ROPE)[:, :, first_block::3, :]
     n = blocks.shape[2]
     pairs = blocks.rearrange("p t n (j e) -> p t n j e", e=2)
     half = [P, TOKEN_TILES, n, ROPE // 2]
     crossed = scratch.tile([P, 2, TOKEN_TILES, n, ROPE // 2], F32, tag="crossed")
-    eng.tensor_tensor(
+    nc.gpsimd.tensor_tensor(
         out=crossed[:, 0], in0=pairs[:, :, :, :, 1], in1=sin_minus.unsqueeze(2).to_broadcast(half), op=ALU.mult
     )
-    eng.tensor_tensor(
+    nc.gpsimd.tensor_tensor(
         out=crossed[:, 1], in0=pairs[:, :, :, :, 0], in1=sin_plus.unsqueeze(2).to_broadcast(half), op=ALU.mult
     )
-    eng.tensor_tensor(
+    nc.gpsimd.tensor_tensor(
         out=blocks, in0=blocks, in1=cos_pair.unsqueeze(2).to_broadcast([P, TOKEN_TILES, n, ROPE]), op=ALU.mult
     )
-    eng.tensor_tensor(out=pairs, in0=pairs, in1=crossed[:].rearrange("p e t n j -> p t n j e"), op=ALU.add)
+    return pairs, crossed[:].rearrange("p e t n j -> p t n j e")
 
 
 def tile_mla_pa_kernel(
@@ -74,35 +82,40 @@ def tile_mla_pa_kernel(
     v_flat = out_1.rearrange("b s h d -> (b s) (h d)")
 
     with ExitStack() as ctx:
+        ctx.enter_context(tc.manual_schedule())
         const = ctx.enter_context(tc.tile_pool(name="const", bufs=1))
         raw = ctx.enter_context(tc.tile_pool(name="raw", bufs=1))
         keep = ctx.enter_context(tc.tile_pool(name="keep", bufs=1))
-        x_stage = ctx.enter_context(tc.tile_pool(name="x_stage", bufs=3))
         stage = ctx.enter_context(tc.tile_pool(name="stage", bufs=4))
         a_pool = ctx.enter_context(tc.tile_pool(name="a_pool", bufs=2))
         w_pool = ctx.enter_context(tc.tile_pool(name="w_pool", bufs=3))
         norm = ctx.enter_context(tc.tile_pool(name="norm", bufs=2))
-        outs = ctx.enter_context(tc.tile_pool(name="outs", bufs=3))
-        scratch = ctx.enter_context(tc.tile_pool(name="scratch", bufs=2))
-        acc_pool = ctx.enter_context(tc.psum_pool(name="acc_pool", bufs=6))
-        turn_pool = ctx.enter_context(tc.psum_pool(name="turn_pool", bufs=2))
+        outs = ctx.enter_context(tc.tile_pool(name="outs", bufs=5))
+        scratch = ctx.enter_context(tc.tile_pool(name="scratch", bufs=3))
+        banks = ctx.enter_context(tc.psum_pool(name="banks", bufs=8))
 
-        ident_f32 = const.tile([P, P], F32)
-        make_identity(nc, ident_f32[:])
         ident_bf = const.tile([P, P], BF16)
         make_identity(nc, ident_bf[:])
-        one = const.tile([P, 1], F32)
-        nc.vector.memset(one[:], 1.0)
-        nc.scalar.sqrt(out=one[:], in_=one[:])
+        ident_f32 = const.tile([P, P], F32)
+        make_identity(nc, ident_f32[:])
         vec_rows = const.tile([P, UNIT], BF16)
         nc.vector.memset(vec_rows[:], 0.0)
-
-        x_sb = raw.tile([P, TOKEN_TILES, DIM], BF16)
-        for tt in range(TOKEN_TILES):
-            nc.sync.dma_start(out=x_sb[:, tt, :], in_=x_rows[tt * P : (tt + 1) * P, :])
+        one = const.tile([P, 1], F32)
+        nc.vector.memset(one[:], 1.0)
 
         def load_row(row, count, vector):
             nc.sync.dma_start(out=vec_rows[row : row + count, :], in_=vector.rearrange("(r c) -> r c", c=UNIT))
+
+        load_row(ROW_LATENT_BIAS, 1, wkv_a_b[ROPE_COLS:])
+        load_row(ROW_GAIN, 1, kvn_g)
+        load_row(ROW_SHIFT, 1, kvn_b)
+        load_row(ROW_ROPE_BIAS, 2, wkv_a_b[:ROPE_COLS])
+        load_row(ROW_WK_BIAS, 4, wk_b)
+        load_row(ROW_WV_BIAS, 4, wv_b)
+        cos_sin = const.tile([P, 2, SEQ_TILES, ROPE // 2], BF16)
+        nc.sync.dma_start(out=cos_sin[:, 0], in_=cos.rearrange("(a p) j -> p a j", p=P))
+        nc.sync.dma_start(out=cos_sin[:, 1], in_=sin.rearrange("(a p) j -> p a j", p=P))
+        nc.scalar.sqrt(out=one[:], in_=one[:])
 
         def load_first_stage(tile_, col0, width):
             for g in range(PASSES):
@@ -115,113 +128,152 @@ def tile_mla_pa_kernel(
 
         def load_second_stage(tile_, weight):
             view = weight.rearrange("(t p) n -> p t n", p=P)
-            for half in range(2):
-                cols = slice(half * NOPE_COLS // 2, (half + 1) * NOPE_COLS // 2)
+            for part in range(2):
+                cols = slice(part * NOPE_COLS // 2, (part + 1) * NOPE_COLS // 2)
                 nc.sync.dma_start(out=tile_[:, :, cols], in_=view[:, :, cols])
 
-        load_row(ROW_LATENT_BIAS, 1, wkv_a_b[ROPE_COLS:])
-        load_row(ROW_GAIN, 1, kvn_g)
-        load_row(ROW_SHIFT, 1, kvn_b)
         raw_latent = raw.tile([P, PASSES, PACK, RANK], BF16)
-        load_first_stage(raw_latent, ROPE_COLS, RANK)
-        load_row(ROW_ROPE_BIAS, 2, wkv_a_b[:ROPE_COLS])
-        load_row(ROW_WK_BIAS, 4, wk_b)
-        load_row(ROW_WV_BIAS, 4, wv_b)
-        cos_sin = const.tile([P, 2, SEQ_TILES, ROPE // 2], BF16)
-        nc.sync.dma_start(out=cos_sin[:, 0], in_=cos.rearrange("(a p) j -> p a j", p=P))
-        nc.sync.dma_start(out=cos_sin[:, 1], in_=sin.rearrange("(a p) j -> p a j", p=P))
-        raw_rope = raw.tile([P, PASSES, PACK, ROPE_COLS], BF16)
-        load_first_stage(raw_rope, 0, ROPE_COLS)
         raw_wk = raw.tile([P, PACK, NOPE_COLS], BF16)
-        load_second_stage(raw_wk, wk_w)
-        raw_wv = raw.tile([P, PACK, NOPE_COLS], BF16)
-        load_second_stage(raw_wv, wv_w)
-
+        raw_rope = raw.tile([P, PASSES, PACK, ROPE_COLS], BF16)
         x_codes = keep.tile([P, PASSES, TOKENS], U32, align_bytes=64)
         x_scales = keep.tile([P, PASSES, TOKENS], U8, align_bytes=64)
-        for pair in range(TOKEN_TILES // 2):
-            for g in range(PASSES):
-                turned = turn_pool.tile([P, 2, 2, P], F32, tag="turn")
-                for i in range(2):
-                    words = x_sb[:, 2 * pair + i, :].bitcast(F32)
-                    for u in range(2):
-                        col0 = (2 * g + u) * P
-                        nc.tensor.transpose(turned[:, i, u, :], words[:, col0 : col0 + P], ident_f32[:])
-                x_grouped = x_stage.tile([P, 2 * P * PACK], BF16, align_bytes=64)
-                copy(
-                    nc,
-                    g % 2 == 1,
-                    x_grouped[:].bitcast(F32).rearrange("p (i k u) -> p i k u", i=2, u=2),
-                    turned[:].rearrange("p i u k -> p i k u"),
-                )
-                cols = slice(pair * 2 * P, (pair + 1) * 2 * P)
-                nc.vector.quantize_mx(
-                    out=x_codes[:, g, cols].bitcast(FP8X4), scales=x_scales[:, g, cols], in_=x_grouped[:]
-                )
-
         spread = const.tile([P, ROWS, UNIT], BF16)
-        for r in range(0, ROWS, 2):
-            picked = turn_pool.tile([P, 2, UNIT], BF16, tag="turn")
-            for i in range(2):
-                nc.tensor.matmul(
-                    out=picked[:, i, :],
-                    lhsT=ident_bf[:, r + i : r + i + 1].to_broadcast([P, P]),
-                    rhs=vec_rows[:],
-                    start=True,
-                    stop=True,
-                )
-            copy(nc, r % 4 == 2, spread[:, r : r + 2, :], picked[:])
-
         cos_pair = const.tile([P, TOKEN_TILES, ROPE], F32)
         sin_plus = const.tile([P, TOKEN_TILES, ROPE // 2], F32)
         sin_minus = const.tile([P, TOKEN_TILES, ROPE // 2], F32)
-        for b in range(BATCH):
-            tiles = slice(b * SEQ_TILES, (b + 1) * SEQ_TILES)
-            nc.vector.tensor_copy(
-                out=cos_pair[:, tiles, :].rearrange("p a (j e) -> p a j e", e=2),
-                in_=cos_sin[:, 0].unsqueeze(3).to_broadcast([P, SEQ_TILES, ROPE // 2, 2]),
-            )
-            nc.vector.tensor_copy(out=sin_plus[:, tiles, :], in_=cos_sin[:, 1])
-            nc.vector.tensor_scalar(
-                out=sin_minus[:, tiles, :], in0=cos_sin[:, 1], scalar1=-1.0, scalar2=None, op0=ALU.mult
-            )
 
-        def first_stage_unit(raw_tile, col0, vector_helps):
-            codes = a_pool.tile([P, PASSES, UNIT], U32, align_bytes=64, tag="a_codes")
-            scales = a_pool.tile([P, PASSES, UNIT], U8, align_bytes=64, tag="a_scales")
-            sums = [acc_pool.tile([P, UNIT], F32, tag="acc", name="sum%d" % tt) for tt in range(TOKEN_TILES)]
-            for g in range(PASSES):
-                quantise_piece(
-                    nc,
-                    stage,
-                    vector_helps and g % 2 == 1,
-                    raw_tile[:, g, :, col0 : col0 + UNIT],
-                    codes[:, g, :],
-                    scales[:, g, :],
-                )
-                for tt in range(TOKEN_TILES):
-                    tokens = slice(tt * P, (tt + 1) * P)
-                    nc.tensor.matmul_mx(
-                        out=sums[tt][:],
-                        lhsT=x_codes[:, g, tokens].bitcast(FP8X4),
-                        lhsT_scale=x_scales[:, g, tokens],
-                        rhs=codes[:, g, :].bitcast(FP8X4),
-                        rhs_scale=scales[:, g, :],
-                        start=(g == 0),
-                        stop=(g == PASSES - 1),
+        with tc.tile_pool(name="x_home", bufs=1) as x_home, tc.tile_pool(name="x_staging", bufs=3) as x_staging:
+            x_sb = x_home.tile([P, TOKEN_TILES, DIM], BF16)
+            for tt in range(TOKEN_TILES):
+                nc.sync.dma_start(out=x_sb[:, tt, :], in_=x_rows[tt * P : (tt + 1) * P, :])
+            load_first_stage(raw_latent, ROPE_COLS, RANK)
+            load_second_stage(raw_wk, wk_w)
+            load_first_stage(raw_rope, 0, ROPE_COLS)
+
+            for r in range(0, ROWS, 2):
+                picked = banks.tile([P, 2, UNIT], BF16, tag="bank")
+                for i in range(2):
+                    nc.tensor.matmul(
+                        out=picked[:, i, :],
+                        lhsT=ident_bf[:, r + i : r + i + 1].to_broadcast([P, P]),
+                        rhs=vec_rows[:],
+                        start=True,
+                        stop=True,
                     )
-            return sums
+                copy(nc, r % 4 == 0, spread[:, r : r + 2, :], picked[:])
 
-        def finish_k_unit(unit_out, flat_unit):
-            rotate(nc, nc.gpsimd, scratch, unit_out[:], (2 - 8 * flat_unit) % 3, cos_pair[:], sin_minus[:], sin_plus[:])
-            cols = slice(flat_unit * UNIT, (flat_unit + 1) * UNIT)
-            nc.sync.dma_start(out=k_flat[:, cols].rearrange("(t p) c -> p t c", p=P), in_=unit_out[:])
+            for b in range(BATCH):
+                tiles = slice(b * SEQ_TILES, (b + 1) * SEQ_TILES)
+                nc.vector.tensor_copy(
+                    out=cos_pair[:, tiles, :].rearrange("p a (j e) -> p a j e", e=2),
+                    in_=cos_sin[:, 0].unsqueeze(3).to_broadcast([P, SEQ_TILES, ROPE // 2, 2]),
+                )
+                nc.vector.tensor_copy(out=sin_plus[:, tiles, :], in_=cos_sin[:, 1])
+                nc.vector.tensor_scalar(
+                    out=sin_minus[:, tiles, :], in0=cos_sin[:, 1], scalar1=-1.0, scalar2=None, op0=ALU.mult
+                )
 
-        latent_sums = first_stage_unit(raw_latent, 0, True)
+            waiting = []
+            for pair in range(TOKEN_TILES // 2):
+                for g in range(PASSES):
+                    turned = banks.tile([P, 2, 2, P], F32, tag="bank")
+                    for i in range(2):
+                        words = x_sb[:, 2 * pair + i, :].bitcast(F32)
+                        for u in range(2):
+                            col0 = (2 * g + u) * P
+                            nc.tensor.transpose(turned[:, i, u, :], words[:, col0 : col0 + P], ident_f32[:])
+                    x_grouped = x_staging.tile([P, 2 * P * PACK], BF16, align_bytes=64)
+                    copy(
+                        nc,
+                        g % 2 == 1,
+                        x_grouped[:].bitcast(F32).rearrange("p (i k u) -> p i k u", i=2, u=2),
+                        turned[:].rearrange("p i u k -> p i k u"),
+                    )
+                    cols = slice(pair * 2 * P, (pair + 1) * 2 * P)
+                    waiting.append((x_grouped, x_codes[:, g, cols], x_scales[:, g, cols]))
+                    if len(waiting) > 1:
+                        quantise(nc, *waiting[-2])
+            quantise(nc, *waiting[-1])
+
+        late = ctx.enter_context(tc.tile_pool(name="late", bufs=1, reuse_waits="tile"))
+        raw_wv = late.tile([P, PACK, NOPE_COLS], BF16)
+        load_second_stage(raw_wv, wv_w)
+
+        def multiply(sums, lhs_codes, lhs_scales, codes, scales, first, last):
+            for tt in range(TOKEN_TILES):
+                tokens = slice(tt * P, (tt + 1) * P)
+                nc.tensor.matmul_mx(
+                    out=sums[tt][:],
+                    lhsT=lhs_codes[:, tokens].bitcast(FP8X4),
+                    lhsT_scale=lhs_scales[:, tokens],
+                    rhs=codes.bitcast(FP8X4),
+                    rhs_scale=scales,
+                    start=first,
+                    stop=last,
+                )
+
+        def four_banks():
+            return [banks.tile([P, UNIT], F32, tag="bank", name="sum%d" % tt) for tt in range(TOKEN_TILES)]
+
+        def k_rope_unit(i):
+            return {
+                "rows": [raw_rope[:, g, :, i * UNIT : (i + 1) * UNIT] for g in range(PASSES)],
+                "bias": ROW_ROPE_BIAS + i,
+                "flat_unit": NOPE_COLS // UNIT + i,
+                "dest": k_flat[:, NOPE_COLS + i * UNIT : NOPE_COLS + (i + 1) * UNIT],
+            }
+
+        def second_stage_unit(raw_tile, bias_row, flat, i, rotated):
+            return {
+                "rows": [raw_tile[:, :, i * UNIT : (i + 1) * UNIT]],
+                "bias": bias_row + i,
+                "flat_unit": i if rotated else None,
+                "dest": flat[:, i * UNIT : (i + 1) * UNIT],
+            }
+
+        wk_units = [second_stage_unit(raw_wk, ROW_WK_BIAS, k_flat, i, True) for i in range(NOPE_COLS // UNIT)]
+        wv_units = [second_stage_unit(raw_wv, ROW_WV_BIAS, v_flat, i, False) for i in range(NOPE_COLS // UNIT)]
+        units = wk_units + [k_rope_unit(0)] + wv_units[:2] + [k_rope_unit(1)] + wv_units[2:]
+        pieces = [(n, g) for n in range(len(units)) for g in range(len(units[n]["rows"]))]
+        grouped_of = {}
+
+        def regroup_piece(j):
+            if j < len(pieces):
+                n, g = pieces[j]
+                grouped_of[j] = regroup(nc, stage, False, units[n]["rows"][g])
+
+        def quantise_piece(j):
+            if j < len(pieces):
+                n, g = pieces[j]
+                if g == 0:
+                    count = len(units[n]["rows"])
+                    pool, tag = (a_pool, "a") if count == PASSES else (w_pool, "w")
+                    units[n]["codes"] = pool.tile([P, count, UNIT], U32, align_bytes=64, tag=tag + "_codes", name="codes")
+                    units[n]["scales"] = pool.tile([P, count, UNIT], U8, align_bytes=64, tag=tag + "_scales", name="scales")
+                quantise(nc, grouped_of[j], units[n]["codes"][:, g, :], units[n]["scales"][:, g, :])
+
+        latent_codes = a_pool.tile([P, PASSES, UNIT], U32, align_bytes=64, tag="a_codes")
+        latent_scales = a_pool.tile([P, PASSES, UNIT], U8, align_bytes=64, tag="a_scales")
+        latent_sums = four_banks()
+        latent_grouped = [None] * PASSES
+        for g in range(0, PASSES, 2):
+            latent_grouped[g] = regroup(nc, stage, False, raw_latent[:, g, :, :])
+            latent_grouped[g + 1] = regroup(nc, stage, True, raw_latent[:, g + 1, :, :])
+            for h in (g, g + 1):
+                quantise(nc, latent_grouped[h], latent_codes[:, h, :], latent_scales[:, h, :])
+                multiply(
+                    latent_sums, x_codes[:, h, :], x_scales[:, h, :], latent_codes[:, h, :], latent_scales[:, h, :],
+                    h == 0, h == PASSES - 1,
+                )
+        regroup_piece(0)
+        regroup_piece(1)
 
         c_all = keep.tile([P, TOKEN_TILES, RANK], F32)
         c_sum = keep.tile([P, TOKEN_TILES], F32)
+        minus_mean = keep.tile([P, TOKEN_TILES], F32)
+        square_sum = keep.tile([P, TOKEN_TILES], F32)
         for tt in range(TOKEN_TILES):
+            one_tile = slice(tt, tt + 1)
             nc.vector.scalar_tensor_tensor(
                 out=c_all[:, tt, :],
                 in0=latent_sums[tt][:],
@@ -229,32 +281,34 @@ def tile_mla_pa_kernel(
                 in1=spread[:, ROW_LATENT_BIAS, :],
                 op0=ALU.mult,
                 op1=ALU.add,
-                accum_out=c_sum[:, tt : tt + 1],
+                accum_out=c_sum[:, one_tile],
             )
-        minus_mean = keep.tile([P, TOKEN_TILES], F32)
-        nc.vector.tensor_scalar(out=minus_mean[:], in0=c_sum[:], scalar1=-1.0 / RANK, scalar2=None, op0=ALU.mult)
-        square_sum = keep.tile([P, TOKEN_TILES], F32)
-        for tt in range(TOKEN_TILES):
+            nc.vector.tensor_scalar(
+                out=minus_mean[:, one_tile], in0=c_sum[:, one_tile], scalar1=-1.0 / RANK, scalar2=None, op0=ALU.mult
+            )
             squares = norm.tile([P, RANK], BF16, tag="squares")
             nc.scalar.activation(
                 out=squares[:],
                 in_=c_all[:, tt, :],
                 func=ACT.Square,
-                bias=minus_mean[:, tt : tt + 1],
+                bias=minus_mean[:, one_tile],
                 scale=1.0,
-                accum_out=square_sum[:, tt : tt + 1],
+                accum_out=square_sum[:, one_tile],
             )
-        spread_of_c = keep.tile([P, TOKEN_TILES], F32)
+        quantise_piece(0)
+        deviation = keep.tile([P, TOKEN_TILES], F32)
         nc.vector.tensor_scalar(
-            out=spread_of_c[:], in0=square_sum[:], scalar1=1.0 / RANK, scalar2=EPS, op0=ALU.mult, op1=ALU.add
+            out=deviation[:], in0=square_sum[:], scalar1=1.0 / RANK, scalar2=EPS, op0=ALU.mult, op1=ALU.add
         )
-        nc.scalar.sqrt(out=spread_of_c[:], in_=spread_of_c[:])
+        nc.scalar.sqrt(out=deviation[:], in_=deviation[:])
+        regroup_piece(2)
         inv_std = keep.tile([P, TOKEN_TILES], F32)
-        nc.vector.reciprocal(out=inv_std[:], in_=spread_of_c[:])
+        nc.vector.reciprocal(out=inv_std[:], in_=deviation[:])
 
         cn_codes = keep.tile([P, TOKENS], U32, align_bytes=64)
         cn_scales = keep.tile([P, TOKENS], U8, align_bytes=64)
         cn = keep.tile([P, TOKEN_TILES, RANK], BF16)
+        cn_waiting = []
         for tt in range(TOKEN_TILES):
             gained = norm.tile([P, RANK], F32, tag="gained")
             nc.vector.scalar_tensor_tensor(
@@ -273,8 +327,7 @@ def tile_mla_pa_kernel(
                 op0=ALU.mult,
                 op1=ALU.add,
             )
-        for tt in range(TOKEN_TILES):
-            cn_turned = turn_pool.tile([P, PACK, P], BF16, tag="turn")
+            cn_turned = banks.tile([P, PACK, P], BF16, tag="bank")
             for t in range(PACK):
                 nc.tensor.transpose(cn_turned[:, t, :], cn[:, tt, t * P : (t + 1) * P], ident_bf[:])
             cn_grouped = norm.tile([P, P * PACK], BF16, align_bytes=64, tag="cn_grouped")
@@ -282,44 +335,51 @@ def tile_mla_pa_kernel(
                 out=cn_grouped[:].rearrange("p (k t) -> p k t", t=PACK), in_=cn_turned[:].rearrange("p t k -> p k t")
             )
             tokens = slice(tt * P, (tt + 1) * P)
-            nc.vector.quantize_mx(
-                out=cn_codes[:, tokens].bitcast(FP8X4), scales=cn_scales[:, tokens], in_=cn_grouped[:]
-            )
+            cn_waiting.append((cn_grouped, cn_codes[:, tokens], cn_scales[:, tokens]))
+            if tt > 0:
+                quantise(nc, *cn_waiting[tt - 1])
+        quantise_piece(1)
+        quantise(nc, *cn_waiting[-1])
+        regroup_piece(3)
 
-        for i in range(ROPE_COLS // UNIT):
-            rope_sums = first_stage_unit(raw_rope, i * UNIT, False)
-            unit_out = outs.tile([P, TOKEN_TILES, UNIT], F32, tag="unit_out")
+        def multiply_unit(n):
+            unit = units[n]
+            unit["sums"] = four_banks()
+            count = len(unit["rows"])
+            for g in range(count):
+                if count == PASSES:
+                    lhs_codes, lhs_scales = x_codes[:, g, :], x_scales[:, g, :]
+                else:
+                    lhs_codes, lhs_scales = cn_codes[:], cn_scales[:]
+                multiply(
+                    unit["sums"], lhs_codes, lhs_scales, unit["codes"][:, g, :], unit["scales"][:, g, :],
+                    g == 0, g == count - 1,
+                )
+
+        def store(unit, tiles):
+            nc.sync.dma_start(out=unit["dest"].rearrange("(t p) c -> p t c", p=P)[:, tiles, :], in_=unit["out"][:, tiles, :])
+
+        multiply_unit(0)
+        for n in range(len(units)):
+            unit = units[n]
+            if n + 1 < len(units):
+                multiply_unit(n + 1)
+            regroup_piece(PIECES_REGROUPED_AHEAD + 2 * n)
+            regroup_piece(PIECES_REGROUPED_AHEAD + 2 * n + 1)
+            unit["out"] = outs.tile([P, TOKEN_TILES, UNIT], F32, tag="unit_out", name="unit_out")
             for tt in range(TOKEN_TILES):
                 nc.vector.tensor_tensor(
-                    out=unit_out[:, tt, :], in0=rope_sums[tt][:], in1=spread[:, ROW_ROPE_BIAS + i, :], op=ALU.add
+                    out=unit["out"][:, tt, :], in0=unit["sums"][tt][:], in1=spread[:, unit["bias"], :], op=ALU.add
                 )
-            finish_k_unit(unit_out, NOPE_COLS // UNIT + i)
-
-        def second_stage_unit(raw_tile, i, bias_row):
-            codes = w_pool.tile([P, UNIT], U32, align_bytes=64, tag="w_codes")
-            scales = w_pool.tile([P, UNIT], U8, align_bytes=64, tag="w_scales")
-            quantise_piece(nc, stage, False, raw_tile[:, :, i * UNIT : (i + 1) * UNIT], codes[:], scales[:])
-            unit_out = outs.tile([P, TOKEN_TILES, UNIT], F32, tag="unit_out")
-            for tt in range(TOKEN_TILES):
-                tokens = slice(tt * P, (tt + 1) * P)
-                product = acc_pool.tile([P, UNIT], F32, tag="acc")
-                nc.tensor.matmul_mx(
-                    out=product[:],
-                    lhsT=cn_codes[:, tokens].bitcast(FP8X4),
-                    lhsT_scale=cn_scales[:, tokens],
-                    rhs=codes[:].bitcast(FP8X4),
-                    rhs_scale=scales[:],
-                    start=True,
-                    stop=True,
+                if unit["flat_unit"] is None and tt % 2 == 1:
+                    store(unit, slice(tt - 1, tt + 1))
+            if unit["flat_unit"] is not None:
+                unit["add"] = rotate_products(
+                    nc, scratch, unit["out"][:], (2 - 8 * unit["flat_unit"]) % 3, cos_pair[:], sin_minus[:], sin_plus[:]
                 )
-                nc.vector.tensor_tensor(
-                    out=unit_out[:, tt, :], in0=product[:], in1=spread[:, bias_row + i, :], op=ALU.add
-                )
-            return unit_out
-
-        for i in range(NOPE_COLS // UNIT):
-            finish_k_unit(second_stage_unit(raw_wk, i, ROW_WK_BIAS), i)
-        for i in range(NOPE_COLS // UNIT):
-            unit_out = second_stage_unit(raw_wv, i, ROW_WV_BIAS)
-            cols = slice(i * UNIT, (i + 1) * UNIT)
-            nc.sync.dma_start(out=v_flat[:, cols].rearrange("(t p) c -> p t c", p=P), in_=unit_out[:])
+            if n >= ADD_LAG and units[n - ADD_LAG]["flat_unit"] is not None:
+                pairs, crossed = units[n - ADD_LAG]["add"]
+                nc.vector.tensor_tensor(out=pairs, in0=pairs, in1=crossed, op=ALU.add)
+                store(units[n - ADD_LAG], slice(0, TOKEN_TILES))
+            quantise_piece(PIECES_QUANTISED_AHEAD + 2 * n)
+            quantise_piece(PIECES_QUANTISED_AHEAD + 2 * n + 1)

@@ -26,11 +26,9 @@ NOPE_COLS = HEADS * NOPE
 EPS = 1e-5
 FLOPS = 2 * TOKENS * DIM * (ROPE_COLS + RANK) + 2 * 2 * TOKENS * RANK * NOPE_COLS
 
-ROW_LATENT_BIAS, ROW_GAIN, ROW_SHIFT, ROW_ROPE_BIAS, ROW_WK_BIAS, ROW_WV_BIAS, ROWS = 0, 1, 2, 3, 5, 9, 14
+ROW_LATENT_BIAS, ROW_GAIN, ROW_SHIFT, ROWS = 0, 1, 2, 3
 
 ADD_LAG = 2
-PIECES_QUANTISED_AHEAD = 2
-PIECES_REGROUPED_AHEAD = 4
 
 
 def copy(nc, on_vector, out, in_):
@@ -40,19 +38,17 @@ def copy(nc, on_vector, out, in_):
         nc.scalar.copy(out=out, in_=in_)
 
 
-def regroup(nc, stage, on_vector, rows):
-    grouped = stage.tile([P, UNIT * PACK], BF16, align_bytes=64, tag="grouped")
+def regroup(nc, on_vector, grouped, rows):
     copy(
         nc,
         on_vector,
-        grouped[:].rearrange("p (c i t) -> p c t i", i=4, t=PACK),
+        grouped.rearrange("p (c i t) -> p c t i", i=4, t=PACK),
         rows.rearrange("p t (c i) -> p c t i", i=4),
     )
-    return grouped
 
 
 def quantise(nc, grouped, codes, scales):
-    nc.vector.quantize_mx(out=codes.bitcast(FP8X4), scales=scales, in_=grouped[:])
+    nc.vector.quantize_mx(out=codes.bitcast(FP8X4), scales=scales, in_=grouped)
 
 
 def rotate_products(nc, scratch, unit_out, first_block, cos_pair, sin_minus, sin_plus):
@@ -86,163 +82,234 @@ def tile_mla_pa_kernel(
         const = ctx.enter_context(tc.tile_pool(name="const", bufs=1))
         raw = ctx.enter_context(tc.tile_pool(name="raw", bufs=1))
         keep = ctx.enter_context(tc.tile_pool(name="keep", bufs=1))
-        stage = ctx.enter_context(tc.tile_pool(name="stage", bufs=4))
+        stage = ctx.enter_context(tc.tile_pool(name="stage", bufs=10))
         a_pool = ctx.enter_context(tc.tile_pool(name="a_pool", bufs=2))
         w_pool = ctx.enter_context(tc.tile_pool(name="w_pool", bufs=3))
         norm = ctx.enter_context(tc.tile_pool(name="norm", bufs=2))
-        outs = ctx.enter_context(tc.tile_pool(name="outs", bufs=5))
-        scratch = ctx.enter_context(tc.tile_pool(name="scratch", bufs=3))
         banks = ctx.enter_context(tc.psum_pool(name="banks", bufs=8))
 
-        ident_bf = const.tile([P, P], BF16)
-        make_identity(nc, ident_bf[:])
-        ident_f32 = const.tile([P, P], F32)
-        make_identity(nc, ident_f32[:])
         vec_rows = const.tile([P, UNIT], BF16)
-        nc.vector.memset(vec_rows[:], 0.0)
-        one = const.tile([P, 1], F32)
-        nc.vector.memset(one[:], 1.0)
-
-        def load_row(row, count, vector):
-            nc.sync.dma_start(out=vec_rows[row : row + count, :], in_=vector.rearrange("(r c) -> r c", c=UNIT))
-
-        load_row(ROW_LATENT_BIAS, 1, wkv_a_b[ROPE_COLS:])
-        load_row(ROW_GAIN, 1, kvn_g)
-        load_row(ROW_SHIFT, 1, kvn_b)
-        load_row(ROW_ROPE_BIAS, 2, wkv_a_b[:ROPE_COLS])
-        load_row(ROW_WK_BIAS, 4, wk_b)
-        load_row(ROW_WV_BIAS, 4, wv_b)
         cos_sin = const.tile([P, 2, SEQ_TILES, ROPE // 2], BF16)
-        nc.sync.dma_start(out=cos_sin[:, 0], in_=cos.rearrange("(a p) j -> p a j", p=P))
-        nc.sync.dma_start(out=cos_sin[:, 1], in_=sin.rearrange("(a p) j -> p a j", p=P))
-        nc.scalar.sqrt(out=one[:], in_=one[:])
-
-        def load_first_stage(tile_, col0, width):
-            for g in range(PASSES):
-                for u in range(2):
-                    row0 = g * K_PASS + u * 2 * P
-                    nc.sync.dma_start(
-                        out=tile_[:, g, 2 * u : 2 * u + 2, :],
-                        in_=wkv_a_w[row0 : row0 + 2 * P, col0 : col0 + width].rearrange("(q e) c -> q e c", e=2),
-                    )
-
-        def load_second_stage(tile_, weight):
-            view = weight.rearrange("(t p) n -> p t n", p=P)
-            for part in range(2):
-                cols = slice(part * NOPE_COLS // 2, (part + 1) * NOPE_COLS // 2)
-                nc.sync.dma_start(out=tile_[:, :, cols], in_=view[:, :, cols])
-
-        raw_latent = raw.tile([P, PASSES, PACK, RANK], BF16)
-        raw_wk = raw.tile([P, PACK, NOPE_COLS], BF16)
-        raw_rope = raw.tile([P, PASSES, PACK, ROPE_COLS], BF16)
-        x_codes = keep.tile([P, PASSES, TOKENS], U32, align_bytes=64)
-        x_scales = keep.tile([P, PASSES, TOKENS], U8, align_bytes=64)
+        ident_f32 = const.tile([P, P], F32)
+        ident_bf = const.tile([P, P], BF16)
+        eps = const.tile([P, 1], F32)
+        first = const.tile([P, 1], F32)
         spread = const.tile([P, ROWS, UNIT], BF16)
+        wk_bias = const.tile([P, NOPE_COLS], BF16)
+        wv_bias = const.tile([P, NOPE_COLS], BF16)
+        rope_bias = const.tile([P, ROPE_COLS], BF16)
         cos_pair = const.tile([P, TOKEN_TILES, ROPE], F32)
         sin_plus = const.tile([P, TOKEN_TILES, ROPE // 2], F32)
         sin_minus = const.tile([P, TOKEN_TILES, ROPE // 2], F32)
+        raw_wk = raw.tile([P, PACK, NOPE_COLS], BF16)
+        raw_rope = raw.tile([P, PASSES, PACK, ROPE_COLS], BF16)
+        x_codes = keep.tile([P, TOKEN_TILES, PASSES * P], U32, align_bytes=64)
+        x_scales = keep.tile([P, TOKEN_TILES, PASSES * P], U8, align_bytes=64)
+        c_all = keep.tile([P, TOKEN_TILES, RANK], F32)
+        c_sum = keep.tile([P, TOKEN_TILES], F32)
+        minus_mean = keep.tile([P, TOKEN_TILES], F32)
+        square_sum = keep.tile([P, TOKEN_TILES], F32)
+        inv_std = keep.tile([P, TOKEN_TILES], F32)
+        cn = keep.tile([P, TOKEN_TILES, RANK], BF16)
+        cn_codes = keep.tile([P, TOKENS], U32, align_bytes=64)
+        cn_scales = keep.tile([P, TOKENS], U8, align_bytes=64)
 
-        with tc.tile_pool(name="x_home", bufs=1) as x_home, tc.tile_pool(name="x_staging", bufs=3) as x_staging:
-            x_sb = x_home.tile([P, TOKEN_TILES, DIM], BF16)
-            for tt in range(TOKEN_TILES):
+        nc.vector.memset(vec_rows[:], 0.0)
+        nc.vector.memset(eps[:], EPS)
+        make_identity(nc, ident_f32[:])
+        make_identity(nc, ident_bf[:])
+        for row, vector in ((ROW_LATENT_BIAS, wkv_a_b[ROPE_COLS:]), (ROW_GAIN, kvn_g), (ROW_SHIFT, kvn_b)):
+            nc.scalar.dma_start(out=vec_rows[row : row + 1, :], in_=vector.rearrange("(r c) -> r c", c=UNIT))
+        nc.scalar.dma_start(out=cos_sin[:, 0], in_=cos.rearrange("(a p) j -> p a j", p=P))
+        nc.scalar.dma_start(out=cos_sin[:, 1], in_=sin.rearrange("(a p) j -> p a j", p=P))
+        nc.scalar.activation(out=first[:], in_=eps[:], func=ACT.Abs_reciprocal_sqrt, bias=eps[:], scale=1.0)
+
+        def load_first_stage(tile_, g, col0, width):
+            for u in range(2):
+                row0 = g * K_PASS + u * 2 * P
+                nc.sync.dma_start(
+                    out=tile_[:, g, 2 * u : 2 * u + 2, :],
+                    in_=wkv_a_w[row0 : row0 + 2 * P, col0 : col0 + width].rearrange("(q e) c -> q e c", e=2),
+                )
+
+        def load_second_stage(tile_, weight, part, parts):
+            view = weight.rearrange("(t p) n -> p t n", p=P)
+            cols = slice(part * NOPE_COLS // parts, (part + 1) * NOPE_COLS // parts)
+            nc.sync.dma_start(out=tile_[:, :, cols], in_=view[:, :, cols])
+
+        with tc.tile_pool(name="head", bufs=1) as head, tc.tile_pool(name="x_staging", bufs=4) as x_staging:
+            x_sb = head.tile([P, TOKEN_TILES, DIM], BF16)
+            raw_latent = head.tile([P, PASSES, PACK, RANK], BF16)
+
+            def load_x(tt):
                 nc.sync.dma_start(out=x_sb[:, tt, :], in_=x_rows[tt * P : (tt + 1) * P, :])
-            load_first_stage(raw_latent, ROPE_COLS, RANK)
-            load_second_stage(raw_wk, wk_w)
-            load_first_stage(raw_rope, 0, ROPE_COLS)
 
-            for r in range(0, ROWS, 2):
-                picked = banks.tile([P, 2, UNIT], BF16, tag="bank")
-                for i in range(2):
-                    nc.tensor.matmul(
-                        out=picked[:, i, :],
-                        lhsT=ident_bf[:, r + i : r + i + 1].to_broadcast([P, P]),
-                        rhs=vec_rows[:],
-                        start=True,
-                        stop=True,
-                    )
-                copy(nc, r % 4 == 0, spread[:, r : r + 2, :], picked[:])
+            load_first_stage(raw_latent, 0, ROPE_COLS, RANK)
+            load_first_stage(raw_latent, 1, ROPE_COLS, RANK)
+            load_x(0)
+            load_first_stage(raw_latent, 2, ROPE_COLS, RANK)
+            load_x(1)
+            load_first_stage(raw_latent, 3, ROPE_COLS, RANK)
+            load_x(2)
+            load_x(3)
+            load_second_stage(raw_wk, wk_w, 0, 4)
+            load_second_stage(raw_wk, wk_w, 1, 4)
+            nc.sync.dma_start(out=wk_bias[:], in_=wk_b.partition_broadcast(P))
+            load_second_stage(raw_wk, wk_w, 1, 2)
+
+            picked = [None] * ROWS
+            for r in range(ROWS):
+                picked[r] = banks.tile([P, UNIT], BF16, tag="bank", name="picked")
+                nc.tensor.matmul(
+                    out=picked[r][:], lhsT=ident_bf[:, r : r + 1].to_broadcast([P, P]), rhs=vec_rows[:],
+                    start=True, stop=True,
+                )
+
+            def spread_row(r):
+                nc.vector.tensor_copy(out=spread[:, r, :], in_=picked[r][:])
 
             for b in range(BATCH):
                 tiles = slice(b * SEQ_TILES, (b + 1) * SEQ_TILES)
-                nc.vector.tensor_copy(
+                nc.gpsimd.tensor_copy(
                     out=cos_pair[:, tiles, :].rearrange("p a (j e) -> p a j e", e=2),
                     in_=cos_sin[:, 0].unsqueeze(3).to_broadcast([P, SEQ_TILES, ROPE // 2, 2]),
                 )
-                nc.vector.tensor_copy(out=sin_plus[:, tiles, :], in_=cos_sin[:, 1])
-                nc.vector.tensor_scalar(
+                nc.gpsimd.tensor_copy(out=sin_plus[:, tiles, :], in_=cos_sin[:, 1])
+                nc.gpsimd.tensor_scalar(
                     out=sin_minus[:, tiles, :], in0=cos_sin[:, 1], scalar1=-1.0, scalar2=None, op0=ALU.mult
                 )
 
-            waiting = []
-            for pair in range(TOKEN_TILES // 2):
-                for g in range(PASSES):
-                    turned = banks.tile([P, 2, 2, P], F32, tag="bank")
+            latent_codes = a_pool.tile([P, PASSES, UNIT], U32, align_bytes=64, tag="a_codes")
+            latent_scales = a_pool.tile([P, PASSES, UNIT], U8, align_bytes=64, tag="a_scales")
+            latent_grouped = [None] * PASSES
+            latent_sums = [None] * TOKEN_TILES
+            x_grouped = [None] * TOKEN_TILES
+
+            def regroup_latent(g, on_vector):
+                latent_grouped[g] = stage.tile([P, UNIT * PACK], BF16, align_bytes=64, tag="grouped", name="grouped")
+                regroup(nc, on_vector, latent_grouped[g][:], raw_latent[:, g, :, :])
+
+            def quantise_latent(g):
+                quantise(nc, latent_grouped[g][:], latent_codes[:, g, :], latent_scales[:, g, :])
+
+            def turn_x(tt, on_vector):
+                words = x_sb[:, tt, :].bitcast(F32)
+                x_grouped[tt] = x_staging.tile([P, PASSES * P * PACK], BF16, align_bytes=64, tag="x_grouped", name="x_grouped")
+                out_words = x_grouped[tt][:].bitcast(F32).rearrange("p (g k u) -> p g k u", g=PASSES, u=2)
+                for half in range(2):
+                    turned = banks.tile([P, 2, 2, P], F32, tag="bank", name="turned")
                     for i in range(2):
-                        words = x_sb[:, 2 * pair + i, :].bitcast(F32)
                         for u in range(2):
-                            col0 = (2 * g + u) * P
+                            col0 = (2 * (2 * half + i) + u) * P
                             nc.tensor.transpose(turned[:, i, u, :], words[:, col0 : col0 + P], ident_f32[:])
-                    x_grouped = x_staging.tile([P, 2 * P * PACK], BF16, align_bytes=64)
                     copy(
-                        nc,
-                        g % 2 == 1,
-                        x_grouped[:].bitcast(F32).rearrange("p (i k u) -> p i k u", i=2, u=2),
+                        nc, on_vector, out_words[:, 2 * half : 2 * half + 2, :, :],
                         turned[:].rearrange("p i u k -> p i k u"),
                     )
-                    cols = slice(pair * 2 * P, (pair + 1) * 2 * P)
-                    waiting.append((x_grouped, x_codes[:, g, cols], x_scales[:, g, cols]))
-                    if len(waiting) > 1:
-                        quantise(nc, *waiting[-2])
-            quantise(nc, *waiting[-1])
+
+            def quantise_x(tt):
+                quantise(nc, x_grouped[tt][:], x_codes[:, tt, :], x_scales[:, tt, :])
+
+            def open_latent(tt):
+                latent_sums[tt] = banks.tile([P, UNIT], F32, tag="bank", name="latent_sum")
+
+            def multiply_latent(tt, passes):
+                for g in passes:
+                    tokens = slice(g * P, (g + 1) * P)
+                    nc.tensor.matmul_mx(
+                        out=latent_sums[tt][:],
+                        lhsT=x_codes[:, tt, tokens].bitcast(FP8X4),
+                        lhsT_scale=x_scales[:, tt, tokens],
+                        rhs=latent_codes[:, g, :].bitcast(FP8X4),
+                        rhs_scale=latent_scales[:, g, :],
+                        start=g == 0,
+                        stop=g == PASSES - 1,
+                    )
+
+            regroup_latent(0, True)
+            regroup_latent(1, False)
+            spread_row(ROW_LATENT_BIAS)
+            turn_x(0, False)
+            quantise_latent(0)
+            regroup_latent(2, True)
+            spread_row(ROW_GAIN)
+            quantise_latent(1)
+            turn_x(1, False)
+            quantise_latent(2)
+            turn_x(2, False)
+            regroup_latent(3, True)
+            quantise_x(0)
+            open_latent(0)
+            multiply_latent(0, (0, 1, 2))
+            quantise_x(1)
+            turn_x(3, False)
+            quantise_latent(3)
+            multiply_latent(0, (3,))
+            open_latent(1)
+            multiply_latent(1, (0, 1, 2, 3))
+            spread_row(ROW_SHIFT)
+            quantise_x(2)
+            open_latent(2)
+            multiply_latent(2, (0, 1, 2, 3))
+            quantise_x(3)
+            open_latent(3)
+            multiply_latent(3, (0, 1, 2, 3))
 
         late = ctx.enter_context(tc.tile_pool(name="late", bufs=1, reuse_waits="tile"))
+        outs = ctx.enter_context(tc.tile_pool(name="outs", bufs=5, reuse_waits="tile"))
+        scratch = ctx.enter_context(tc.tile_pool(name="scratch", bufs=3, reuse_waits="tile"))
         raw_wv = late.tile([P, PACK, NOPE_COLS], BF16)
-        load_second_stage(raw_wv, wv_w)
-
-        def multiply(sums, lhs_codes, lhs_scales, codes, scales, first, last):
-            for tt in range(TOKEN_TILES):
-                tokens = slice(tt * P, (tt + 1) * P)
-                nc.tensor.matmul_mx(
-                    out=sums[tt][:],
-                    lhsT=lhs_codes[:, tokens].bitcast(FP8X4),
-                    lhsT_scale=lhs_scales[:, tokens],
-                    rhs=codes.bitcast(FP8X4),
-                    rhs_scale=scales,
-                    start=first,
-                    stop=last,
-                )
-
-        def four_banks():
-            return [banks.tile([P, UNIT], F32, tag="bank", name="sum%d" % tt) for tt in range(TOKEN_TILES)]
+        load_second_stage(raw_wv, wv_w, 0, 2)
+        nc.sync.dma_start(out=rope_bias[:], in_=wkv_a_b[:ROPE_COLS].partition_broadcast(P))
+        nc.sync.dma_start(out=wv_bias[:], in_=wv_b.partition_broadcast(P))
+        for g in range(PASSES):
+            load_first_stage(raw_rope, g, 0, ROPE_COLS)
+        load_second_stage(raw_wv, wv_w, 1, 2)
 
         def k_rope_unit(i):
             return {
                 "rows": [raw_rope[:, g, :, i * UNIT : (i + 1) * UNIT] for g in range(PASSES)],
-                "bias": ROW_ROPE_BIAS + i,
+                "bias": rope_bias[:, i * UNIT : (i + 1) * UNIT],
                 "flat_unit": NOPE_COLS // UNIT + i,
                 "dest": k_flat[:, NOPE_COLS + i * UNIT : NOPE_COLS + (i + 1) * UNIT],
             }
 
-        def second_stage_unit(raw_tile, bias_row, flat, i, rotated):
+        def second_stage_unit(raw_tile, bias, flat, i, rotated):
             return {
                 "rows": [raw_tile[:, :, i * UNIT : (i + 1) * UNIT]],
-                "bias": bias_row + i,
+                "bias": bias[:, i * UNIT : (i + 1) * UNIT],
                 "flat_unit": i if rotated else None,
                 "dest": flat[:, i * UNIT : (i + 1) * UNIT],
             }
 
-        wk_units = [second_stage_unit(raw_wk, ROW_WK_BIAS, k_flat, i, True) for i in range(NOPE_COLS // UNIT)]
-        wv_units = [second_stage_unit(raw_wv, ROW_WV_BIAS, v_flat, i, False) for i in range(NOPE_COLS // UNIT)]
-        units = wk_units + [k_rope_unit(0)] + wv_units[:2] + [k_rope_unit(1)] + wv_units[2:]
+        wk_units = [second_stage_unit(raw_wk, wk_bias, k_flat, i, True) for i in range(NOPE_COLS // UNIT)]
+        wv_units = [second_stage_unit(raw_wv, wv_bias, v_flat, i, False) for i in range(NOPE_COLS // UNIT)]
+        units = wk_units + wv_units[:1] + [k_rope_unit(0)] + wv_units[1:2] + [k_rope_unit(1)] + wv_units[2:]
         pieces = [(n, g) for n in range(len(units)) for g in range(len(units[n]["rows"]))]
         grouped_of = {}
+        regrouped = []
+        quantised = []
 
-        def regroup_piece(j):
+        def regroup_next(halves=(0, 1)):
+            j = len(regrouped)
             if j < len(pieces):
                 n, g = pieces[j]
-                grouped_of[j] = regroup(nc, stage, False, units[n]["rows"][g])
+                if j not in grouped_of:
+                    grouped_of[j] = stage.tile([P, UNIT * PACK], BF16, align_bytes=64, tag="grouped", name="grouped")
+                if len(halves) == 2:
+                    regroup(nc, False, grouped_of[j][:], units[n]["rows"][g])
+                else:
+                    h = halves[0]
+                    width = UNIT // 2
+                    regroup(
+                        nc, False, grouped_of[j][:, h * width * PACK : (h + 1) * width * PACK],
+                        units[n]["rows"][g][:, :, h * width : (h + 1) * width],
+                    )
+                if 1 in halves:
+                    regrouped.append(j)
 
-        def quantise_piece(j):
+        def quantise_next():
+            j = len(quantised)
             if j < len(pieces):
                 n, g = pieces[j]
                 if g == 0:
@@ -250,136 +317,158 @@ def tile_mla_pa_kernel(
                     pool, tag = (a_pool, "a") if count == PASSES else (w_pool, "w")
                     units[n]["codes"] = pool.tile([P, count, UNIT], U32, align_bytes=64, tag=tag + "_codes", name="codes")
                     units[n]["scales"] = pool.tile([P, count, UNIT], U8, align_bytes=64, tag=tag + "_scales", name="scales")
-                quantise(nc, grouped_of[j], units[n]["codes"][:, g, :], units[n]["scales"][:, g, :])
+                quantise(nc, grouped_of[j][:], units[n]["codes"][:, g, :], units[n]["scales"][:, g, :])
+                quantised.append(j)
 
-        latent_codes = a_pool.tile([P, PASSES, UNIT], U32, align_bytes=64, tag="a_codes")
-        latent_scales = a_pool.tile([P, PASSES, UNIT], U8, align_bytes=64, tag="a_scales")
-        latent_sums = four_banks()
-        latent_grouped = [None] * PASSES
-        for g in range(0, PASSES, 2):
-            latent_grouped[g] = regroup(nc, stage, False, raw_latent[:, g, :, :])
-            latent_grouped[g + 1] = regroup(nc, stage, True, raw_latent[:, g + 1, :, :])
-            for h in (g, g + 1):
-                quantise(nc, latent_grouped[h], latent_codes[:, h, :], latent_scales[:, h, :])
-                multiply(
-                    latent_sums, x_codes[:, h, :], x_scales[:, h, :], latent_codes[:, h, :], latent_scales[:, h, :],
-                    h == 0, h == PASSES - 1,
-                )
-        regroup_piece(0)
-        regroup_piece(1)
-
-        c_all = keep.tile([P, TOKEN_TILES, RANK], F32)
-        c_sum = keep.tile([P, TOKEN_TILES], F32)
-        minus_mean = keep.tile([P, TOKEN_TILES], F32)
-        square_sum = keep.tile([P, TOKEN_TILES], F32)
-        for tt in range(TOKEN_TILES):
-            one_tile = slice(tt, tt + 1)
+        def add_latent_bias(tt):
             nc.vector.scalar_tensor_tensor(
-                out=c_all[:, tt, :],
-                in0=latent_sums[tt][:],
-                scalar=1.0,
-                in1=spread[:, ROW_LATENT_BIAS, :],
-                op0=ALU.mult,
-                op1=ALU.add,
-                accum_out=c_sum[:, one_tile],
+                out=c_all[:, tt, :], in0=latent_sums[tt][:], scalar=1.0, in1=spread[:, ROW_LATENT_BIAS, :],
+                op0=ALU.mult, op1=ALU.add, accum_out=c_sum[:, tt : tt + 1],
             )
-            nc.vector.tensor_scalar(
-                out=minus_mean[:, one_tile], in0=c_sum[:, one_tile], scalar1=-1.0 / RANK, scalar2=None, op0=ALU.mult
-            )
-            squares = norm.tile([P, RANK], BF16, tag="squares")
+
+        def statistics(tt):
+            one_tile = slice(tt, tt + 1)
+            nc.scalar.mul(out=minus_mean[:, one_tile], in_=c_sum[:, one_tile], mul=-1.0 / RANK)
+            squares = norm.tile([P, RANK], BF16, tag="squares", name="squares")
             nc.scalar.activation(
-                out=squares[:],
-                in_=c_all[:, tt, :],
-                func=ACT.Square,
-                bias=minus_mean[:, one_tile],
-                scale=1.0,
+                out=squares[:], in_=c_all[:, tt, :], func=ACT.Square, bias=minus_mean[:, one_tile], scale=1.0,
                 accum_out=square_sum[:, one_tile],
             )
-        quantise_piece(0)
-        deviation = keep.tile([P, TOKEN_TILES], F32)
-        nc.vector.tensor_scalar(
-            out=deviation[:], in0=square_sum[:], scalar1=1.0 / RANK, scalar2=EPS, op0=ALU.mult, op1=ALU.add
-        )
-        nc.scalar.sqrt(out=deviation[:], in_=deviation[:])
-        regroup_piece(2)
-        inv_std = keep.tile([P, TOKEN_TILES], F32)
-        nc.vector.reciprocal(out=inv_std[:], in_=deviation[:])
+            nc.scalar.activation(
+                out=inv_std[:, one_tile], in_=square_sum[:, one_tile], func=ACT.Abs_reciprocal_sqrt, bias=eps[:],
+                scale=1.0 / RANK,
+            )
 
-        cn_codes = keep.tile([P, TOKENS], U32, align_bytes=64)
-        cn_scales = keep.tile([P, TOKENS], U8, align_bytes=64)
-        cn = keep.tile([P, TOKEN_TILES, RANK], BF16)
-        cn_waiting = []
-        for tt in range(TOKEN_TILES):
-            gained = norm.tile([P, RANK], F32, tag="gained")
+        gained_of = {}
+
+        def apply_gain(tt):
+            gained_of[tt] = norm.tile([P, RANK], F32, tag="gained", name="gained")
             nc.vector.scalar_tensor_tensor(
-                out=gained[:],
-                in0=c_all[:, tt, :],
-                scalar=minus_mean[:, tt : tt + 1],
-                in1=spread[:, ROW_GAIN, :],
-                op0=ALU.add,
-                op1=ALU.mult,
+                out=gained_of[tt][:], in0=c_all[:, tt, :], scalar=minus_mean[:, tt : tt + 1],
+                in1=spread[:, ROW_GAIN, :], op0=ALU.add, op1=ALU.mult,
             )
+
+        def apply_shift(tt):
             nc.vector.scalar_tensor_tensor(
-                out=cn[:, tt, :],
-                in0=gained[:],
-                scalar=inv_std[:, tt : tt + 1],
-                in1=spread[:, ROW_SHIFT, :],
-                op0=ALU.mult,
-                op1=ALU.add,
+                out=cn[:, tt, :], in0=gained_of[tt][:], scalar=inv_std[:, tt : tt + 1],
+                in1=spread[:, ROW_SHIFT, :], op0=ALU.mult, op1=ALU.add,
             )
-            cn_turned = banks.tile([P, PACK, P], BF16, tag="bank")
+
+        cn_grouped_of = {}
+
+        def turn_cn(tt):
+            cn_turned = banks.tile([P, PACK, P], BF16, tag="bank", name="cn_turned")
             for t in range(PACK):
                 nc.tensor.transpose(cn_turned[:, t, :], cn[:, tt, t * P : (t + 1) * P], ident_bf[:])
-            cn_grouped = norm.tile([P, P * PACK], BF16, align_bytes=64, tag="cn_grouped")
+            cn_grouped_of[tt] = norm.tile([P, P * PACK], BF16, align_bytes=64, tag="cn_grouped", name="cn_grouped")
             nc.scalar.copy(
-                out=cn_grouped[:].rearrange("p (k t) -> p k t", t=PACK), in_=cn_turned[:].rearrange("p t k -> p k t")
+                out=cn_grouped_of[tt][:].rearrange("p (k t) -> p k t", t=PACK),
+                in_=cn_turned[:].rearrange("p t k -> p k t"),
             )
+
+        def quantise_cn(tt):
             tokens = slice(tt * P, (tt + 1) * P)
-            cn_waiting.append((cn_grouped, cn_codes[:, tokens], cn_scales[:, tokens]))
-            if tt > 0:
-                quantise(nc, *cn_waiting[tt - 1])
-        quantise_piece(1)
-        quantise(nc, *cn_waiting[-1])
-        regroup_piece(3)
+            quantise(nc, cn_grouped_of[tt][:], cn_codes[:, tokens], cn_scales[:, tokens])
+
+        def one_pass(unit, tt, g, last):
+            if len(unit["rows"]) == PASSES:
+                tokens = slice(g * P, (g + 1) * P)
+                lhs_codes, lhs_scales = x_codes[:, tt, tokens], x_scales[:, tt, tokens]
+            else:
+                tokens = slice(tt * P, (tt + 1) * P)
+                lhs_codes, lhs_scales = cn_codes[:, tokens], cn_scales[:, tokens]
+            nc.tensor.matmul_mx(
+                out=unit["sums"][tt][:],
+                lhsT=lhs_codes.bitcast(FP8X4),
+                lhsT_scale=lhs_scales,
+                rhs=unit["codes"][:, g, :].bitcast(FP8X4),
+                rhs_scale=unit["scales"][:, g, :],
+                start=g == 0,
+                stop=last,
+            )
+
+        def open_banks(n):
+            units[n]["sums"] = [banks.tile([P, UNIT], F32, tag="bank", name="sum%d" % tt) for tt in range(TOKEN_TILES)]
 
         def multiply_unit(n):
-            unit = units[n]
-            unit["sums"] = four_banks()
-            count = len(unit["rows"])
+            open_banks(n)
+            count = len(units[n]["rows"])
             for g in range(count):
-                if count == PASSES:
-                    lhs_codes, lhs_scales = x_codes[:, g, :], x_scales[:, g, :]
-                else:
-                    lhs_codes, lhs_scales = cn_codes[:], cn_scales[:]
-                multiply(
-                    unit["sums"], lhs_codes, lhs_scales, unit["codes"][:, g, :], unit["scales"][:, g, :],
-                    g == 0, g == count - 1,
-                )
+                for tt in range(TOKEN_TILES):
+                    one_pass(units[n], tt, g, g == count - 1)
 
         def store(unit, tiles):
             nc.sync.dma_start(out=unit["dest"].rearrange("(t p) c -> p t c", p=P)[:, tiles, :], in_=unit["out"][:, tiles, :])
 
-        multiply_unit(0)
-        for n in range(len(units)):
+        def add_bias(n, tt):
+            nc.vector.tensor_tensor(
+                out=units[n]["out"][:, tt, :], in0=units[n]["sums"][tt][:], in1=units[n]["bias"], op=ALU.add
+            )
+
+        add_latent_bias(0)
+        regroup_next((0,))
+        statistics(0)
+        add_latent_bias(1)
+        statistics(1)
+        add_latent_bias(2)
+        statistics(2)
+        apply_gain(0)
+        add_latent_bias(3)
+        statistics(3)
+        apply_shift(0)
+        turn_cn(0)
+        apply_gain(1)
+        apply_shift(1)
+        turn_cn(1)
+        regroup_next((1,))
+        apply_gain(2)
+        quantise_cn(0)
+        apply_shift(2)
+        turn_cn(2)
+        apply_gain(3)
+        quantise_cn(1)
+        apply_shift(3)
+        turn_cn(3)
+        quantise_next()
+        quantise_cn(2)
+        regroup_next()
+        quantise_cn(3)
+
+        def unit_adds(n):
             unit = units[n]
-            if n + 1 < len(units):
-                multiply_unit(n + 1)
-            regroup_piece(PIECES_REGROUPED_AHEAD + 2 * n)
-            regroup_piece(PIECES_REGROUPED_AHEAD + 2 * n + 1)
             unit["out"] = outs.tile([P, TOKEN_TILES, UNIT], F32, tag="unit_out", name="unit_out")
             for tt in range(TOKEN_TILES):
-                nc.vector.tensor_tensor(
-                    out=unit["out"][:, tt, :], in0=unit["sums"][tt][:], in1=spread[:, unit["bias"], :], op=ALU.add
-                )
+                if tt == 2 and n + 1 < len(units):
+                    quantise_upto(pieces_of(n + 2))
+                    multiply_unit(n + 1)
+                add_bias(n, tt)
                 if unit["flat_unit"] is None and tt % 2 == 1:
                     store(unit, slice(tt - 1, tt + 1))
             if unit["flat_unit"] is not None:
                 unit["add"] = rotate_products(
                     nc, scratch, unit["out"][:], (2 - 8 * unit["flat_unit"]) % 3, cos_pair[:], sin_minus[:], sin_plus[:]
                 )
-            if n >= ADD_LAG and units[n - ADD_LAG]["flat_unit"] is not None:
-                pairs, crossed = units[n - ADD_LAG]["add"]
+
+        def finish(n):
+            if n >= 0 and units[n]["flat_unit"] is not None:
+                pairs, crossed = units[n]["add"]
                 nc.vector.tensor_tensor(out=pairs, in0=pairs, in1=crossed, op=ALU.add)
-                store(units[n - ADD_LAG], slice(0, TOKEN_TILES))
-            quantise_piece(PIECES_QUANTISED_AHEAD + 2 * n)
-            quantise_piece(PIECES_QUANTISED_AHEAD + 2 * n + 1)
+                store(units[n], slice(0, TOKEN_TILES))
+
+        def quantise_upto(count):
+            while len(quantised) < min(count, len(pieces)):
+                while len(regrouped) <= len(quantised):
+                    regroup_next()
+                quantise_next()
+
+        def pieces_of(n):
+            return sum(len(u["rows"]) for u in units[:n])
+
+        multiply_unit(0)
+        for n in range(len(units)):
+            unit_adds(n)
+            if n + 2 < len(units):
+                quantise_upto(pieces_of(n + 2) + len(units[n + 2]["rows"]) // 2)
+            finish(n - ADD_LAG)
+        for n in range(len(units) - ADD_LAG, len(units)):
+            finish(n)

@@ -26,7 +26,10 @@ NOPE_COLS = HEADS * NOPE
 EPS = 1e-5
 FLOPS = 2 * TOKENS * DIM * (ROPE_COLS + RANK) + 2 * 2 * TOKENS * RANK * NOPE_COLS
 
-ROW_LATENT_BIAS, ROW_GAIN, ROW_SHIFT, ROWS = 0, 1, 2, 3
+ROW_LATENT_BIAS, ROW_GAIN, ROW_SHIFT, ROW_WK_BIAS, ROW_ROPE_BIAS, ROW_WV_BIAS, ROWS = 0, 1, 2, 4, 8, 10, 14
+
+WK_CHUNKS = (512, 512, 1024)
+WV_CHUNKS = (1024, 1024)
 
 ADD_LAG = 2
 
@@ -95,14 +98,11 @@ def tile_mla_pa_kernel(
         eps = const.tile([P, 1], F32)
         first = const.tile([P, 1], F32)
         spread = const.tile([P, ROWS, UNIT], BF16)
-        wk_bias = const.tile([P, NOPE_COLS], BF16)
-        wv_bias = const.tile([P, NOPE_COLS], BF16)
-        rope_bias = const.tile([P, ROPE_COLS], BF16)
         cos_pair = const.tile([P, TOKEN_TILES, ROPE], F32)
         sin_plus = const.tile([P, TOKEN_TILES, ROPE // 2], F32)
         sin_minus = const.tile([P, TOKEN_TILES, ROPE // 2], F32)
-        raw_wk = raw.tile([P, PACK, NOPE_COLS], BF16)
-        raw_rope = raw.tile([P, PASSES, PACK, ROPE_COLS], BF16)
+        raw_wk = [raw.tile([P, PACK, width], BF16, tag="raw_wk%d" % c, name="raw_wk") for c, width in enumerate(WK_CHUNKS)]
+        raw_rope = [raw.tile([P, PACK, ROPE_COLS], BF16, tag="raw_rope%d" % g, name="raw_rope") for g in range(PASSES)]
         x_codes = keep.tile([P, TOKEN_TILES, PASSES * P], U32, align_bytes=64)
         x_scales = keep.tile([P, TOKEN_TILES, PASSES * P], U8, align_bytes=64)
         c_all = keep.tile([P, TOKEN_TILES, RANK], F32)
@@ -114,12 +114,19 @@ def tile_mla_pa_kernel(
         cn_codes = keep.tile([P, TOKENS], U32, align_bytes=64)
         cn_scales = keep.tile([P, TOKENS], U8, align_bytes=64)
 
-        nc.vector.memset(vec_rows[:], 0.0)
+        nc.vector.memset(vec_rows[:].bitcast(U32), 0)
         nc.vector.memset(eps[:], EPS)
         make_identity(nc, ident_f32[:])
         make_identity(nc, ident_bf[:])
-        for row, vector in ((ROW_LATENT_BIAS, wkv_a_b[ROPE_COLS:]), (ROW_GAIN, kvn_g), (ROW_SHIFT, kvn_b)):
-            nc.scalar.dma_start(out=vec_rows[row : row + 1, :], in_=vector.rearrange("(r c) -> r c", c=UNIT))
+        for row, count, vector in (
+            (ROW_LATENT_BIAS, 1, wkv_a_b[ROPE_COLS:]),
+            (ROW_GAIN, 1, kvn_g),
+            (ROW_SHIFT, 1, kvn_b),
+            (ROW_WK_BIAS, 4, wk_b),
+            (ROW_ROPE_BIAS, 2, wkv_a_b[:ROPE_COLS]),
+            (ROW_WV_BIAS, 4, wv_b),
+        ):
+            nc.sync.dma_start(out=vec_rows[row : row + count, :], in_=vector.rearrange("(r c) -> r c", c=UNIT))
         nc.scalar.dma_start(out=cos_sin[:, 0], in_=cos.rearrange("(a p) j -> p a j", p=P))
         nc.scalar.dma_start(out=cos_sin[:, 1], in_=sin.rearrange("(a p) j -> p a j", p=P))
         nc.scalar.activation(out=first[:], in_=eps[:], func=ACT.Abs_reciprocal_sqrt, bias=eps[:], scale=1.0)
@@ -128,45 +135,44 @@ def tile_mla_pa_kernel(
             for u in range(2):
                 row0 = g * K_PASS + u * 2 * P
                 nc.sync.dma_start(
-                    out=tile_[:, g, 2 * u : 2 * u + 2, :],
+                    out=tile_[:, 2 * u : 2 * u + 2, :],
                     in_=wkv_a_w[row0 : row0 + 2 * P, col0 : col0 + width].rearrange("(q e) c -> q e c", e=2),
                 )
 
-        def load_second_stage(tile_, weight, part, parts):
-            view = weight.rearrange("(t p) n -> p t n", p=P)
-            cols = slice(part * NOPE_COLS // parts, (part + 1) * NOPE_COLS // parts)
-            nc.sync.dma_start(out=tile_[:, :, cols], in_=view[:, :, cols])
+        def load_second_stage(tile_, weight, col0, width):
+            nc.sync.dma_start(out=tile_[:], in_=weight[:, col0 : col0 + width].rearrange("(t p) n -> p t n", p=P))
 
         with tc.tile_pool(name="head", bufs=1) as head, tc.tile_pool(name="x_staging", bufs=4) as x_staging:
             x_sb = head.tile([P, TOKEN_TILES, DIM], BF16)
-            raw_latent = head.tile([P, PASSES, PACK, RANK], BF16)
+            raw_latent = [head.tile([P, PACK, RANK], BF16, tag="raw_latent%d" % g, name="raw_latent") for g in range(PASSES)]
 
             def load_x(tt):
                 nc.sync.dma_start(out=x_sb[:, tt, :], in_=x_rows[tt * P : (tt + 1) * P, :])
 
-            load_first_stage(raw_latent, 0, ROPE_COLS, RANK)
-            load_first_stage(raw_latent, 1, ROPE_COLS, RANK)
+            load_first_stage(raw_latent[0], 0, ROPE_COLS, RANK)
+            load_first_stage(raw_latent[1], 1, ROPE_COLS, RANK)
             load_x(0)
-            load_first_stage(raw_latent, 2, ROPE_COLS, RANK)
+            load_first_stage(raw_latent[2], 2, ROPE_COLS, RANK)
             load_x(1)
-            load_first_stage(raw_latent, 3, ROPE_COLS, RANK)
+            load_first_stage(raw_latent[3], 3, ROPE_COLS, RANK)
             load_x(2)
             load_x(3)
-            load_second_stage(raw_wk, wk_w, 0, 4)
-            load_second_stage(raw_wk, wk_w, 1, 4)
-            nc.sync.dma_start(out=wk_bias[:], in_=wk_b.partition_broadcast(P))
-            load_second_stage(raw_wk, wk_w, 1, 2)
+            for c, width in enumerate(WK_CHUNKS):
+                load_second_stage(raw_wk[c], wk_w, sum(WK_CHUNKS[:c]), width)
 
-            picked = [None] * ROWS
-            for r in range(ROWS):
-                picked[r] = banks.tile([P, UNIT], BF16, tag="bank", name="picked")
-                nc.tensor.matmul(
-                    out=picked[r][:], lhsT=ident_bf[:, r : r + 1].to_broadcast([P, P]), rhs=vec_rows[:],
-                    start=True, stop=True,
-                )
+            picked = {}
 
-            def spread_row(r):
-                nc.vector.tensor_copy(out=spread[:, r, :], in_=picked[r][:])
+            def pick_rows(r, count):
+                picked[r] = banks.tile([P, count, UNIT], BF16, tag="bank", name="picked")
+                for i in range(count):
+                    nc.tensor.matmul(
+                        out=picked[r][:, i, :], lhsT=ident_bf[:, r + i : r + i + 1].to_broadcast([P, P]), rhs=vec_rows[:],
+                        start=True, stop=True,
+                    )
+
+            def spread_rows(r, on_vector):
+                bank = picked[r]
+                copy(nc, on_vector, spread[:, r : r + bank.shape[1], :], bank[:])
 
             for b in range(BATCH):
                 tiles = slice(b * SEQ_TILES, (b + 1) * SEQ_TILES)
@@ -187,7 +193,7 @@ def tile_mla_pa_kernel(
 
             def regroup_latent(g, on_vector):
                 latent_grouped[g] = stage.tile([P, UNIT * PACK], BF16, align_bytes=64, tag="grouped", name="grouped")
-                regroup(nc, on_vector, latent_grouped[g][:], raw_latent[:, g, :, :])
+                regroup(nc, on_vector, latent_grouped[g][:], raw_latent[g][:])
 
             def quantise_latent(g):
                 quantise(nc, latent_grouped[g][:], latent_codes[:, g, :], latent_scales[:, g, :])
@@ -226,16 +232,24 @@ def tile_mla_pa_kernel(
                         stop=g == PASSES - 1,
                     )
 
+            pick_rows(ROW_LATENT_BIAS, 2)
+            pick_rows(ROW_SHIFT, 1)
+            pick_rows(ROW_WK_BIAS, 2)
+            pick_rows(ROW_WK_BIAS + 2, 2)
             regroup_latent(0, True)
             regroup_latent(1, False)
-            spread_row(ROW_LATENT_BIAS)
+            spread_rows(ROW_LATENT_BIAS, True)
             turn_x(0, False)
             quantise_latent(0)
+            spread_rows(ROW_SHIFT, True)
+            spread_rows(ROW_WK_BIAS, True)
+            pick_rows(ROW_ROPE_BIAS, 2)
             regroup_latent(2, True)
-            spread_row(ROW_GAIN)
+            spread_rows(ROW_WK_BIAS + 2, True)
             quantise_latent(1)
             turn_x(1, False)
             quantise_latent(2)
+            pick_rows(ROW_WV_BIAS, 2)
             turn_x(2, False)
             regroup_latent(3, True)
             quantise_x(0)
@@ -247,7 +261,6 @@ def tile_mla_pa_kernel(
             multiply_latent(0, (3,))
             open_latent(1)
             multiply_latent(1, (0, 1, 2, 3))
-            spread_row(ROW_SHIFT)
             quantise_x(2)
             open_latent(2)
             multiply_latent(2, (0, 1, 2, 3))
@@ -258,32 +271,32 @@ def tile_mla_pa_kernel(
         late = ctx.enter_context(tc.tile_pool(name="late", bufs=1, reuse_waits="tile"))
         outs = ctx.enter_context(tc.tile_pool(name="outs", bufs=5, reuse_waits="tile"))
         scratch = ctx.enter_context(tc.tile_pool(name="scratch", bufs=3, reuse_waits="tile"))
-        raw_wv = late.tile([P, PACK, NOPE_COLS], BF16)
-        load_second_stage(raw_wv, wv_w, 0, 2)
-        nc.sync.dma_start(out=rope_bias[:], in_=wkv_a_b[:ROPE_COLS].partition_broadcast(P))
-        nc.sync.dma_start(out=wv_bias[:], in_=wv_b.partition_broadcast(P))
+        raw_wv = [late.tile([P, PACK, width], BF16, tag="raw_wv%d" % c, name="raw_wv") for c, width in enumerate(WV_CHUNKS)]
+        load_second_stage(raw_wv[0], wv_w, 0, WV_CHUNKS[0])
         for g in range(PASSES):
-            load_first_stage(raw_rope, g, 0, ROPE_COLS)
-        load_second_stage(raw_wv, wv_w, 1, 2)
+            load_first_stage(raw_rope[g], g, 0, ROPE_COLS)
+        load_second_stage(raw_wv[1], wv_w, WV_CHUNKS[0], WV_CHUNKS[1])
 
         def k_rope_unit(i):
             return {
-                "rows": [raw_rope[:, g, :, i * UNIT : (i + 1) * UNIT] for g in range(PASSES)],
-                "bias": rope_bias[:, i * UNIT : (i + 1) * UNIT],
+                "rows": [raw_rope[g][:, :, i * UNIT : (i + 1) * UNIT] for g in range(PASSES)],
+                "bias": spread[:, ROW_ROPE_BIAS + i, :],
                 "flat_unit": NOPE_COLS // UNIT + i,
                 "dest": k_flat[:, NOPE_COLS + i * UNIT : NOPE_COLS + (i + 1) * UNIT],
             }
 
-        def second_stage_unit(raw_tile, bias, flat, i, rotated):
+        def second_stage_unit(tiles, chunks, bias_row, flat, i, rotated):
+            c = max(j for j in range(len(chunks)) if sum(chunks[:j]) <= i * UNIT)
+            col0 = i * UNIT - sum(chunks[:c])
             return {
-                "rows": [raw_tile[:, :, i * UNIT : (i + 1) * UNIT]],
-                "bias": bias[:, i * UNIT : (i + 1) * UNIT],
+                "rows": [tiles[c][:, :, col0 : col0 + UNIT]],
+                "bias": spread[:, bias_row + i, :],
                 "flat_unit": i if rotated else None,
                 "dest": flat[:, i * UNIT : (i + 1) * UNIT],
             }
 
-        wk_units = [second_stage_unit(raw_wk, wk_bias, k_flat, i, True) for i in range(NOPE_COLS // UNIT)]
-        wv_units = [second_stage_unit(raw_wv, wv_bias, v_flat, i, False) for i in range(NOPE_COLS // UNIT)]
+        wk_units = [second_stage_unit(raw_wk, WK_CHUNKS, ROW_WK_BIAS, k_flat, i, True) for i in range(NOPE_COLS // UNIT)]
+        wv_units = [second_stage_unit(raw_wv, WV_CHUNKS, ROW_WV_BIAS, v_flat, i, False) for i in range(NOPE_COLS // UNIT)]
         units = wk_units + wv_units[:1] + [k_rope_unit(0)] + wv_units[1:2] + [k_rope_unit(1)] + wv_units[2:]
         pieces = [(n, g) for n in range(len(units)) for g in range(len(units[n]["rows"]))]
         grouped_of = {}
@@ -429,10 +442,15 @@ def tile_mla_pa_kernel(
         quantise_cn(1)
         apply_shift(3)
         turn_cn(3)
+        pick_rows(ROW_WV_BIAS + 2, 2)
         quantise_next()
         quantise_cn(2)
         regroup_next()
         quantise_cn(3)
+        regroup_next()
+        spread_rows(ROW_WV_BIAS, False)
+        spread_rows(ROW_ROPE_BIAS, False)
+        spread_rows(ROW_WV_BIAS + 2, False)
 
         def unit_adds(n):
             unit = units[n]

@@ -27,6 +27,7 @@ EPS = 1e-5
 FLOPS = 2 * TOKENS * DIM * (ROPE_COLS + RANK) + 2 * 2 * TOKENS * RANK * NOPE_COLS
 
 ROW_LATENT_BIAS, ROW_GAIN, ROW_SHIFT, ROW_WK_BIAS, ROW_ROPE_BIAS, ROW_WV_BIAS, ROWS = 0, 1, 2, 4, 8, 10, 14
+NORM_ROWS = 3
 
 WK_CHUNKS = (512, 512, 1024)
 WV_CHUNKS = (1024, 1024)
@@ -34,17 +35,19 @@ WV_CHUNKS = (1024, 1024)
 ADD_LAG = 2
 
 
-def copy(nc, on_vector, out, in_):
-    if on_vector:
+def copy(nc, engine, out, in_):
+    if engine == "vector":
         nc.vector.tensor_copy(out=out, in_=in_)
-    else:
+    elif engine == "scalar":
         nc.scalar.copy(out=out, in_=in_)
+    else:
+        nc.gpsimd.tensor_scalar(out=out, in0=in_, scalar1=1.0, scalar2=0.0, op0=ALU.mult, op1=ALU.add)
 
 
-def regroup(nc, on_vector, grouped, rows):
+def regroup(nc, engine, grouped, rows):
     copy(
         nc,
-        on_vector,
+        engine,
         grouped.rearrange("p (c i t) -> p c t i", i=4, t=PACK),
         rows.rearrange("p t (c i) -> p c t i", i=4),
     )
@@ -58,8 +61,9 @@ def rotate_products(nc, scratch, unit_out, first_block, cos_pair, sin_minus, sin
     blocks = unit_out.rearrange("p t (k d) -> p t k d", d=ROPE)[:, :, first_block::3, :]
     n = blocks.shape[2]
     pairs = blocks.rearrange("p t n (j e) -> p t n j e", e=2)
-    half = [P, TOKEN_TILES, n, ROPE // 2]
-    crossed = scratch.tile([P, 2, TOKEN_TILES, n, ROPE // 2], F32, tag="crossed")
+    tiles = blocks.shape[1]
+    half = [P, tiles, n, ROPE // 2]
+    crossed = scratch.tile([P, 2, tiles, n, ROPE // 2], F32, tag="crossed")
     nc.gpsimd.tensor_tensor(
         out=crossed[:, 0], in0=pairs[:, :, :, :, 1], in1=sin_minus.unsqueeze(2).to_broadcast(half), op=ALU.mult
     )
@@ -67,7 +71,7 @@ def rotate_products(nc, scratch, unit_out, first_block, cos_pair, sin_minus, sin
         out=crossed[:, 1], in0=pairs[:, :, :, :, 0], in1=sin_plus.unsqueeze(2).to_broadcast(half), op=ALU.mult
     )
     nc.gpsimd.tensor_tensor(
-        out=blocks, in0=blocks, in1=cos_pair.unsqueeze(2).to_broadcast([P, TOKEN_TILES, n, ROPE]), op=ALU.mult
+        out=blocks, in0=blocks, in1=cos_pair.unsqueeze(2).to_broadcast([P, tiles, n, ROPE]), op=ALU.mult
     )
     return pairs, crossed[:].rearrange("p e t n j -> p t n j e")
 
@@ -91,13 +95,15 @@ def tile_mla_pa_kernel(
         norm = ctx.enter_context(tc.tile_pool(name="norm", bufs=2))
         banks = ctx.enter_context(tc.psum_pool(name="banks", bufs=8))
 
-        vec_rows = const.tile([P, UNIT], BF16)
+        norm_rows = const.tile([P, UNIT], BF16)
+        bias_rows = const.tile([P, UNIT], BF16)
         cos_sin = const.tile([P, 2, SEQ_TILES, ROPE // 2], BF16)
         ident_f32 = const.tile([P, P], F32)
         ident_bf = const.tile([P, P], BF16)
         eps = const.tile([P, 1], F32)
         first = const.tile([P, 1], F32)
         spread = const.tile([P, ROWS, UNIT], BF16)
+        norm_cols = const.tile([P, NORM_ROWS, PACK], F32)
         cos_pair = const.tile([P, TOKEN_TILES, ROPE], F32)
         sin_plus = const.tile([P, TOKEN_TILES, ROPE // 2], F32)
         sin_minus = const.tile([P, TOKEN_TILES, ROPE // 2], F32)
@@ -110,25 +116,22 @@ def tile_mla_pa_kernel(
         minus_mean = keep.tile([P, TOKEN_TILES], F32)
         square_sum = keep.tile([P, TOKEN_TILES], F32)
         inv_std = keep.tile([P, TOKEN_TILES], F32)
-        cn = keep.tile([P, TOKEN_TILES, RANK], BF16)
         cn_codes = keep.tile([P, TOKENS], U32, align_bytes=64)
         cn_scales = keep.tile([P, TOKENS], U8, align_bytes=64)
 
-        nc.vector.memset(vec_rows[:].bitcast(U32), 0)
+        nc.vector.memset(norm_rows[:].bitcast(U32), 0)
         nc.vector.memset(eps[:], EPS)
+        nc.vector.memset(bias_rows[:].bitcast(U32), 0)
         make_identity(nc, ident_f32[:])
         make_identity(nc, ident_bf[:])
+        nc.gpsimd.dma_start(out=cos_sin[:, 0], in_=cos.rearrange("(a p) j -> p a j", p=P))
+        nc.gpsimd.dma_start(out=cos_sin[:, 1], in_=sin.rearrange("(a p) j -> p a j", p=P))
         for row, count, vector in (
-            (ROW_LATENT_BIAS, 1, wkv_a_b[ROPE_COLS:]),
-            (ROW_GAIN, 1, kvn_g),
-            (ROW_SHIFT, 1, kvn_b),
             (ROW_WK_BIAS, 4, wk_b),
             (ROW_ROPE_BIAS, 2, wkv_a_b[:ROPE_COLS]),
             (ROW_WV_BIAS, 4, wv_b),
         ):
-            nc.sync.dma_start(out=vec_rows[row : row + count, :], in_=vector.rearrange("(r c) -> r c", c=UNIT))
-        nc.scalar.dma_start(out=cos_sin[:, 0], in_=cos.rearrange("(a p) j -> p a j", p=P))
-        nc.scalar.dma_start(out=cos_sin[:, 1], in_=sin.rearrange("(a p) j -> p a j", p=P))
+            nc.gpsimd.dma_start(out=bias_rows[row : row + count, :], in_=vector.rearrange("(r c) -> r c", c=UNIT))
         nc.scalar.activation(out=first[:], in_=eps[:], func=ACT.Abs_reciprocal_sqrt, bias=eps[:], scale=1.0)
 
         def load_first_stage(tile_, g, col0, width):
@@ -150,13 +153,12 @@ def tile_mla_pa_kernel(
                 nc.sync.dma_start(out=x_sb[:, tt, :], in_=x_rows[tt * P : (tt + 1) * P, :])
 
             load_first_stage(raw_latent[0], 0, ROPE_COLS, RANK)
-            load_first_stage(raw_latent[1], 1, ROPE_COLS, RANK)
-            load_x(0)
-            load_first_stage(raw_latent[2], 2, ROPE_COLS, RANK)
-            load_x(1)
-            load_first_stage(raw_latent[3], 3, ROPE_COLS, RANK)
-            load_x(2)
-            load_x(3)
+            for row, vector in ((ROW_LATENT_BIAS, wkv_a_b[ROPE_COLS:]), (ROW_GAIN, kvn_g), (ROW_SHIFT, kvn_b)):
+                nc.sync.dma_start(out=norm_rows[row : row + 1, :], in_=vector.rearrange("(r c) -> r c", c=UNIT))
+            for g in range(1, PASSES):
+                load_first_stage(raw_latent[g], g, ROPE_COLS, RANK)
+            for tt in range(TOKEN_TILES):
+                load_x(tt)
             for c, width in enumerate(WK_CHUNKS):
                 load_second_stage(raw_wk[c], wk_w, sum(WK_CHUNKS[:c]), width)
 
@@ -166,13 +168,19 @@ def tile_mla_pa_kernel(
                 picked[r] = banks.tile([P, count, UNIT], BF16, tag="bank", name="picked")
                 for i in range(count):
                     nc.tensor.matmul(
-                        out=picked[r][:, i, :], lhsT=ident_bf[:, r + i : r + i + 1].to_broadcast([P, P]), rhs=vec_rows[:],
+                        out=picked[r][:, i, :], lhsT=ident_bf[:, r + i : r + i + 1].to_broadcast([P, P]), rhs=norm_rows[:] if r < NORM_ROWS else bias_rows[:],
                         start=True, stop=True,
                     )
 
-            def spread_rows(r, on_vector):
+            def turn_norm_rows():
+                turned_rows = banks.tile([P, PACK, P], BF16, tag="bank", name="turned_rows")
+                for t in range(PACK):
+                    nc.tensor.transpose(turned_rows[:, t, :], norm_rows[:, t * P : (t + 1) * P], ident_bf[:])
+                nc.vector.tensor_copy(out=norm_cols[:], in_=turned_rows[:, :, :NORM_ROWS].rearrange("p t r -> p r t"))
+
+            def spread_rows(r, engine):
                 bank = picked[r]
-                copy(nc, on_vector, spread[:, r : r + bank.shape[1], :], bank[:])
+                copy(nc, engine, spread[:, r : r + bank.shape[1], :], bank[:])
 
             for b in range(BATCH):
                 tiles = slice(b * SEQ_TILES, (b + 1) * SEQ_TILES)
@@ -191,14 +199,14 @@ def tile_mla_pa_kernel(
             latent_sums = [None] * TOKEN_TILES
             x_grouped = [None] * TOKEN_TILES
 
-            def regroup_latent(g, on_vector):
+            def regroup_latent(g, engine):
                 latent_grouped[g] = stage.tile([P, UNIT * PACK], BF16, align_bytes=64, tag="grouped", name="grouped")
-                regroup(nc, on_vector, latent_grouped[g][:], raw_latent[g][:])
+                regroup(nc, engine, latent_grouped[g][:], raw_latent[g][:])
 
             def quantise_latent(g):
                 quantise(nc, latent_grouped[g][:], latent_codes[:, g, :], latent_scales[:, g, :])
 
-            def turn_x(tt, on_vector):
+            def turn_x(tt, engine):
                 words = x_sb[:, tt, :].bitcast(F32)
                 x_grouped[tt] = x_staging.tile([P, PASSES * P * PACK], BF16, align_bytes=64, tag="x_grouped", name="x_grouped")
                 out_words = x_grouped[tt][:].bitcast(F32).rearrange("p (g k u) -> p g k u", g=PASSES, u=2)
@@ -209,7 +217,7 @@ def tile_mla_pa_kernel(
                             col0 = (2 * (2 * half + i) + u) * P
                             nc.tensor.transpose(turned[:, i, u, :], words[:, col0 : col0 + P], ident_f32[:])
                     copy(
-                        nc, on_vector, out_words[:, 2 * half : 2 * half + 2, :, :],
+                        nc, engine, out_words[:, 2 * half : 2 * half + 2, :, :],
                         turned[:].rearrange("p i u k -> p i k u"),
                     )
 
@@ -232,41 +240,27 @@ def tile_mla_pa_kernel(
                         stop=g == PASSES - 1,
                     )
 
-            pick_rows(ROW_LATENT_BIAS, 2)
-            pick_rows(ROW_SHIFT, 1)
-            pick_rows(ROW_WK_BIAS, 2)
-            pick_rows(ROW_WK_BIAS + 2, 2)
-            regroup_latent(0, True)
-            regroup_latent(1, False)
-            spread_rows(ROW_LATENT_BIAS, True)
-            turn_x(0, False)
+            regroup_latent(0, "vector")
+            pick_rows(ROW_LATENT_BIAS, 1)
+            turn_norm_rows()
+            spread_rows(ROW_LATENT_BIAS, "scalar")
+            regroup_latent(1, "scalar")
             quantise_latent(0)
-            spread_rows(ROW_SHIFT, True)
-            spread_rows(ROW_WK_BIAS, True)
-            pick_rows(ROW_ROPE_BIAS, 2)
-            regroup_latent(2, True)
-            spread_rows(ROW_WK_BIAS + 2, True)
+            regroup_latent(2, "vector")
             quantise_latent(1)
-            turn_x(1, False)
             quantise_latent(2)
-            pick_rows(ROW_WV_BIAS, 2)
-            turn_x(2, False)
-            regroup_latent(3, True)
-            quantise_x(0)
-            open_latent(0)
-            multiply_latent(0, (0, 1, 2))
-            quantise_x(1)
-            turn_x(3, False)
+            regroup_latent(3, "scalar")
+            turn_x(0, "vector")
             quantise_latent(3)
-            multiply_latent(0, (3,))
+            turn_x(1, "scalar")
+            quantise_x(0)
+            turn_x(2, "scalar")
+            open_latent(0)
+            multiply_latent(0, (0, 1, 2, 3))
+            turn_x(3, "scalar")
+            quantise_x(1)
             open_latent(1)
             multiply_latent(1, (0, 1, 2, 3))
-            quantise_x(2)
-            open_latent(2)
-            multiply_latent(2, (0, 1, 2, 3))
-            quantise_x(3)
-            open_latent(3)
-            multiply_latent(3, (0, 1, 2, 3))
 
         late = ctx.enter_context(tc.tile_pool(name="late", bufs=1, reuse_waits="tile"))
         outs = ctx.enter_context(tc.tile_pool(name="outs", bufs=5, reuse_waits="tile"))
@@ -297,29 +291,31 @@ def tile_mla_pa_kernel(
 
         wk_units = [second_stage_unit(raw_wk, WK_CHUNKS, ROW_WK_BIAS, k_flat, i, True) for i in range(NOPE_COLS // UNIT)]
         wv_units = [second_stage_unit(raw_wv, WV_CHUNKS, ROW_WV_BIAS, v_flat, i, False) for i in range(NOPE_COLS // UNIT)]
-        units = wk_units + wv_units[:1] + [k_rope_unit(0)] + wv_units[1:2] + [k_rope_unit(1)] + wv_units[2:]
+        units = [wk_units[0], wk_units[1], wk_units[2], wk_units[3], wv_units[0], k_rope_unit(0), wv_units[1], k_rope_unit(1), wv_units[2], wv_units[3]]
         pieces = [(n, g) for n in range(len(units)) for g in range(len(units[n]["rows"]))]
         grouped_of = {}
         regrouped = []
         quantised = []
 
-        def regroup_next(halves=(0, 1)):
+        def regroup_half(h):
             j = len(regrouped)
-            if j < len(pieces):
-                n, g = pieces[j]
-                if j not in grouped_of:
-                    grouped_of[j] = stage.tile([P, UNIT * PACK], BF16, align_bytes=64, tag="grouped", name="grouped")
-                if len(halves) == 2:
-                    regroup(nc, False, grouped_of[j][:], units[n]["rows"][g])
-                else:
-                    h = halves[0]
-                    width = UNIT // 2
-                    regroup(
-                        nc, False, grouped_of[j][:, h * width * PACK : (h + 1) * width * PACK],
-                        units[n]["rows"][g][:, :, h * width : (h + 1) * width],
-                    )
-                if 1 in halves:
-                    regrouped.append(j)
+            n, g = pieces[j]
+            if h == 0:
+                grouped_of[j] = stage.tile([P, UNIT * PACK], BF16, align_bytes=64, tag="grouped", name="grouped")
+            width = UNIT // 2
+            regroup(
+                nc, "scalar", grouped_of[j][:, h * width * PACK : (h + 1) * width * PACK],
+                units[n]["rows"][g][:, :, h * width : (h + 1) * width],
+            )
+            if h == 1:
+                regrouped.append(j)
+
+        def regroup_next(engine="scalar"):
+            j = len(regrouped)
+            n, g = pieces[j]
+            grouped_of[j] = stage.tile([P, UNIT * PACK], BF16, align_bytes=64, tag="grouped", name="grouped")
+            regroup(nc, engine, grouped_of[j][:], units[n]["rows"][g])
+            regrouped.append(j)
 
         def quantise_next():
             j = len(quantised)
@@ -352,32 +348,32 @@ def tile_mla_pa_kernel(
                 scale=1.0 / RANK,
             )
 
-        gained_of = {}
+        normed_of = {}
 
-        def apply_gain(tt):
-            gained_of[tt] = norm.tile([P, RANK], F32, tag="gained", name="gained")
-            nc.vector.scalar_tensor_tensor(
-                out=gained_of[tt][:], in0=c_all[:, tt, :], scalar=minus_mean[:, tt : tt + 1],
-                in1=spread[:, ROW_GAIN, :], op0=ALU.add, op1=ALU.mult,
+        def normalise(tt):
+            normed_of[tt] = norm.tile([P, RANK], F32, tag="normed", name="normed")
+            nc.vector.tensor_scalar(
+                out=normed_of[tt][:], in0=c_all[:, tt, :], scalar1=minus_mean[:, tt : tt + 1],
+                scalar2=inv_std[:, tt : tt + 1], op0=ALU.add, op1=ALU.mult,
             )
 
-        def apply_shift(tt):
-            nc.vector.scalar_tensor_tensor(
-                out=cn[:, tt, :], in0=gained_of[tt][:], scalar=inv_std[:, tt : tt + 1],
-                in1=spread[:, ROW_SHIFT, :], op0=ALU.mult, op1=ALU.add,
-            )
-
+        cn_of = {}
         cn_grouped_of = {}
 
         def turn_cn(tt):
-            cn_turned = banks.tile([P, PACK, P], BF16, tag="bank", name="cn_turned")
+            turned = banks.tile([P, PACK, P], F32, tag="bank", name="normed_turned")
             for t in range(PACK):
-                nc.tensor.transpose(cn_turned[:, t, :], cn[:, tt, t * P : (t + 1) * P], ident_bf[:])
+                nc.tensor.transpose(turned[:, t, :], normed_of[tt][:, t * P : (t + 1) * P], ident_f32[:])
+            cn_of[tt] = norm.tile([P, PACK, P], BF16, tag="cn", name="cn")
+            for t in range(PACK):
+                nc.scalar.activation(
+                    out=cn_of[tt][:, t, :], in_=turned[:, t, :], func=ACT.Identity,
+                    bias=norm_cols[:, ROW_SHIFT, t : t + 1], scale=norm_cols[:, ROW_GAIN, t : t + 1],
+                )
+
+        def regroup_cn(tt, engine):
             cn_grouped_of[tt] = norm.tile([P, P * PACK], BF16, align_bytes=64, tag="cn_grouped", name="cn_grouped")
-            nc.scalar.copy(
-                out=cn_grouped_of[tt][:].rearrange("p (k t) -> p k t", t=PACK),
-                in_=cn_turned[:].rearrange("p t k -> p k t"),
-            )
+            regroup(nc, engine, cn_grouped_of[tt][:], cn_of[tt][:])
 
         def quantise_cn(tt):
             tokens = slice(tt * P, (tt + 1) * P)
@@ -419,63 +415,92 @@ def tile_mla_pa_kernel(
             )
 
         add_latent_bias(0)
-        regroup_next((0,))
+        quantise_x(2)
+        open_latent(2)
+        multiply_latent(2, (0, 1, 2, 3))
+        pick_rows(ROW_WK_BIAS, 2)
         statistics(0)
         add_latent_bias(1)
+        quantise_x(3)
+        open_latent(3)
+        multiply_latent(3, (0, 1, 2, 3))
         statistics(1)
+        normalise(0)
+        turn_cn(0)
         add_latent_bias(2)
+        normalise(1)
+        turn_cn(1)
         statistics(2)
-        apply_gain(0)
         add_latent_bias(3)
         statistics(3)
-        apply_shift(0)
-        turn_cn(0)
-        apply_gain(1)
-        apply_shift(1)
-        turn_cn(1)
-        regroup_next((1,))
-        apply_gain(2)
-        quantise_cn(0)
-        apply_shift(2)
+        regroup_next("vector")
+        regroup_cn(0, "vector")
+        normalise(2)
         turn_cn(2)
-        apply_gain(3)
-        quantise_cn(1)
-        apply_shift(3)
+        quantise_next()
+        quantise_cn(0)
+        regroup_cn(1, "vector")
+        normalise(3)
         turn_cn(3)
-        pick_rows(ROW_WV_BIAS + 2, 2)
+        regroup_next("vector")
+        quantise_cn(1)
+        regroup_cn(2, "vector")
+        spread_rows(ROW_WK_BIAS, "scalar")
         quantise_next()
         quantise_cn(2)
-        regroup_next()
+        regroup_cn(3, "vector")
+        pick_rows(ROW_WK_BIAS + 2, 2)
+        pick_rows(ROW_ROPE_BIAS, 2)
+        pick_rows(ROW_WV_BIAS, 2)
+        regroup_next("scalar")
+        spread_rows(ROW_WK_BIAS + 2, "scalar")
         quantise_cn(3)
-        regroup_next()
-        spread_rows(ROW_WV_BIAS, False)
-        spread_rows(ROW_ROPE_BIAS, False)
-        spread_rows(ROW_WV_BIAS + 2, False)
+        spread_rows(ROW_ROPE_BIAS, "scalar")
+        spread_rows(ROW_WV_BIAS, "scalar")
+        pick_rows(ROW_WV_BIAS + 2, 2)
+        spread_rows(ROW_WV_BIAS + 2, "scalar")
 
         def unit_adds(n):
             unit = units[n]
             unit["out"] = outs.tile([P, TOKEN_TILES, UNIT], F32, tag="unit_out", name="unit_out")
             for tt in range(TOKEN_TILES):
-                if tt == 2 and n + 1 < len(units):
-                    quantise_upto(pieces_of(n + 2))
-                    multiply_unit(n + 1)
+                if tt == 2:
+                    if n + 1 < len(units):
+                        quantise_upto(pieces_of(n + 2))
+                        multiply_unit(n + 1)
+                    if n + 2 < len(units):
+                        quantise_upto(pieces_of(n + 2) + len(units[n + 2]["rows"]) // 2)
+                    finish(n - ADD_LAG)
                 add_bias(n, tt)
-                if unit["flat_unit"] is None and tt % 2 == 1:
-                    store(unit, slice(tt - 1, tt + 1))
-            if unit["flat_unit"] is not None:
-                unit["add"] = rotate_products(
-                    nc, scratch, unit["out"][:], (2 - 8 * unit["flat_unit"]) % 3, cos_pair[:], sin_minus[:], sin_plus[:]
-                )
+                if unit["flat_unit"] is None:
+                    if n in (8, 9):
+                        store(unit, slice(tt, tt + 1))
+                    elif tt % 2 == 1:
+                        store(unit, slice(tt - 1, tt + 1))
+                elif n in (7,):
+                    if tt % 2 == 1:
+                        rotate(n, slice(tt - 1, tt + 1))
+                elif tt == TOKEN_TILES - 1:
+                    rotate(n, slice(0, TOKEN_TILES))
+
+        def rotate(n, tiles):
+            unit = units[n]
+            unit.setdefault("adds", []).append(
+                rotate_products(
+                    nc, scratch, unit["out"][:, tiles, :], (2 - 8 * unit["flat_unit"]) % 3, cos_pair[:, tiles, :],
+                    sin_minus[:, tiles, :], sin_plus[:, tiles, :],
+                ) + (tiles,)
+            )
 
         def finish(n):
-            if n >= 0 and units[n]["flat_unit"] is not None:
-                pairs, crossed = units[n]["add"]
-                nc.vector.tensor_tensor(out=pairs, in0=pairs, in1=crossed, op=ALU.add)
-                store(units[n], slice(0, TOKEN_TILES))
+            if n >= 0:
+                for pairs, crossed, tiles in units[n].get("adds", []):
+                    nc.vector.tensor_tensor(out=pairs, in0=pairs, in1=crossed, op=ALU.add)
+                    store(units[n], tiles)
 
         def quantise_upto(count):
             while len(quantised) < min(count, len(pieces)):
-                while len(regrouped) <= len(quantised):
+                if len(regrouped) <= len(quantised):
                     regroup_next()
                 quantise_next()
 
@@ -485,8 +510,5 @@ def tile_mla_pa_kernel(
         multiply_unit(0)
         for n in range(len(units)):
             unit_adds(n)
-            if n + 2 < len(units):
-                quantise_upto(pieces_of(n + 2) + len(units[n + 2]["rows"]) // 2)
-            finish(n - ADD_LAG)
         for n in range(len(units) - ADD_LAG, len(units)):
             finish(n)

@@ -199,6 +199,11 @@ def tile_mla_pa_kernel(
             latent_sums = [None] * TOKEN_TILES
             x_grouped = [None] * TOKEN_TILES
 
+            def keep_warm(count, rhs):
+                bank = banks.tile([P, UNIT], F32, tag="bank", name="unread")
+                for i in range(count):
+                    nc.tensor.matmul(out=bank[:], lhsT=ident_bf[:], rhs=rhs, start=True, stop=True)
+
             def regroup_latent(g, engine):
                 latent_grouped[g] = stage.tile([P, UNIT * PACK], BF16, align_bytes=64, tag="grouped", name="grouped")
                 regroup(nc, engine, latent_grouped[g][:], raw_latent[g][:])
@@ -244,15 +249,20 @@ def tile_mla_pa_kernel(
             pick_rows(ROW_LATENT_BIAS, 1)
             turn_norm_rows()
             spread_rows(ROW_LATENT_BIAS, "scalar")
+            keep_warm(2, raw_latent[1][:, 0, :])
             regroup_latent(1, "scalar")
             quantise_latent(0)
+            keep_warm(2, raw_latent[2][:, 0, :])
             regroup_latent(2, "vector")
             quantise_latent(1)
             quantise_latent(2)
+            keep_warm(2, raw_latent[3][:, 0, :])
             regroup_latent(3, "scalar")
             turn_x(0, "vector")
+            keep_warm(2, x_sb[:, 0, :UNIT])
             quantise_latent(3)
             turn_x(1, "scalar")
+            keep_warm(2, x_sb[:, 1, :UNIT])
             quantise_x(0)
             turn_x(2, "scalar")
             open_latent(0)
@@ -430,6 +440,7 @@ def tile_mla_pa_kernel(
         add_latent_bias(2)
         normalise(1)
         turn_cn(1)
+        pick_rows(ROW_WK_BIAS + 2, 2)
         statistics(2)
         add_latent_bias(3)
         statistics(3)
@@ -437,11 +448,13 @@ def tile_mla_pa_kernel(
         regroup_cn(0, "vector")
         normalise(2)
         turn_cn(2)
+        pick_rows(ROW_ROPE_BIAS, 2)
         quantise_next()
         quantise_cn(0)
         regroup_cn(1, "vector")
         normalise(3)
         turn_cn(3)
+        pick_rows(ROW_WV_BIAS, 2)
         regroup_next("vector")
         quantise_cn(1)
         regroup_cn(2, "vector")
@@ -449,9 +462,6 @@ def tile_mla_pa_kernel(
         quantise_next()
         quantise_cn(2)
         regroup_cn(3, "vector")
-        pick_rows(ROW_WK_BIAS + 2, 2)
-        pick_rows(ROW_ROPE_BIAS, 2)
-        pick_rows(ROW_WV_BIAS, 2)
         regroup_next("scalar")
         spread_rows(ROW_WK_BIAS + 2, "scalar")
         quantise_cn(3)

@@ -406,15 +406,23 @@ def tile_mla_pa_kernel(
                 stop=last,
             )
 
-        def open_banks(n):
-            units[n]["sums"] = [banks.tile([P, UNIT], F32, tag="bank", name="sum%d" % tt) for tt in range(TOKEN_TILES)]
+        def open_bank(n):
+            units[n].setdefault("sums", []).append(banks.tile([P, UNIT], F32, tag="bank", name="unit_sum"))
+            return units[n]["sums"][-1]
 
         def multiply_unit(n):
-            open_banks(n)
-            count = len(units[n]["rows"])
-            for g in range(count):
+            unit = units[n]
+            while len(unit.get("sums", [])) < TOKEN_TILES:
+                open_bank(n)
+            count = len(unit["rows"])
+            ready = min(count, len(quantised) - pieces_of(n))
+            for g in range(unit.get("passes", 0), ready):
                 for tt in range(TOKEN_TILES):
-                    one_pass(units[n], tt, g, g == count - 1)
+                    one_pass(unit, tt, g, g == count - 1)
+            unit["passes"] = ready
+
+        def pieces_of(n):
+            return sum(len(u["rows"]) for u in units[:n])
 
         def store(unit, tiles):
             nc.sync.dma_start(out=unit["dest"].rearrange("(t p) c -> p t c", p=P)[:, tiles, :], in_=unit["out"][:, tiles, :])
@@ -474,6 +482,8 @@ def tile_mla_pa_kernel(
             unit = units[n]
             unit["out"] = outs.tile([P, TOKEN_TILES, UNIT], F32, tag="unit_out", name="unit_out")
             for tt in range(TOKEN_TILES):
+                if tt == 0 and n + 1 < len(units) and len(quantised) > pieces_of(n + 1):
+                    multiply_unit(n + 1)
                 if tt == 2:
                     if n + 1 < len(units):
                         quantise_upto(pieces_of(n + 2))
@@ -482,6 +492,11 @@ def tile_mla_pa_kernel(
                         quantise_upto(pieces_of(n + 2) + len(units[n + 2]["rows"]) // 2)
                     finish(n - ADD_LAG)
                 add_bias(n, tt)
+                if n + 2 < len(units) and (tt > 1 or len(units[n + 1]["rows"]) == 1):
+                    bank = open_bank(n + 2)
+                    nc.tensor.matmul(
+                        out=bank[:, :P], lhsT=ident_f32[:], rhs=ident_f32[:], start=True, stop=True
+                    )
                 if unit["flat_unit"] is None:
                     if n in (8, 9):
                         store(unit, slice(tt, tt + 1))
@@ -513,9 +528,6 @@ def tile_mla_pa_kernel(
                 if len(regrouped) <= len(quantised):
                     regroup_next()
                 quantise_next()
-
-        def pieces_of(n):
-            return sum(len(u["rows"]) for u in units[:n])
 
         multiply_unit(0)
         for n in range(len(units)):

@@ -126,12 +126,6 @@ def tile_mla_pa_kernel(
         make_identity(nc, ident_bf[:])
         nc.gpsimd.dma_start(out=cos_sin[:, 0], in_=cos.rearrange("(a p) j -> p a j", p=P))
         nc.gpsimd.dma_start(out=cos_sin[:, 1], in_=sin.rearrange("(a p) j -> p a j", p=P))
-        for row, count, vector in (
-            (ROW_WK_BIAS, 4, wk_b),
-            (ROW_ROPE_BIAS, 2, wkv_a_b[:ROPE_COLS]),
-            (ROW_WV_BIAS, 4, wv_b),
-        ):
-            nc.gpsimd.dma_start(out=bias_rows[row : row + count, :], in_=vector.rearrange("(r c) -> r c", c=UNIT))
         nc.scalar.activation(out=first[:], in_=eps[:], func=ACT.Abs_reciprocal_sqrt, bias=eps[:], scale=1.0)
 
         def load_first_stage(tile_, g, col0, width):
@@ -157,6 +151,12 @@ def tile_mla_pa_kernel(
                 nc.sync.dma_start(out=norm_rows[row : row + 1, :], in_=vector.rearrange("(r c) -> r c", c=UNIT))
             for g in range(1, PASSES):
                 load_first_stage(raw_latent[g], g, ROPE_COLS, RANK)
+            for row, count, vector in (
+                (ROW_WK_BIAS, 4, wk_b),
+                (ROW_ROPE_BIAS, 2, wkv_a_b[:ROPE_COLS]),
+                (ROW_WV_BIAS, 4, wv_b),
+            ):
+                nc.sync.dma_start(out=bias_rows[row : row + count, :], in_=vector.rearrange("(r c) -> r c", c=UNIT))
             for tt in range(TOKEN_TILES):
                 load_x(tt)
             for c, width in enumerate(WK_CHUNKS):
@@ -259,14 +259,16 @@ def tile_mla_pa_kernel(
             keep_warm(2, raw_latent[3][:, 0, :])
             regroup_latent(3, "scalar")
             turn_x(0, "vector")
-            keep_warm(2, x_sb[:, 0, :UNIT])
+            pick_rows(ROW_WK_BIAS, 2)
             quantise_latent(3)
+            spread_rows(ROW_WK_BIAS, "scalar")
             turn_x(1, "scalar")
-            keep_warm(2, x_sb[:, 1, :UNIT])
+            pick_rows(ROW_WK_BIAS + 2, 2)
             quantise_x(0)
             turn_x(2, "scalar")
             open_latent(0)
             multiply_latent(0, (0, 1, 2, 3))
+            spread_rows(ROW_WK_BIAS + 2, "scalar")
             turn_x(3, "scalar")
             quantise_x(1)
             open_latent(1)
@@ -436,7 +438,6 @@ def tile_mla_pa_kernel(
         quantise_x(2)
         open_latent(2)
         multiply_latent(2, (0, 1, 2, 3))
-        pick_rows(ROW_WK_BIAS, 2)
         statistics(0)
         add_latent_bias(1)
         quantise_x(3)
@@ -448,7 +449,7 @@ def tile_mla_pa_kernel(
         add_latent_bias(2)
         normalise(1)
         turn_cn(1)
-        pick_rows(ROW_WK_BIAS + 2, 2)
+        pick_rows(ROW_ROPE_BIAS, 2)
         statistics(2)
         add_latent_bias(3)
         statistics(3)
@@ -456,26 +457,23 @@ def tile_mla_pa_kernel(
         regroup_cn(0, "vector")
         normalise(2)
         turn_cn(2)
-        pick_rows(ROW_ROPE_BIAS, 2)
+        pick_rows(ROW_WV_BIAS, 2)
         quantise_next()
         quantise_cn(0)
         regroup_cn(1, "vector")
         normalise(3)
         turn_cn(3)
-        pick_rows(ROW_WV_BIAS, 2)
+        pick_rows(ROW_WV_BIAS + 2, 2)
         regroup_next("vector")
         quantise_cn(1)
         regroup_cn(2, "vector")
-        spread_rows(ROW_WK_BIAS, "scalar")
         quantise_next()
         quantise_cn(2)
         regroup_cn(3, "vector")
         regroup_next("scalar")
-        spread_rows(ROW_WK_BIAS + 2, "scalar")
         quantise_cn(3)
         spread_rows(ROW_ROPE_BIAS, "scalar")
         spread_rows(ROW_WV_BIAS, "scalar")
-        pick_rows(ROW_WV_BIAS + 2, 2)
         spread_rows(ROW_WV_BIAS + 2, "scalar")
 
         def unit_adds(n):
@@ -492,7 +490,7 @@ def tile_mla_pa_kernel(
                         quantise_upto(pieces_of(n + 2) + len(units[n + 2]["rows"]) // 2)
                     finish(n - ADD_LAG)
                 add_bias(n, tt)
-                if n + 2 < len(units) and (tt > 1 or len(units[n + 1]["rows"]) == 1):
+                if n + 2 < len(units) and len(units[n + 1]["rows"]) == 1 and len(units[n + 2]["rows"]) == 1:
                     bank = open_bank(n + 2)
                     nc.tensor.matmul(
                         out=bank[:, :P], lhsT=ident_f32[:], rhs=ident_f32[:], start=True, stop=True

@@ -303,7 +303,7 @@ def tile_mla_pa_kernel(
 
         wk_units = [second_stage_unit(raw_wk, WK_CHUNKS, ROW_WK_BIAS, k_flat, i, True) for i in range(NOPE_COLS // UNIT)]
         wv_units = [second_stage_unit(raw_wv, WV_CHUNKS, ROW_WV_BIAS, v_flat, i, False) for i in range(NOPE_COLS // UNIT)]
-        units = [wk_units[0], wk_units[1], wk_units[2], wk_units[3], wv_units[0], k_rope_unit(0), wv_units[1], k_rope_unit(1), wv_units[2], wv_units[3]]
+        units = [wk_units[0], wk_units[1], wv_units[0], wk_units[2], wv_units[1], wk_units[3], k_rope_unit(0), wv_units[2], k_rope_unit(1), wv_units[3]]
         pieces = [(n, g) for n in range(len(units)) for g in range(len(units[n]["rows"]))]
         grouped_of = {}
         regrouped = []
@@ -480,27 +480,13 @@ def tile_mla_pa_kernel(
             unit = units[n]
             unit["out"] = outs.tile([P, TOKEN_TILES, UNIT], F32, tag="unit_out", name="unit_out")
             for tt in range(TOKEN_TILES):
-                if tt == 0 and n + 1 < len(units) and len(quantised) > pieces_of(n + 1):
-                    multiply_unit(n + 1)
-                if tt == 2:
-                    if n + 1 < len(units):
-                        quantise_upto(pieces_of(n + 2))
-                        multiply_unit(n + 1)
-                    if n + 2 < len(units):
-                        quantise_upto(pieces_of(n + 2) + len(units[n + 2]["rows"]) // 2)
-                    finish(n - ADD_LAG)
                 add_bias(n, tt)
-                if n + 2 < len(units) and len(units[n + 1]["rows"]) == 1 and len(units[n + 2]["rows"]) == 1:
-                    bank = open_bank(n + 2)
-                    nc.tensor.matmul(
-                        out=bank[:, :P], lhsT=ident_f32[:], rhs=ident_f32[:], start=True, stop=True
-                    )
                 if unit["flat_unit"] is None:
                     if n in (8, 9):
                         store(unit, slice(tt, tt + 1))
                     elif tt % 2 == 1:
                         store(unit, slice(tt - 1, tt + 1))
-                elif n in (7,):
+                elif n in (8,):
                     if tt % 2 == 1:
                         rotate(n, slice(tt - 1, tt + 1))
                 elif tt == TOKEN_TILES - 1:
@@ -527,8 +513,16 @@ def tile_mla_pa_kernel(
                     regroup_next()
                 quantise_next()
 
+        quantise_upto(pieces_of(2))
         multiply_unit(0)
-        for n in range(len(units)):
+        multiply_unit(1)
+        for n in range(0, len(units), 2):
             unit_adds(n)
-        for n in range(len(units) - ADD_LAG, len(units)):
-            finish(n)
+            unit_adds(n + 1)
+            for m in (n + 2, n + 3):
+                if m < len(units):
+                    quantise_upto(pieces_of(m + 1))
+                    multiply_unit(m)
+            for m in (n - 1, n):
+                finish(m)
+        finish(len(units) - 1)

@@ -57,23 +57,24 @@ def quantise(nc, grouped, codes, scales):
     nc.vector.quantize_mx(out=codes.bitcast(FP8X4), scales=scales, in_=grouped)
 
 
-def rotate_products(nc, scratch, unit_out, first_block, cos_pair, sin_minus, sin_plus):
+def rotate_products(engine, scratch, unit_out, first_block, cos_pair, sin_minus, sin_plus):
     blocks = unit_out.rearrange("p t (k d) -> p t k d", d=ROPE)[:, :, first_block::3, :]
     n = blocks.shape[2]
     pairs = blocks.rearrange("p t n (j e) -> p t n j e", e=2)
     tiles = blocks.shape[1]
     half = [P, tiles, n, ROPE // 2]
     crossed = scratch.tile([P, 2, tiles, n, ROPE // 2], F32, tag="crossed")
-    nc.gpsimd.tensor_tensor(
+    engine.tensor_tensor(
         out=crossed[:, 0], in0=pairs[:, :, :, :, 1], in1=sin_minus.unsqueeze(2).to_broadcast(half), op=ALU.mult
     )
-    nc.gpsimd.tensor_tensor(
+    engine.tensor_tensor(
         out=crossed[:, 1], in0=pairs[:, :, :, :, 0], in1=sin_plus.unsqueeze(2).to_broadcast(half), op=ALU.mult
     )
-    nc.gpsimd.tensor_tensor(
-        out=blocks, in0=blocks, in1=cos_pair.unsqueeze(2).to_broadcast([P, tiles, n, ROPE]), op=ALU.mult
+    straight = scratch.tile([P, tiles, n, ROPE], F32, tag="straight")
+    engine.tensor_tensor(
+        out=straight[:], in0=blocks, in1=cos_pair.unsqueeze(2).to_broadcast([P, tiles, n, ROPE]), op=ALU.mult
     )
-    return pairs, crossed[:].rearrange("p e t n j -> p t n j e")
+    return pairs, straight[:].rearrange("p t n (j e) -> p t n j e", e=2), crossed[:].rearrange("p e t n j -> p t n j e")
 
 
 def tile_mla_pa_kernel(
@@ -276,7 +277,7 @@ def tile_mla_pa_kernel(
 
         late = ctx.enter_context(tc.tile_pool(name="late", bufs=1, reuse_waits="tile"))
         outs = ctx.enter_context(tc.tile_pool(name="outs", bufs=5, reuse_waits="tile"))
-        scratch = ctx.enter_context(tc.tile_pool(name="scratch", bufs=3, reuse_waits="tile"))
+        scratch = ctx.enter_context(tc.tile_pool(name="scratch", bufs=2, reuse_waits="tile"))
         raw_wv = [late.tile([P, PACK, width], BF16, tag="raw_wv%d" % c, name="raw_wv") for c, width in enumerate(WV_CHUNKS)]
         load_second_stage(raw_wv[0], wv_w, 0, WV_CHUNKS[0])
         for g in range(PASSES):
@@ -476,36 +477,40 @@ def tile_mla_pa_kernel(
         spread_rows(ROW_WV_BIAS, "scalar")
         spread_rows(ROW_WV_BIAS + 2, "scalar")
 
-        def unit_adds(n):
+        def drain(n, rotated_together=TOKEN_TILES, engines=(None, None, None, None)):
             unit = units[n]
             unit["out"] = outs.tile([P, TOKEN_TILES, UNIT], F32, tag="unit_out", name="unit_out")
             for tt in range(TOKEN_TILES):
                 add_bias(n, tt)
                 if unit["flat_unit"] is None:
-                    if n in (8, 9):
+                    if n == len(units) - 1:
                         store(unit, slice(tt, tt + 1))
                     elif tt % 2 == 1:
                         store(unit, slice(tt - 1, tt + 1))
-                elif n in (8,):
-                    if tt % 2 == 1:
-                        rotate(n, slice(tt - 1, tt + 1))
-                elif tt == TOKEN_TILES - 1:
-                    rotate(n, slice(0, TOKEN_TILES))
+                elif (tt + 1) % rotated_together == 0:
+                    rotate(n, slice(tt + 1 - rotated_together, tt + 1), engines[tt // rotated_together])
 
-        def rotate(n, tiles):
+        def rotate(n, tiles, engine=None):
+            if engine == "later":
+                return
             unit = units[n]
             unit.setdefault("adds", []).append(
                 rotate_products(
-                    nc, scratch, unit["out"][:, tiles, :], (2 - 8 * unit["flat_unit"]) % 3, cos_pair[:, tiles, :],
+                    engine or nc.gpsimd, scratch, unit["out"][:, tiles, :], (2 - 8 * unit["flat_unit"]) % 3, cos_pair[:, tiles, :],
                     sin_minus[:, tiles, :], sin_plus[:, tiles, :],
                 ) + (tiles,)
             )
 
-        def finish(n):
-            if n >= 0:
-                for pairs, crossed, tiles in units[n].get("adds", []):
-                    nc.vector.tensor_tensor(out=pairs, in0=pairs, in1=crossed, op=ALU.add)
-                    store(units[n], tiles)
+        def finish(n, parts=None):
+            adds = units[n].get("adds", []) if n >= 0 else []
+            for i in range(len(adds)) if parts is None else parts:
+                pairs, straight, crossed, tiles = adds[i]
+                nc.vector.tensor_tensor(out=pairs, in0=straight, in1=crossed, op=ALU.add)
+                store(units[n], tiles)
+
+        def regroup_upto(count, engine="scalar"):
+            while len(regrouped) < count:
+                regroup_next(engine)
 
         def quantise_upto(count):
             while len(quantised) < min(count, len(pieces)):
@@ -516,13 +521,42 @@ def tile_mla_pa_kernel(
         quantise_upto(pieces_of(2))
         multiply_unit(0)
         multiply_unit(1)
-        for n in range(0, len(units), 2):
-            unit_adds(n)
-            unit_adds(n + 1)
-            for m in (n + 2, n + 3):
-                if m < len(units):
-                    quantise_upto(pieces_of(m + 1))
-                    multiply_unit(m)
-            for m in (n - 1, n):
-                finish(m)
-        finish(len(units) - 1)
+        drain(0)
+        drain(1)
+        quantise_upto(pieces_of(3))
+        multiply_unit(2)
+        quantise_upto(pieces_of(4))
+        multiply_unit(3)
+        finish(0)
+        drain(2)
+        drain(3)
+        quantise_upto(pieces_of(5))
+        multiply_unit(4)
+        quantise_upto(pieces_of(6))
+        multiply_unit(5)
+        finish(1)
+        quantise_upto(pieces_of(6) + 1)
+        drain(4)
+        drain(5)
+        quantise_upto(pieces_of(7))
+        multiply_unit(6)
+        quantise_upto(pieces_of(8))
+        multiply_unit(7)
+        finish(3)
+        drain(6, 2, (nc.gpsimd, "later"))
+        drain(7)
+        quantise_upto(pieces_of(9))
+        multiply_unit(8)
+        quantise_upto(pieces_of(10))
+        multiply_unit(9)
+        finish(5)
+        rotate(6, slice(2, 4), nc.vector)
+        finish(6)
+        drain(8, 2, (nc.gpsimd, "later"))
+
+        drain(9)
+
+        rotate(8, slice(2, 3), nc.vector)
+        finish(8, (0, 1))
+        rotate(8, slice(3, 4), nc.vector)
+        finish(8, (2,))

@@ -212,7 +212,7 @@ def tile_mla_pa_kernel(
             def quantise_latent(g):
                 quantise(nc, latent_grouped[g][:], latent_codes[:, g, :], latent_scales[:, g, :])
 
-            def turn_x(tt, engine):
+            def turn_x(tt, engines):
                 words = x_sb[:, tt, :].bitcast(F32)
                 x_grouped[tt] = x_staging.tile([P, PASSES * P * PACK], BF16, align_bytes=64, tag="x_grouped", name="x_grouped")
                 out_words = x_grouped[tt][:].bitcast(F32).rearrange("p (g k u) -> p g k u", g=PASSES, u=2)
@@ -223,7 +223,7 @@ def tile_mla_pa_kernel(
                             col0 = (2 * (2 * half + i) + u) * P
                             nc.tensor.transpose(turned[:, i, u, :], words[:, col0 : col0 + P], ident_f32[:])
                     copy(
-                        nc, engine, out_words[:, 2 * half : 2 * half + 2, :, :],
+                        nc, engines[half], out_words[:, 2 * half : 2 * half + 2, :, :],
                         turned[:].rearrange("p i u k -> p i k u"),
                     )
 
@@ -259,18 +259,18 @@ def tile_mla_pa_kernel(
             quantise_latent(2)
             keep_warm(2, raw_latent[3][:, 0, :])
             regroup_latent(3, "scalar")
-            turn_x(0, "vector")
+            turn_x(0, ("vector", "vector"))
             pick_rows(ROW_WK_BIAS, 2)
             quantise_latent(3)
             spread_rows(ROW_WK_BIAS, "scalar")
-            turn_x(1, "scalar")
+            turn_x(1, ("scalar", "scalar"))
             pick_rows(ROW_WK_BIAS + 2, 2)
             quantise_x(0)
-            turn_x(2, "scalar")
+            turn_x(2, ("scalar", "scalar"))
             open_latent(0)
             multiply_latent(0, (0, 1, 2, 3))
             spread_rows(ROW_WK_BIAS + 2, "scalar")
-            turn_x(3, "scalar")
+            turn_x(3, ("scalar", "scalar"))
             quantise_x(1)
             open_latent(1)
             multiply_latent(1, (0, 1, 2, 3))
@@ -348,14 +348,20 @@ def tile_mla_pa_kernel(
                 op0=ALU.mult, op1=ALU.add, accum_out=c_sum[:, tt : tt + 1],
             )
 
-        def statistics(tt):
+        def negate_mean(tt):
             one_tile = slice(tt, tt + 1)
             nc.scalar.mul(out=minus_mean[:, one_tile], in_=c_sum[:, one_tile], mul=-1.0 / RANK)
+
+        def sum_squares(tt):
+            one_tile = slice(tt, tt + 1)
             squares = norm.tile([P, RANK], BF16, tag="squares", name="squares")
             nc.scalar.activation(
                 out=squares[:], in_=c_all[:, tt, :], func=ACT.Square, bias=minus_mean[:, one_tile], scale=1.0,
                 accum_out=square_sum[:, one_tile],
             )
+
+        def invert_std(tt):
+            one_tile = slice(tt, tt + 1)
             nc.scalar.activation(
                 out=inv_std[:, one_tile], in_=square_sum[:, one_tile], func=ACT.Abs_reciprocal_sqrt, bias=eps[:],
                 scale=1.0 / RANK,
@@ -370,17 +376,20 @@ def tile_mla_pa_kernel(
                 scalar2=inv_std[:, tt : tt + 1], op0=ALU.add, op1=ALU.mult,
             )
 
+        turned_of = {}
         cn_of = {}
         cn_grouped_of = {}
 
         def turn_cn(tt):
-            turned = banks.tile([P, PACK, P], F32, tag="bank", name="normed_turned")
+            turned_of[tt] = banks.tile([P, PACK, P], F32, tag="bank", name="normed_turned")
             for t in range(PACK):
-                nc.tensor.transpose(turned[:, t, :], normed_of[tt][:, t * P : (t + 1) * P], ident_f32[:])
+                nc.tensor.transpose(turned_of[tt][:, t, :], normed_of[tt][:, t * P : (t + 1) * P], ident_f32[:])
+
+        def scale_cn(tt):
             cn_of[tt] = norm.tile([P, PACK, P], BF16, tag="cn", name="cn")
             for t in range(PACK):
                 nc.scalar.activation(
-                    out=cn_of[tt][:, t, :], in_=turned[:, t, :], func=ACT.Identity,
+                    out=cn_of[tt][:, t, :], in_=turned_of[tt][:, t, :], func=ACT.Identity,
                     bias=norm_cols[:, ROW_SHIFT, t : t + 1], scale=norm_cols[:, ROW_GAIN, t : t + 1],
                 )
 
@@ -439,32 +448,44 @@ def tile_mla_pa_kernel(
         quantise_x(2)
         open_latent(2)
         multiply_latent(2, (0, 1, 2, 3))
-        statistics(0)
+        negate_mean(0)
+        sum_squares(0)
+        invert_std(0)
         add_latent_bias(1)
         quantise_x(3)
         open_latent(3)
         multiply_latent(3, (0, 1, 2, 3))
-        statistics(1)
+        negate_mean(1)
+        sum_squares(1)
+        invert_std(1)
         normalise(0)
         turn_cn(0)
         add_latent_bias(2)
+        negate_mean(2)
+        sum_squares(2)
         normalise(1)
         turn_cn(1)
         pick_rows(ROW_ROPE_BIAS, 2)
-        statistics(2)
         add_latent_bias(3)
-        statistics(3)
-        regroup_next("vector")
-        regroup_cn(0, "vector")
+        scale_cn(0)
+        invert_std(2)
+        negate_mean(3)
+        sum_squares(3)
         normalise(2)
         turn_cn(2)
         pick_rows(ROW_WV_BIAS, 2)
+        regroup_next("vector")
+        scale_cn(1)
+        invert_std(3)
+        regroup_cn(0, "vector")
+        scale_cn(2)
         quantise_next()
         quantise_cn(0)
-        regroup_cn(1, "vector")
         normalise(3)
         turn_cn(3)
         pick_rows(ROW_WV_BIAS + 2, 2)
+        regroup_cn(1, "vector")
+        scale_cn(3)
         regroup_next("vector")
         quantise_cn(1)
         regroup_cn(2, "vector")
@@ -476,7 +497,6 @@ def tile_mla_pa_kernel(
         spread_rows(ROW_ROPE_BIAS, "scalar")
         spread_rows(ROW_WV_BIAS, "scalar")
         spread_rows(ROW_WV_BIAS + 2, "scalar")
-
         def drain(n, rotated_together=TOKEN_TILES, engines=(None, None, None, None)):
             unit = units[n]
             unit["out"] = outs.tile([P, TOKEN_TILES, UNIT], F32, tag="unit_out", name="unit_out")
@@ -523,21 +543,24 @@ def tile_mla_pa_kernel(
         multiply_unit(1)
         drain(0)
         drain(1)
-        quantise_upto(pieces_of(3))
+        quantise_upto(3)
         multiply_unit(2)
-        quantise_upto(pieces_of(4))
+        quantise_upto(4)
         multiply_unit(3)
         finish(0)
         drain(2)
         drain(3)
-        quantise_upto(pieces_of(5))
+        quantise_upto(5)
         multiply_unit(4)
-        quantise_upto(pieces_of(6))
+        quantise_upto(6)
         multiply_unit(5)
         finish(1)
-        quantise_upto(pieces_of(6) + 1)
+        quantise_upto(7)
         drain(4)
         drain(5)
+        regroup_upto(8)
+        regroup_upto(9, "vector")
+        regroup_upto(11)
         quantise_upto(pieces_of(7))
         multiply_unit(6)
         quantise_upto(pieces_of(8))
@@ -545,6 +568,7 @@ def tile_mla_pa_kernel(
         finish(3)
         drain(6, 2, (nc.gpsimd, "later"))
         drain(7)
+
         quantise_upto(pieces_of(9))
         multiply_unit(8)
         quantise_upto(pieces_of(10))
@@ -553,9 +577,7 @@ def tile_mla_pa_kernel(
         rotate(6, slice(2, 4), nc.vector)
         finish(6)
         drain(8, 2, (nc.gpsimd, "later"))
-
         drain(9)
-
         rotate(8, slice(2, 3), nc.vector)
         finish(8, (0, 1))
         rotate(8, slice(3, 4), nc.vector)

@@ -97,7 +97,6 @@ def tile_mla_pa_kernel(
         banks = ctx.enter_context(tc.psum_pool(name="banks", bufs=8))
 
         norm_rows = const.tile([P, UNIT], BF16)
-        bias_rows = const.tile([P, UNIT], BF16)
         cos_sin = const.tile([P, 2, SEQ_TILES, ROPE // 2], BF16)
         ident_f32 = const.tile([P, P], F32)
         ident_bf = const.tile([P, P], BF16)
@@ -122,7 +121,6 @@ def tile_mla_pa_kernel(
 
         nc.vector.memset(norm_rows[:].bitcast(U32), 0)
         nc.vector.memset(eps[:], EPS)
-        nc.vector.memset(bias_rows[:].bitcast(U32), 0)
         make_identity(nc, ident_f32[:])
         make_identity(nc, ident_bf[:])
         nc.gpsimd.dma_start(out=cos_sin[:, 0], in_=cos.rearrange("(a p) j -> p a j", p=P))
@@ -136,6 +134,12 @@ def tile_mla_pa_kernel(
                     out=tile_[:, 2 * u : 2 * u + 2, :],
                     in_=wkv_a_w[row0 : row0 + 2 * P, col0 : col0 + width].rearrange("(q e) c -> q e c", e=2),
                 )
+
+        def load_spread(row, vector):
+            count = vector.shape[0] // UNIT
+            nc.sync.dma_start(
+                out=spread[:, row : row + count, :].rearrange("p r c -> p (r c)"), in_=vector.partition_broadcast(P)
+            )
 
         def load_second_stage(tile_, weight, col0, width):
             nc.sync.dma_start(out=tile_[:], in_=weight[:, col0 : col0 + width].rearrange("(t p) n -> p t n", p=P))
@@ -152,16 +156,11 @@ def tile_mla_pa_kernel(
                 nc.sync.dma_start(out=norm_rows[row : row + 1, :], in_=vector.rearrange("(r c) -> r c", c=UNIT))
             for g in range(1, PASSES):
                 load_first_stage(raw_latent[g], g, ROPE_COLS, RANK)
-            for row, count, vector in (
-                (ROW_WK_BIAS, 4, wk_b),
-                (ROW_ROPE_BIAS, 2, wkv_a_b[:ROPE_COLS]),
-                (ROW_WV_BIAS, 4, wv_b),
-            ):
-                nc.sync.dma_start(out=bias_rows[row : row + count, :], in_=vector.rearrange("(r c) -> r c", c=UNIT))
             for tt in range(TOKEN_TILES):
                 load_x(tt)
             for c, width in enumerate(WK_CHUNKS):
                 load_second_stage(raw_wk[c], wk_w, sum(WK_CHUNKS[:c]), width)
+            load_spread(ROW_WK_BIAS, wk_b)
 
             picked = {}
 
@@ -169,7 +168,7 @@ def tile_mla_pa_kernel(
                 picked[r] = banks.tile([P, count, UNIT], BF16, tag="bank", name="picked")
                 for i in range(count):
                     nc.tensor.matmul(
-                        out=picked[r][:, i, :], lhsT=ident_bf[:, r + i : r + i + 1].to_broadcast([P, P]), rhs=norm_rows[:] if r < NORM_ROWS else bias_rows[:],
+                        out=picked[r][:, i, :], lhsT=ident_bf[:, r + i : r + i + 1].to_broadcast([P, P]), rhs=norm_rows[:],
                         start=True, stop=True,
                     )
 
@@ -260,16 +259,14 @@ def tile_mla_pa_kernel(
             keep_warm(2, raw_latent[3][:, 0, :])
             regroup_latent(3, "scalar")
             turn_x(0, ("vector", "vector"))
-            pick_rows(ROW_WK_BIAS, 2)
+            keep_warm(2, raw_latent[0][:, 0, :])
             quantise_latent(3)
-            spread_rows(ROW_WK_BIAS, "scalar")
             turn_x(1, ("scalar", "scalar"))
-            pick_rows(ROW_WK_BIAS + 2, 2)
+            keep_warm(2, raw_latent[0][:, 1, :])
             quantise_x(0)
             turn_x(2, ("scalar", "scalar"))
             open_latent(0)
             multiply_latent(0, (0, 1, 2, 3))
-            spread_rows(ROW_WK_BIAS + 2, "scalar")
             turn_x(3, ("scalar", "scalar"))
             quantise_x(1)
             open_latent(1)
@@ -280,9 +277,11 @@ def tile_mla_pa_kernel(
         scratch = ctx.enter_context(tc.tile_pool(name="scratch", bufs=2, reuse_waits="tile"))
         raw_wv = [late.tile([P, PACK, width], BF16, tag="raw_wv%d" % c, name="raw_wv") for c, width in enumerate(WV_CHUNKS)]
         load_second_stage(raw_wv[0], wv_w, 0, WV_CHUNKS[0])
+        load_spread(ROW_WV_BIAS, wv_b)
         for g in range(PASSES):
             load_first_stage(raw_rope[g], g, 0, ROPE_COLS)
         load_second_stage(raw_wv[1], wv_w, WV_CHUNKS[0], WV_CHUNKS[1])
+        load_spread(ROW_ROPE_BIAS, wkv_a_b[:ROPE_COLS])
 
         def k_rope_unit(i):
             return {
@@ -465,7 +464,7 @@ def tile_mla_pa_kernel(
         sum_squares(2)
         normalise(1)
         turn_cn(1)
-        pick_rows(ROW_ROPE_BIAS, 2)
+        keep_warm(2, raw_wk[0][:, 0, :])
         add_latent_bias(3)
         scale_cn(0)
         invert_std(2)
@@ -473,7 +472,7 @@ def tile_mla_pa_kernel(
         sum_squares(3)
         normalise(2)
         turn_cn(2)
-        pick_rows(ROW_WV_BIAS, 2)
+        keep_warm(2, raw_wk[0][:, 1, :])
         regroup_next("vector")
         scale_cn(1)
         invert_std(3)
@@ -483,7 +482,7 @@ def tile_mla_pa_kernel(
         quantise_cn(0)
         normalise(3)
         turn_cn(3)
-        pick_rows(ROW_WV_BIAS + 2, 2)
+        keep_warm(2, raw_wk[0][:, 2, :])
         regroup_cn(1, "vector")
         scale_cn(3)
         regroup_next("vector")
@@ -494,9 +493,6 @@ def tile_mla_pa_kernel(
         regroup_cn(3, "vector")
         regroup_next("scalar")
         quantise_cn(3)
-        spread_rows(ROW_ROPE_BIAS, "scalar")
-        spread_rows(ROW_WV_BIAS, "scalar")
-        spread_rows(ROW_WV_BIAS + 2, "scalar")
         def drain(n, rotated_together=TOKEN_TILES, engines=(None, None, None, None)):
             unit = units[n]
             unit["out"] = outs.tile([P, TOKEN_TILES, UNIT], F32, tag="unit_out", name="unit_out")

@@ -493,26 +493,29 @@ def tile_mla_pa_kernel(
         regroup_cn(3, "vector")
         regroup_next("scalar")
         quantise_cn(3)
-        def drain(n, rotated_together=TOKEN_TILES, engines=(None, None, None, None)):
+        WHOLE = ((0, TOKEN_TILES),)
+
+        def drain(n, tiles=range(TOKEN_TILES), groups=WHOLE):
             unit = units[n]
-            unit["out"] = outs.tile([P, TOKEN_TILES, UNIT], F32, tag="unit_out", name="unit_out")
-            for tt in range(TOKEN_TILES):
+            if tiles[0] == 0:
+                unit["out"] = outs.tile([P, TOKEN_TILES, UNIT], F32, tag="unit_out", name="unit_out")
+            for tt in tiles:
                 add_bias(n, tt)
                 if unit["flat_unit"] is None:
                     if n == len(units) - 1:
                         store(unit, slice(tt, tt + 1))
                     elif tt % 2 == 1:
                         store(unit, slice(tt - 1, tt + 1))
-                elif (tt + 1) % rotated_together == 0:
-                    rotate(n, slice(tt + 1 - rotated_together, tt + 1), engines[tt // rotated_together])
+                else:
+                    for first_tile, end_tile in groups:
+                        if tt + 1 == end_tile:
+                            rotate(nc.gpsimd, n, slice(first_tile, end_tile))
 
-        def rotate(n, tiles, engine=None):
-            if engine == "later":
-                return
+        def rotate(engine, n, tiles):
             unit = units[n]
             unit.setdefault("adds", []).append(
                 rotate_products(
-                    engine or nc.gpsimd, scratch, unit["out"][:, tiles, :], (2 - 8 * unit["flat_unit"]) % 3, cos_pair[:, tiles, :],
+                    engine, scratch, unit["out"][:, tiles, :], (2 - 8 * unit["flat_unit"]) % 3, cos_pair[:, tiles, :],
                     sin_minus[:, tiles, :], sin_plus[:, tiles, :],
                 ) + (tiles,)
             )
@@ -554,15 +557,13 @@ def tile_mla_pa_kernel(
         quantise_upto(7)
         drain(4)
         drain(5)
-        regroup_upto(8)
-        regroup_upto(9, "vector")
-        regroup_upto(11)
+
         quantise_upto(pieces_of(7))
         multiply_unit(6)
         quantise_upto(pieces_of(8))
         multiply_unit(7)
         finish(3)
-        drain(6, 2, (nc.gpsimd, "later"))
+        drain(6, groups=((0, 2),))
         drain(7)
 
         quantise_upto(pieces_of(9))
@@ -570,11 +571,11 @@ def tile_mla_pa_kernel(
         quantise_upto(pieces_of(10))
         multiply_unit(9)
         finish(5)
-        rotate(6, slice(2, 4), nc.vector)
+        rotate(nc.vector, 6, slice(2, 4))
         finish(6)
-        drain(8, 2, (nc.gpsimd, "later"))
+        drain(8, groups=((0, 2),))
         drain(9)
-        rotate(8, slice(2, 3), nc.vector)
+        rotate(nc.vector, 8, slice(2, 3))
         finish(8, (0, 1))
-        rotate(8, slice(3, 4), nc.vector)
+        rotate(nc.vector, 8, slice(3, 4))
         finish(8, (2,))

@@ -29,11 +29,6 @@ FLOPS = 2 * TOKENS * DIM * (ROPE_COLS + RANK) + 2 * 2 * TOKENS * RANK * NOPE_COL
 ROW_LATENT_BIAS, ROW_GAIN, ROW_SHIFT, ROW_WK_BIAS, ROW_ROPE_BIAS, ROW_WV_BIAS, ROWS = 0, 1, 2, 4, 8, 10, 14
 NORM_ROWS = 3
 
-WK_CHUNKS = (512, 512, 1024)
-WV_CHUNKS = (1024, 1024)
-
-ADD_LAG = 2
-
 
 def copy(nc, engine, out, in_):
     if engine == "vector":
@@ -92,7 +87,7 @@ def tile_mla_pa_kernel(
         keep = ctx.enter_context(tc.tile_pool(name="keep", bufs=1))
         stage = ctx.enter_context(tc.tile_pool(name="stage", bufs=10))
         a_pool = ctx.enter_context(tc.tile_pool(name="a_pool", bufs=2))
-        w_pool = ctx.enter_context(tc.tile_pool(name="w_pool", bufs=3))
+        w_pool = ctx.enter_context(tc.tile_pool(name="w_pool", bufs=4))
         norm = ctx.enter_context(tc.tile_pool(name="norm", bufs=2))
         banks = ctx.enter_context(tc.psum_pool(name="banks", bufs=8))
 
@@ -107,7 +102,7 @@ def tile_mla_pa_kernel(
         cos_pair = const.tile([P, TOKEN_TILES, ROPE], F32)
         sin_plus = const.tile([P, TOKEN_TILES, ROPE // 2], F32)
         sin_minus = const.tile([P, TOKEN_TILES, ROPE // 2], F32)
-        raw_wk = [raw.tile([P, PACK, width], BF16, tag="raw_wk%d" % c, name="raw_wk") for c, width in enumerate(WK_CHUNKS)]
+        raw_wk = raw.tile([P, PACK, NOPE_COLS], BF16)
         raw_rope = [raw.tile([P, PACK, ROPE_COLS], BF16, tag="raw_rope%d" % g, name="raw_rope") for g in range(PASSES)]
         x_codes = keep.tile([P, TOKEN_TILES, PASSES * P], U32, align_bytes=64)
         x_scales = keep.tile([P, TOKEN_TILES, PASSES * P], U8, align_bytes=64)
@@ -141,8 +136,8 @@ def tile_mla_pa_kernel(
                 out=spread[:, row : row + count, :].rearrange("p r c -> p (r c)"), in_=vector.partition_broadcast(P)
             )
 
-        def load_second_stage(tile_, weight, col0, width):
-            nc.sync.dma_start(out=tile_[:], in_=weight[:, col0 : col0 + width].rearrange("(t p) n -> p t n", p=P))
+        def load_second_stage(tile_, weight):
+            nc.sync.dma_start(out=tile_[:], in_=weight.rearrange("(t p) n -> p t n", p=P))
 
         with tc.tile_pool(name="head", bufs=1) as head, tc.tile_pool(name="x_staging", bufs=4) as x_staging:
             x_sb = head.tile([P, TOKEN_TILES, DIM], BF16)
@@ -158,8 +153,7 @@ def tile_mla_pa_kernel(
                 load_first_stage(raw_latent[g], g, ROPE_COLS, RANK)
             for tt in range(TOKEN_TILES):
                 load_x(tt)
-            for c, width in enumerate(WK_CHUNKS):
-                load_second_stage(raw_wk[c], wk_w, sum(WK_CHUNKS[:c]), width)
+            load_second_stage(raw_wk, wk_w)
             load_spread(ROW_WK_BIAS, wk_b)
 
             picked = {}
@@ -275,71 +269,96 @@ def tile_mla_pa_kernel(
         late = ctx.enter_context(tc.tile_pool(name="late", bufs=1, reuse_waits="tile"))
         outs = ctx.enter_context(tc.tile_pool(name="outs", bufs=5, reuse_waits="tile"))
         scratch = ctx.enter_context(tc.tile_pool(name="scratch", bufs=2, reuse_waits="tile"))
-        raw_wv = [late.tile([P, PACK, width], BF16, tag="raw_wv%d" % c, name="raw_wv") for c, width in enumerate(WV_CHUNKS)]
-        load_second_stage(raw_wv[0], wv_w, 0, WV_CHUNKS[0])
+        raw_wv = late.tile([P, PACK, NOPE_COLS], BF16)
+        load_second_stage(raw_wv, wv_w)
         load_spread(ROW_WV_BIAS, wv_b)
         for g in range(PASSES):
             load_first_stage(raw_rope[g], g, 0, ROPE_COLS)
-        load_second_stage(raw_wv[1], wv_w, WV_CHUNKS[0], WV_CHUNKS[1])
         load_spread(ROW_ROPE_BIAS, wkv_a_b[:ROPE_COLS])
 
-        def k_rope_unit(i):
-            return {
-                "rows": [raw_rope[g][:, :, i * UNIT : (i + 1) * UNIT] for g in range(PASSES)],
-                "bias": spread[:, ROW_ROPE_BIAS + i, :],
-                "flat_unit": NOPE_COLS // UNIT + i,
-                "dest": k_flat[:, NOPE_COLS + i * UNIT : NOPE_COLS + (i + 1) * UNIT],
-            }
+        def second_stage_pieces(tile_, i):
+            return [tile_[:, :, i * UNIT : (i + 1) * UNIT]]
 
-        def second_stage_unit(tiles, chunks, bias_row, flat, i, rotated):
-            c = max(j for j in range(len(chunks)) if sum(chunks[:j]) <= i * UNIT)
-            col0 = i * UNIT - sum(chunks[:c])
-            return {
-                "rows": [tiles[c][:, :, col0 : col0 + UNIT]],
-                "bias": spread[:, bias_row + i, :],
-                "flat_unit": i if rotated else None,
-                "dest": flat[:, i * UNIT : (i + 1) * UNIT],
-            }
+        def k_rope_pieces(i):
+            return [raw_rope[g][:, :, i * UNIT : (i + 1) * UNIT] for g in range(PASSES)]
 
-        wk_units = [second_stage_unit(raw_wk, WK_CHUNKS, ROW_WK_BIAS, k_flat, i, True) for i in range(NOPE_COLS // UNIT)]
-        wv_units = [second_stage_unit(raw_wv, WV_CHUNKS, ROW_WV_BIAS, v_flat, i, False) for i in range(NOPE_COLS // UNIT)]
-        units = [wk_units[0], wk_units[1], wv_units[0], wk_units[2], wv_units[1], wk_units[3], k_rope_unit(0), wv_units[2], k_rope_unit(1), wv_units[3]]
-        pieces = [(n, g) for n in range(len(units)) for g in range(len(units[n]["rows"]))]
+        columns = [
+            second_stage_pieces(raw_wk, 0), second_stage_pieces(raw_wk, 1),
+            second_stage_pieces(raw_wv, 0), second_stage_pieces(raw_wv, 1),
+            second_stage_pieces(raw_wk, 2), second_stage_pieces(raw_wk, 3),
+            k_rope_pieces(0),
+            second_stage_pieces(raw_wv, 2), second_stage_pieces(raw_wv, 3),
+            k_rope_pieces(1),
+        ]
+        WK_COLUMNS, WV_COLUMNS, K_ROPE_COLUMNS = (0, 1, 4, 5), (2, 3, 7, 8), (6, 9)
+        pieces = [(c, g) for c in range(len(columns)) for g in range(len(columns[c]))]
+        codes_of = {}
         grouped_of = {}
         regrouped = []
         quantised = []
 
-        def regroup_half(h):
+        def regroup_half(h, engine="scalar"):
             j = len(regrouped)
-            n, g = pieces[j]
+            c, g = pieces[j]
             if h == 0:
                 grouped_of[j] = stage.tile([P, UNIT * PACK], BF16, align_bytes=64, tag="grouped", name="grouped")
             width = UNIT // 2
             regroup(
-                nc, "scalar", grouped_of[j][:, h * width * PACK : (h + 1) * width * PACK],
-                units[n]["rows"][g][:, :, h * width : (h + 1) * width],
+                nc, engine, grouped_of[j][:, h * width * PACK : (h + 1) * width * PACK],
+                columns[c][g][:, :, h * width : (h + 1) * width],
             )
             if h == 1:
                 regrouped.append(j)
 
         def regroup_next(engine="scalar"):
             j = len(regrouped)
-            n, g = pieces[j]
+            c, g = pieces[j]
             grouped_of[j] = stage.tile([P, UNIT * PACK], BF16, align_bytes=64, tag="grouped", name="grouped")
-            regroup(nc, engine, grouped_of[j][:], units[n]["rows"][g])
+            regroup(nc, engine, grouped_of[j][:], columns[c][g])
             regrouped.append(j)
 
         def quantise_next():
             j = len(quantised)
             if j < len(pieces):
-                n, g = pieces[j]
+                c, g = pieces[j]
                 if g == 0:
-                    count = len(units[n]["rows"])
+                    count = len(columns[c])
                     pool, tag = (a_pool, "a") if count == PASSES else (w_pool, "w")
-                    units[n]["codes"] = pool.tile([P, count, UNIT], U32, align_bytes=64, tag=tag + "_codes", name="codes")
-                    units[n]["scales"] = pool.tile([P, count, UNIT], U8, align_bytes=64, tag=tag + "_scales", name="scales")
-                quantise(nc, grouped_of[j][:], units[n]["codes"][:, g, :], units[n]["scales"][:, g, :])
+                    codes_of[c] = (
+                        pool.tile([P, count, UNIT], U32, align_bytes=64, tag=tag + "_codes", name="codes"),
+                        pool.tile([P, count, UNIT], U8, align_bytes=64, tag=tag + "_scales", name="scales"),
+                    )
+                quantise(nc, grouped_of[j][:], codes_of[c][0][:, g, :], codes_of[c][1][:, g, :])
                 quantised.append(j)
+
+        def wk_unit(i):
+            return {
+                "columns": WK_COLUMNS[i : i + 1],
+                "bias_row": ROW_WK_BIAS + i,
+                "tiles": slice(0, TOKEN_TILES),
+                "first_block": (2 - 8 * i) % 3,
+                "dest": k_flat[:, i * UNIT : (i + 1) * UNIT],
+            }
+
+        def wv_unit(i, half):
+            return {
+                "columns": WV_COLUMNS[2 * i : 2 * i + 2],
+                "bias_row": ROW_WV_BIAS + 2 * i,
+                "tiles": slice(2 * half, 2 * half + 2),
+                "first_block": None,
+                "dest": v_flat[:, 2 * i * UNIT : 2 * (i + 1) * UNIT],
+            }
+
+        def k_rope_unit(i):
+            return {
+                "columns": K_ROPE_COLUMNS[i : i + 1],
+                "bias_row": ROW_ROPE_BIAS + i,
+                "tiles": slice(0, TOKEN_TILES),
+                "first_block": (2 - 32 - 8 * i) % 3,
+                "dest": k_flat[:, NOPE_COLS + i * UNIT : NOPE_COLS + (i + 1) * UNIT],
+            }
+
+        units = [wk_unit(0), wk_unit(1), wv_unit(0, 0), wk_unit(2), wv_unit(0, 1), wk_unit(3), k_rope_unit(0), wv_unit(1, 0), k_rope_unit(1), wv_unit(1, 1)]
 
         def add_latent_bias(tt):
             nc.vector.scalar_tensor_tensor(
@@ -400,48 +419,93 @@ def tile_mla_pa_kernel(
             tokens = slice(tt * P, (tt + 1) * P)
             quantise(nc, cn_grouped_of[tt][:], cn_codes[:, tokens], cn_scales[:, tokens])
 
-        def one_pass(unit, tt, g, last):
-            if len(unit["rows"]) == PASSES:
+        def pieces_of(n):
+            return sum(len(columns[c]) for c in range(max(units[n]["columns"]) + 1))
+
+        def one_pass(n, i, g, last):
+            unit = units[n]
+            halves = len(unit["columns"])
+            c = unit["columns"][i % halves]
+            tt = unit["tiles"].start + i // halves
+            if len(columns[c]) == PASSES:
                 tokens = slice(g * P, (g + 1) * P)
                 lhs_codes, lhs_scales = x_codes[:, tt, tokens], x_scales[:, tt, tokens]
             else:
                 tokens = slice(tt * P, (tt + 1) * P)
                 lhs_codes, lhs_scales = cn_codes[:, tokens], cn_scales[:, tokens]
             nc.tensor.matmul_mx(
-                out=unit["sums"][tt][:],
+                out=unit["sums"][i][:],
                 lhsT=lhs_codes.bitcast(FP8X4),
                 lhsT_scale=lhs_scales,
-                rhs=unit["codes"][:, g, :].bitcast(FP8X4),
-                rhs_scale=unit["scales"][:, g, :],
+                rhs=codes_of[c][0][:, g, :].bitcast(FP8X4),
+                rhs_scale=codes_of[c][1][:, g, :],
                 start=g == 0,
                 stop=last,
             )
 
-        def open_bank(n):
-            units[n].setdefault("sums", []).append(banks.tile([P, UNIT], F32, tag="bank", name="unit_sum"))
-            return units[n]["sums"][-1]
-
         def multiply_unit(n):
             unit = units[n]
-            while len(unit.get("sums", [])) < TOKEN_TILES:
-                open_bank(n)
-            count = len(unit["rows"])
-            ready = min(count, len(quantised) - pieces_of(n))
+            if "sums" not in unit:
+                unit["sums"] = [None] * 4
+                for i in range(4):
+                    unit["sums"][i] = banks.tile([P, UNIT], F32, tag="bank", name="unit_sum")
+            count = len(columns[unit["columns"][0]])
+            ready = min(count, count - (pieces_of(n) - len(quantised)))
             for g in range(unit.get("passes", 0), ready):
-                for tt in range(TOKEN_TILES):
-                    one_pass(unit, tt, g, g == count - 1)
+                for i in range(4):
+                    one_pass(n, i, g, g == count - 1)
             unit["passes"] = ready
 
-        def pieces_of(n):
-            return sum(len(u["rows"]) for u in units[:n])
-
         def store(unit, tiles):
-            nc.sync.dma_start(out=unit["dest"].rearrange("(t p) c -> p t c", p=P)[:, tiles, :], in_=unit["out"][:, tiles, :])
-
-        def add_bias(n, tt):
-            nc.vector.tensor_tensor(
-                out=units[n]["out"][:, tt, :], in0=units[n]["sums"][tt][:], in1=units[n]["bias"], op=ALU.add
+            first_tile = unit["tiles"].start
+            nc.sync.dma_start(
+                out=unit["dest"].rearrange("(t p) c -> p t c", p=P)[:, first_tile + tiles.start : first_tile + tiles.stop, :],
+                in_=unit["out"][:, tiles, :],
             )
+
+        def drain(n, parts=range(4), groups=None):
+            unit = units[n]
+            halves = len(unit["columns"])
+            count = 4 // halves
+            if parts[0] == 0:
+                unit["out"] = outs.tile([P, count, halves * UNIT], F32, tag="unit_out", name="unit_out")
+            for i in parts:
+                tile_, half = i // halves, i % halves
+                nc.vector.tensor_tensor(
+                    out=unit["out"][:, tile_, half * UNIT : (half + 1) * UNIT], in0=unit["sums"][i][:],
+                    in1=spread[:, unit["bias_row"] + half, :], op=ALU.add,
+                )
+                if half == halves - 1:
+                    if unit["first_block"] is None:
+                        store(unit, slice(tile_, tile_ + 1))
+                    else:
+                        for first_tile, end_tile in groups or ((0, count),):
+                            if tile_ + 1 == end_tile:
+                                rotate(nc.gpsimd, n, slice(first_tile, end_tile))
+
+        def rotate(engine, n, tiles):
+            unit = units[n]
+            first_tile = unit["tiles"].start
+            of_tokens = slice(first_tile + tiles.start, first_tile + tiles.stop)
+            unit.setdefault("adds", []).append(
+                rotate_products(
+                    engine, scratch, unit["out"][:, tiles, :], unit["first_block"], cos_pair[:, of_tokens, :],
+                    sin_minus[:, of_tokens, :], sin_plus[:, of_tokens, :],
+                ) + (tiles,)
+            )
+
+        def finish(n, parts=None):
+            adds = units[n]["adds"]
+            for i in range(len(adds)) if parts is None else parts:
+                pairs, straight, crossed, tiles = adds[i]
+                nc.vector.tensor_tensor(out=pairs, in0=straight, in1=crossed, op=ALU.add)
+                store(units[n], tiles)
+
+        def quantise_upto(count):
+            while len(quantised) < min(count, len(pieces)):
+                if len(regrouped) <= len(quantised):
+                    regroup_next()
+                quantise_next()
 
         add_latent_bias(0)
         quantise_x(2)
@@ -464,7 +528,7 @@ def tile_mla_pa_kernel(
         sum_squares(2)
         normalise(1)
         turn_cn(1)
-        keep_warm(2, raw_wk[0][:, 0, :])
+        keep_warm(2, raw_wk[:, 0, :UNIT])
         add_latent_bias(3)
         scale_cn(0)
         invert_std(2)
@@ -472,7 +536,7 @@ def tile_mla_pa_kernel(
         sum_squares(3)
         normalise(2)
         turn_cn(2)
-        keep_warm(2, raw_wk[0][:, 1, :])
+        keep_warm(2, raw_wk[:, 1, :UNIT])
         regroup_next("vector")
         scale_cn(1)
         invert_std(3)
@@ -482,7 +546,7 @@ def tile_mla_pa_kernel(
         quantise_cn(0)
         normalise(3)
         turn_cn(3)
-        keep_warm(2, raw_wk[0][:, 2, :])
+        keep_warm(2, raw_wk[:, 2, :UNIT])
         regroup_cn(1, "vector")
         scale_cn(3)
         regroup_next("vector")
@@ -493,63 +557,18 @@ def tile_mla_pa_kernel(
         regroup_cn(3, "vector")
         regroup_next("scalar")
         quantise_cn(3)
-        WHOLE = ((0, TOKEN_TILES),)
-
-        def drain(n, tiles=range(TOKEN_TILES), groups=WHOLE):
-            unit = units[n]
-            if tiles[0] == 0:
-                unit["out"] = outs.tile([P, TOKEN_TILES, UNIT], F32, tag="unit_out", name="unit_out")
-            for tt in tiles:
-                add_bias(n, tt)
-                if unit["flat_unit"] is None:
-                    if n == len(units) - 1:
-                        store(unit, slice(tt, tt + 1))
-                    elif tt % 2 == 1:
-                        store(unit, slice(tt - 1, tt + 1))
-                else:
-                    for first_tile, end_tile in groups:
-                        if tt + 1 == end_tile:
-                            rotate(nc.gpsimd, n, slice(first_tile, end_tile))
-
-        def rotate(engine, n, tiles):
-            unit = units[n]
-            unit.setdefault("adds", []).append(
-                rotate_products(
-                    engine, scratch, unit["out"][:, tiles, :], (2 - 8 * unit["flat_unit"]) % 3, cos_pair[:, tiles, :],
-                    sin_minus[:, tiles, :], sin_plus[:, tiles, :],
-                ) + (tiles,)
-            )
-
-        def finish(n, parts=None):
-            adds = units[n].get("adds", []) if n >= 0 else []
-            for i in range(len(adds)) if parts is None else parts:
-                pairs, straight, crossed, tiles = adds[i]
-                nc.vector.tensor_tensor(out=pairs, in0=straight, in1=crossed, op=ALU.add)
-                store(units[n], tiles)
-
-        def regroup_upto(count, engine="scalar"):
-            while len(regrouped) < count:
-                regroup_next(engine)
-
-        def quantise_upto(count):
-            while len(quantised) < min(count, len(pieces)):
-                if len(regrouped) <= len(quantised):
-                    regroup_next()
-                quantise_next()
-
-        quantise_upto(pieces_of(2))
+        quantise_upto(2)
         multiply_unit(0)
         multiply_unit(1)
         drain(0)
         drain(1)
-        quantise_upto(3)
-        multiply_unit(2)
         quantise_upto(4)
+        multiply_unit(2)
+        quantise_upto(5)
         multiply_unit(3)
         finish(0)
         drain(2)
         drain(3)
-        quantise_upto(5)
         multiply_unit(4)
         quantise_upto(6)
         multiply_unit(5)
@@ -557,18 +576,15 @@ def tile_mla_pa_kernel(
         quantise_upto(7)
         drain(4)
         drain(5)
-
-        quantise_upto(pieces_of(7))
+        quantise_upto(10)
         multiply_unit(6)
-        quantise_upto(pieces_of(8))
+        quantise_upto(12)
         multiply_unit(7)
         finish(3)
         drain(6, groups=((0, 2),))
         drain(7)
-
-        quantise_upto(pieces_of(9))
+        quantise_upto(16)
         multiply_unit(8)
-        quantise_upto(pieces_of(10))
         multiply_unit(9)
         finish(5)
         rotate(nc.vector, 6, slice(2, 4))

@@ -286,11 +286,10 @@ def tile_mla_pa_kernel(
             second_stage_pieces(raw_wk, 0), second_stage_pieces(raw_wk, 1),
             second_stage_pieces(raw_wv, 0), second_stage_pieces(raw_wv, 1),
             second_stage_pieces(raw_wk, 2), second_stage_pieces(raw_wk, 3),
-            k_rope_pieces(0),
             second_stage_pieces(raw_wv, 2), second_stage_pieces(raw_wv, 3),
-            k_rope_pieces(1),
+            k_rope_pieces(0), k_rope_pieces(1),
         ]
-        WK_COLUMNS, WV_COLUMNS, K_ROPE_COLUMNS = (0, 1, 4, 5), (2, 3, 7, 8), (6, 9)
+        WK_COLUMNS, WV_COLUMNS, K_ROPE_COLUMNS = (0, 1, 4, 5), (2, 3, 6, 7), (8, 9)
         pieces = [(c, g) for c in range(len(columns)) for g in range(len(columns[c]))]
         codes_of = {}
         grouped_of = {}
@@ -331,22 +330,13 @@ def tile_mla_pa_kernel(
                 quantise(nc, grouped_of[j][:], codes_of[c][0][:, g, :], codes_of[c][1][:, g, :])
                 quantised.append(j)
 
-        def wk_unit(i):
+        def wide_unit(column_pair, bias_row, flat, i, half, rotated):
             return {
-                "columns": WK_COLUMNS[i : i + 1],
-                "bias_row": ROW_WK_BIAS + i,
-                "tiles": slice(0, TOKEN_TILES),
-                "first_block": (2 - 8 * i) % 3,
-                "dest": k_flat[:, i * UNIT : (i + 1) * UNIT],
-            }
-
-        def wv_unit(i, half):
-            return {
-                "columns": WV_COLUMNS[2 * i : 2 * i + 2],
-                "bias_row": ROW_WV_BIAS + 2 * i,
+                "columns": column_pair,
+                "bias_row": bias_row + 2 * i,
                 "tiles": slice(2 * half, 2 * half + 2),
-                "first_block": None,
-                "dest": v_flat[:, 2 * i * UNIT : 2 * (i + 1) * UNIT],
+                "first_block": (2 - 16 * i) % 3 if rotated else None,
+                "dest": flat[:, 2 * i * UNIT : 2 * (i + 1) * UNIT],
             }
 
         def k_rope_unit(i):
@@ -358,7 +348,13 @@ def tile_mla_pa_kernel(
                 "dest": k_flat[:, NOPE_COLS + i * UNIT : NOPE_COLS + (i + 1) * UNIT],
             }
 
-        units = [wk_unit(0), wk_unit(1), wv_unit(0, 0), wk_unit(2), wv_unit(0, 1), wk_unit(3), k_rope_unit(0), wv_unit(1, 0), k_rope_unit(1), wv_unit(1, 1)]
+        def wk_unit(i, half):
+            return wide_unit(WK_COLUMNS[2 * i : 2 * i + 2], ROW_WK_BIAS, k_flat, i, half, True)
+
+        def wv_unit(i, half):
+            return wide_unit(WV_COLUMNS[2 * i : 2 * i + 2], ROW_WV_BIAS, v_flat, i, half, False)
+
+        units = [wk_unit(0, 0), wk_unit(0, 1), wv_unit(0, 0), wv_unit(0, 1), wk_unit(1, 0), wv_unit(1, 0), wk_unit(1, 1), wv_unit(1, 1), k_rope_unit(0), k_rope_unit(1)]
 
         def add_latent_bias(tt):
             nc.vector.scalar_tensor_tensor(
@@ -450,7 +446,7 @@ def tile_mla_pa_kernel(
                 for i in range(4):
                     unit["sums"][i] = banks.tile([P, UNIT], F32, tag="bank", name="unit_sum")
             count = len(columns[unit["columns"][0]])
-            ready = min(count, count - (pieces_of(n) - len(quantised)))
+            ready = max(0, min(count, count - (pieces_of(n) - len(quantised))))
             for g in range(unit.get("passes", 0), ready):
                 for i in range(4):
                     one_pass(n, i, g, g == count - 1)
@@ -479,7 +475,7 @@ def tile_mla_pa_kernel(
                     if unit["first_block"] is None:
                         store(unit, slice(tile_, tile_ + 1))
                     else:
-                        for first_tile, end_tile in groups or ((0, count),):
+                        for first_tile, end_tile in ((0, count),) if groups is None else groups:
                             if tile_ + 1 == end_tile:
                                 rotate(nc.gpsimd, n, slice(first_tile, end_tile))
 
@@ -500,6 +496,10 @@ def tile_mla_pa_kernel(
                 pairs, straight, crossed, tiles = adds[i]
                 nc.vector.tensor_tensor(out=pairs, in0=straight, in1=crossed, op=ALU.add)
                 store(units[n], tiles)
+
+        def regroup_upto(count, engine="scalar"):
+            while len(regrouped) < count:
+                regroup_next(engine)
 
         def quantise_upto(count):
             while len(quantised) < min(count, len(pieces)):
@@ -561,37 +561,42 @@ def tile_mla_pa_kernel(
         multiply_unit(0)
         multiply_unit(1)
         drain(0)
-        drain(1)
         quantise_upto(4)
         multiply_unit(2)
-        quantise_upto(5)
+        drain(1)
         multiply_unit(3)
-        finish(0)
         drain(2)
         drain(3)
-        multiply_unit(4)
-        quantise_upto(6)
-        multiply_unit(5)
+        finish(0)
         finish(1)
-        quantise_upto(7)
+        quantise_upto(8)
+        multiply_unit(4)
+        multiply_unit(5)
         drain(4)
-        drain(5)
         quantise_upto(10)
         multiply_unit(6)
-        quantise_upto(12)
+        drain(5)
         multiply_unit(7)
-        finish(3)
-        drain(6, groups=((0, 2),))
-        drain(7)
-        quantise_upto(16)
+        drain(6)
+        finish(4)
+        quantise_upto(13)
         multiply_unit(8)
+        drain(7)
         multiply_unit(9)
-        finish(5)
-        rotate(nc.vector, 6, slice(2, 4))
+        drain(8, groups=())
         finish(6)
-        drain(8, groups=((0, 2),))
-        drain(9)
-        rotate(nc.vector, 8, slice(2, 3))
-        finish(8, (0, 1))
-        rotate(nc.vector, 8, slice(3, 4))
-        finish(8, (2,))
+        quantise_upto(15)
+        multiply_unit(9)
+        quantise_upto(16)
+        multiply_unit(9)
+        rotate(nc.vector, 8, slice(0, 4))
+        finish(8)
+        quantise_upto(16)
+        multiply_unit(9)
+        drain(9, groups=())
+        rotate(nc.vector, 9, slice(0, 1))
+        rotate(nc.vector, 9, slice(1, 2))
+        finish(9, (0, 1))
+        rotate(nc.vector, 9, slice(2, 3))
+        rotate(nc.vector, 9, slice(3, 4))
+        finish(9, (2, 3))

@@ -85,7 +85,7 @@ def tile_mla_pa_kernel(
         const = ctx.enter_context(tc.tile_pool(name="const", bufs=1))
         raw = ctx.enter_context(tc.tile_pool(name="raw", bufs=1))
         keep = ctx.enter_context(tc.tile_pool(name="keep", bufs=1))
-        stage = ctx.enter_context(tc.tile_pool(name="stage", bufs=10))
+        stage = ctx.enter_context(tc.tile_pool(name="stage", bufs=8))
         a_pool = ctx.enter_context(tc.tile_pool(name="a_pool", bufs=2))
         w_pool = ctx.enter_context(tc.tile_pool(name="w_pool", bufs=4))
         norm = ctx.enter_context(tc.tile_pool(name="norm", bufs=2))
@@ -118,8 +118,8 @@ def tile_mla_pa_kernel(
         nc.vector.memset(eps[:], EPS)
         make_identity(nc, ident_f32[:])
         make_identity(nc, ident_bf[:])
-        nc.gpsimd.dma_start(out=cos_sin[:, 0], in_=cos.rearrange("(a p) j -> p a j", p=P))
-        nc.gpsimd.dma_start(out=cos_sin[:, 1], in_=sin.rearrange("(a p) j -> p a j", p=P))
+        nc.scalar.dma_start(out=cos_sin[:, 0], in_=cos.rearrange("(a p) j -> p a j", p=P))
+        nc.scalar.dma_start(out=cos_sin[:, 1], in_=sin.rearrange("(a p) j -> p a j", p=P))
         nc.scalar.activation(out=first[:], in_=eps[:], func=ACT.Abs_reciprocal_sqrt, bias=eps[:], scale=1.0)
 
         def load_first_stage(tile_, g, col0, width):
@@ -178,14 +178,12 @@ def tile_mla_pa_kernel(
 
             for b in range(BATCH):
                 tiles = slice(b * SEQ_TILES, (b + 1) * SEQ_TILES)
-                nc.gpsimd.tensor_copy(
+                nc.scalar.copy(
                     out=cos_pair[:, tiles, :].rearrange("p a (j e) -> p a j e", e=2),
                     in_=cos_sin[:, 0].unsqueeze(3).to_broadcast([P, SEQ_TILES, ROPE // 2, 2]),
                 )
-                nc.gpsimd.tensor_copy(out=sin_plus[:, tiles, :], in_=cos_sin[:, 1])
-                nc.gpsimd.tensor_scalar(
-                    out=sin_minus[:, tiles, :], in0=cos_sin[:, 1], scalar1=-1.0, scalar2=None, op0=ALU.mult
-                )
+                nc.scalar.copy(out=sin_plus[:, tiles, :], in_=cos_sin[:, 1])
+                nc.scalar.mul(out=sin_minus[:, tiles, :], in_=cos_sin[:, 1], mul=-1.0)
 
             latent_codes = a_pool.tile([P, PASSES, UNIT], U32, align_bytes=64, tag="a_codes")
             latent_scales = a_pool.tile([P, PASSES, UNIT], U8, align_bytes=64, tag="a_scales")
@@ -267,7 +265,7 @@ def tile_mla_pa_kernel(
             multiply_latent(1, (0, 1, 2, 3))
 
         late = ctx.enter_context(tc.tile_pool(name="late", bufs=1, reuse_waits="tile"))
-        outs = ctx.enter_context(tc.tile_pool(name="outs", bufs=5, reuse_waits="tile"))
+        outs = ctx.enter_context(tc.tile_pool(name="outs", bufs=6, reuse_waits="tile"))
         scratch = ctx.enter_context(tc.tile_pool(name="scratch", bufs=2, reuse_waits="tile"))
         raw_wv = late.tile([P, PACK, NOPE_COLS], BF16)
         load_second_stage(raw_wv, wv_w)
@@ -530,6 +528,7 @@ def tile_mla_pa_kernel(
         turn_cn(1)
         keep_warm(2, raw_wk[:, 0, :UNIT])
         add_latent_bias(3)
+        regroup_half(0, "vector")
         scale_cn(0)
         invert_std(2)
         negate_mean(3)
@@ -537,7 +536,7 @@ def tile_mla_pa_kernel(
         normalise(2)
         turn_cn(2)
         keep_warm(2, raw_wk[:, 1, :UNIT])
-        regroup_next("vector")
+        regroup_half(1, "vector")
         scale_cn(1)
         invert_std(3)
         regroup_cn(0, "vector")

from contextlib import ExitStack

import concourse.mybir as mybir
from concourse.masks import make_identity

F32 = mybir.dt.float32
BF16 = mybir.dt.bfloat16
U32 = mybir.dt.uint32
U8 = mybir.dt.uint8
FP8X4 = mybir.dt.float8_e4m3fn_x4
ALU = mybir.AluOpType
ACT = mybir.ActivationFunctionType

P = 128
PACK = 4
K_PASS = P * PACK
BATCH, SEQ, DIM, HEADS, NOPE, ROPE, RANK = 2, 256, 2048, 16, 128, 64, 512
HEAD = NOPE + ROPE
TOKENS = BATCH * SEQ
TOKEN_TILES = TOKENS // P
SEQ_TILES = SEQ // P
PASSES = DIM // K_PASS
UNIT = 512
ROPE_COLS = HEADS * ROPE
NOPE_COLS = HEADS * NOPE
EPS = 1e-5
FLOPS = 2 * TOKENS * DIM * (ROPE_COLS + RANK) + 2 * 2 * TOKENS * RANK * NOPE_COLS

ROW_LATENT_BIAS, ROW_GAIN, ROW_SHIFT, ROW_WK_BIAS, ROW_ROPE_BIAS, ROW_WV_BIAS, ROWS = 0, 1, 2, 4, 8, 10, 14
NORM_ROWS = 3


def copy(nc, engine, out, in_):
    if engine == "vector":
        nc.vector.tensor_copy(out=out, in_=in_)
    elif engine == "scalar":
        nc.scalar.copy(out=out, in_=in_)
    else:
        nc.gpsimd.tensor_scalar(out=out, in0=in_, scalar1=1.0, scalar2=0.0, op0=ALU.mult, op1=ALU.add)


def regroup(nc, engine, grouped, rows):
    copy(
        nc,
        engine,
        grouped.rearrange("p (c i t) -> p c t i", i=4, t=PACK),
        rows.rearrange("p t (c i) -> p c t i", i=4),
    )


def quantise(nc, grouped, codes, scales):
    nc.vector.quantize_mx(out=codes.bitcast(FP8X4), scales=scales, in_=grouped)


def rotate_products(engine, scratch, unit_out, first_block, cos_pair, sin_minus, sin_plus):
    blocks = unit_out.rearrange("p t (k d) -> p t k d", d=ROPE)[:, :, first_block::3, :]
    n = blocks.shape[2]
    pairs = blocks.rearrange("p t n (j e) -> p t n j e", e=2)
    tiles = blocks.shape[1]
    half = [P, tiles, n, ROPE // 2]
    crossed = scratch.tile([P, 2, tiles, n, ROPE // 2], F32, tag="crossed")
    engine.tensor_tensor(
        out=crossed[:, 0], in0=pairs[:, :, :, :, 1], in1=sin_minus.unsqueeze(2).to_broadcast(half), op=ALU.mult
    )
    engine.tensor_tensor(
        out=crossed[:, 1], in0=pairs[:, :, :, :, 0], in1=sin_plus.unsqueeze(2).to_broadcast(half), op=ALU.mult
    )
    straight = scratch.tile([P, tiles, n, ROPE], F32, tag="straight")
    engine.tensor_tensor(
        out=straight[:], in0=blocks, in1=cos_pair.unsqueeze(2).to_broadcast([P, tiles, n, ROPE]), op=ALU.mult
    )
    return pairs, straight[:].rearrange("p t n (j e) -> p t n j e", e=2), crossed[:].rearrange("p e t n j -> p t n j e")


def tile_mla_pa_kernel(
    tc, x, wkv_a_w, wkv_a_b, kvn_g, kvn_b, wk_w, wk_b, wv_w, wv_b, cos, sin, out_0, out_1
):
    nc = tc.nc
    x_rows = x.flatten_outer_dims()
    k_flat = out_0.rearrange("b s h d -> (b s) (h d)")
    v_flat = out_1.rearrange("b s h d -> (b s) (h d)")

    with ExitStack() as ctx:
        ctx.enter_context(tc.manual_schedule())
        const = ctx.enter_context(tc.tile_pool(name="const", bufs=1))
        raw = ctx.enter_context(tc.tile_pool(name="raw", bufs=1))
        keep = ctx.enter_context(tc.tile_pool(name="keep", bufs=1))
        stage = ctx.enter_context(tc.tile_pool(name="stage", bufs=8))
        a_pool = ctx.enter_context(tc.tile_pool(name="a_pool", bufs=2))
        w_pool = ctx.enter_context(tc.tile_pool(name="w_pool", bufs=4))
        norm = ctx.enter_context(tc.tile_pool(name="norm", bufs=2))
        banks = ctx.enter_context(tc.psum_pool(name="banks", bufs=8))

        norm_rows = const.tile([P, UNIT], BF16)
        cos_sin = const.tile([P, 2, SEQ_TILES, ROPE // 2], BF16)
        ident_f32 = const.tile([P, P], F32)
        ident_bf = const.tile([P, P], BF16)
        eps = const.tile([P, 1], F32)
        first = const.tile([P, 1], F32)
        spread = const.tile([P, ROWS, UNIT], BF16)
        norm_cols = const.tile([P, NORM_ROWS, PACK], F32)
        cos_pair = const.tile([P, TOKEN_TILES, ROPE], F32)
        sin_plus = const.tile([P, TOKEN_TILES, ROPE // 2], F32)
        sin_minus = const.tile([P, TOKEN_TILES, ROPE // 2], F32)
        raw_wk = raw.tile([P, PACK, NOPE_COLS], BF16)
        raw_rope = [raw.tile([P, PACK, ROPE_COLS], BF16, tag="raw_rope%d" % g, name="raw_rope") for g in range(PASSES)]
        x_codes = keep.tile([P, TOKEN_TILES, PASSES * P], U32, align_bytes=64)
        x_scales = keep.tile([P, TOKEN_TILES, PASSES * P], U8, align_bytes=64)
        c_all = keep.tile([P, TOKEN_TILES, RANK], F32)
        c_sum = keep.tile([P, TOKEN_TILES], F32)
        minus_mean = keep.tile([P, TOKEN_TILES], F32)
        square_sum = keep.tile([P, TOKEN_TILES], F32)
        inv_std = keep.tile([P, TOKEN_TILES], F32)
        cn_codes = keep.tile([P, TOKENS], U32, align_bytes=64)
        cn_scales = keep.tile([P, TOKENS], U8, align_bytes=64)

        nc.vector.memset(norm_rows[:].bitcast(U32), 0)
        nc.vector.memset(eps[:], EPS)
        make_identity(nc, ident_f32[:])
        make_identity(nc, ident_bf[:])
        nc.scalar.dma_start(out=cos_sin[:, 0], in_=cos.rearrange("(a p) j -> p a j", p=P))
        nc.scalar.dma_start(out=cos_sin[:, 1], in_=sin.rearrange("(a p) j -> p a j", p=P))
        nc.scalar.activation(out=first[:], in_=eps[:], func=ACT.Abs_reciprocal_sqrt, bias=eps[:], scale=1.0)

        def load_first_stage(tile_, g, col0, width):
            for u in range(2):
                row0 = g * K_PASS + u * 2 * P
                nc.sync.dma_start(
                    out=tile_[:, 2 * u : 2 * u + 2, :],
                    in_=wkv_a_w[row0 : row0 + 2 * P, col0 : col0 + width].rearrange("(q e) c -> q e c", e=2),
                )

        def load_spread(row, vector):
            count = vector.shape[0] // UNIT
            nc.sync.dma_start(
                out=spread[:, row : row + count, :].rearrange("p r c -> p (r c)"), in_=vector.partition_broadcast(P)
            )

        def load_second_stage(tile_, weight):
            nc.sync.dma_start(out=tile_[:], in_=weight.rearrange("(t p) n -> p t n", p=P))

        with tc.tile_pool(name="head", bufs=1) as head, tc.tile_pool(name="x_staging", bufs=4) as x_staging:
            x_sb = head.tile([P, TOKEN_TILES, DIM], BF16)
            raw_latent = [head.tile([P, PACK, RANK], BF16, tag="raw_latent%d" % g, name="raw_latent") for g in range(PASSES)]

            def load_x(tt):
                nc.sync.dma_start(out=x_sb[:, tt, :], in_=x_rows[tt * P : (tt + 1) * P, :])

            load_first_stage(raw_latent[0], 0, ROPE_COLS, RANK)
            for row, vector in ((ROW_LATENT_BIAS, wkv_a_b[ROPE_COLS:]), (ROW_GAIN, kvn_g), (ROW_SHIFT, kvn_b)):
                nc.sync.dma_start(out=norm_rows[row : row + 1, :], in_=vector.rearrange("(r c) -> r c", c=UNIT))
            for g in range(1, PASSES):
                load_first_stage(raw_latent[g], g, ROPE_COLS, RANK)
            for tt in range(TOKEN_TILES):
                load_x(tt)
            load_second_stage(raw_wk, wk_w)
            load_spread(ROW_WK_BIAS, wk_b)

            picked = {}

            def pick_rows(r, count):
                picked[r] = banks.tile([P, count, UNIT], BF16, tag="bank", name="picked")
                for i in range(count):
                    nc.tensor.matmul(
                        out=picked[r][:, i, :], lhsT=ident_bf[:, r + i : r + i + 1].to_broadcast([P, P]), rhs=norm_rows[:],
                        start=True, stop=True,
                    )

            def turn_norm_rows():
                turned_rows = banks.tile([P, PACK, P], BF16, tag="bank", name="turned_rows")
                for t in range(PACK):
                    nc.tensor.transpose(turned_rows[:, t, :], norm_rows[:, t * P : (t + 1) * P], ident_bf[:])
                nc.vector.tensor_copy(out=norm_cols[:], in_=turned_rows[:, :, :NORM_ROWS].rearrange("p t r -> p r t"))

            def spread_rows(r, engine):
                bank = picked[r]
                copy(nc, engine, spread[:, r : r + bank.shape[1], :], bank[:])

            for b in range(BATCH):
                tiles = slice(b * SEQ_TILES, (b + 1) * SEQ_TILES)
                nc.scalar.copy(
                    out=cos_pair[:, tiles, :].rearrange("p a (j e) -> p a j e", e=2),
                    in_=cos_sin[:, 0].unsqueeze(3).to_broadcast([P, SEQ_TILES, ROPE // 2, 2]),
                )
                nc.scalar.copy(out=sin_plus[:, tiles, :], in_=cos_sin[:, 1])
                nc.scalar.mul(out=sin_minus[:, tiles, :], in_=cos_sin[:, 1], mul=-1.0)

            latent_codes = a_pool.tile([P, PASSES, UNIT], U32, align_bytes=64, tag="a_codes")
            latent_scales = a_pool.tile([P, PASSES, UNIT], U8, align_bytes=64, tag="a_scales")
            latent_grouped = [None] * PASSES
            latent_sums = [None] * TOKEN_TILES
            x_grouped = [None] * TOKEN_TILES

            def keep_warm(count, rhs):
                bank = banks.tile([P, UNIT], F32, tag="bank", name="unread")
                for i in range(count):
                    nc.tensor.matmul(out=bank[:], lhsT=ident_bf[:], rhs=rhs, start=True, stop=True)

            def regroup_latent(g, engine):
                latent_grouped[g] = stage.tile([P, UNIT * PACK], BF16, align_bytes=64, tag="grouped", name="grouped")
                regroup(nc, engine, latent_grouped[g][:], raw_latent[g][:])

            def quantise_latent(g):
                quantise(nc, latent_grouped[g][:], latent_codes[:, g, :], latent_scales[:, g, :])

            def turn_x(tt, engines):
                words = x_sb[:, tt, :].bitcast(F32)
                x_grouped[tt] = x_staging.tile([P, PASSES * P * PACK], BF16, align_bytes=64, tag="x_grouped", name="x_grouped")
                out_words = x_grouped[tt][:].bitcast(F32).rearrange("p (g k u) -> p g k u", g=PASSES, u=2)
                for half in range(2):
                    turned = banks.tile([P, 2, 2, P], F32, tag="bank", name="turned")
                    for i in range(2):
                        for u in range(2):
                            col0 = (2 * (2 * half + i) + u) * P
                            nc.tensor.transpose(turned[:, i, u, :], words[:, col0 : col0 + P], ident_f32[:])
                    copy(
                        nc, engines[half], out_words[:, 2 * half : 2 * half + 2, :, :],
                        turned[:].rearrange("p i u k -> p i k u"),
                    )

            def quantise_x(tt):
                quantise(nc, x_grouped[tt][:], x_codes[:, tt, :], x_scales[:, tt, :])

            def open_latent(tt):
                latent_sums[tt] = banks.tile([P, UNIT], F32, tag="bank", name="latent_sum")

            def multiply_latent(tt, passes):
                for g in passes:
                    tokens = slice(g * P, (g + 1) * P)
                    nc.tensor.matmul_mx(
                        out=latent_sums[tt][:],
                        lhsT=x_codes[:, tt, tokens].bitcast(FP8X4),
                        lhsT_scale=x_scales[:, tt, tokens],
                        rhs=latent_codes[:, g, :].bitcast(FP8X4),
                        rhs_scale=latent_scales[:, g, :],
                        start=g == 0,
                        stop=g == PASSES - 1,
                    )

            regroup_latent(0, "vector")
            pick_rows(ROW_LATENT_BIAS, 1)
            turn_norm_rows()
            spread_rows(ROW_LATENT_BIAS, "scalar")
            keep_warm(2, raw_latent[1][:, 0, :])
            regroup_latent(1, "scalar")
            quantise_latent(0)
            keep_warm(2, raw_latent[2][:, 0, :])
            regroup_latent(2, "vector")
            quantise_latent(1)
            quantise_latent(2)
            keep_warm(2, raw_latent[3][:, 0, :])
            regroup_latent(3, "scalar")
            turn_x(0, ("vector", "vector"))
            keep_warm(2, raw_latent[0][:, 0, :])
            quantise_latent(3)
            turn_x(1, ("scalar", "scalar"))
            keep_warm(2, raw_latent[0][:, 1, :])
            quantise_x(0)
            turn_x(2, ("scalar", "scalar"))
            open_latent(0)
            multiply_latent(0, (0, 1, 2, 3))
            turn_x(3, ("scalar", "scalar"))
            quantise_x(1)
            open_latent(1)
            multiply_latent(1, (0, 1, 2, 3))

        late = ctx.enter_context(tc.tile_pool(name="late", bufs=1, reuse_waits="tile"))
        outs = ctx.enter_context(tc.tile_pool(name="outs", bufs=6, reuse_waits="tile"))
        scratch = ctx.enter_context(tc.tile_pool(name="scratch", bufs=2, reuse_waits="tile"))
        raw_wv = late.tile([P, PACK, NOPE_COLS], BF16)
        load_second_stage(raw_wv, wv_w)
        load_spread(ROW_WV_BIAS, wv_b)
        for g in range(PASSES):
            load_first_stage(raw_rope[g], g, 0, ROPE_COLS)
        load_spread(ROW_ROPE_BIAS, wkv_a_b[:ROPE_COLS])

        def second_stage_pieces(tile_, i):
            return [tile_[:, :, i * UNIT : (i + 1) * UNIT]]

        def k_rope_pieces(i):
            return [raw_rope[g][:, :, i * UNIT : (i + 1) * UNIT] for g in range(PASSES)]

        columns = [
            second_stage_pieces(raw_wk, 0), second_stage_pieces(raw_wk, 1),
            second_stage_pieces(raw_wv, 0), second_stage_pieces(raw_wv, 1),
            second_stage_pieces(raw_wk, 2), second_stage_pieces(raw_wk, 3),
            second_stage_pieces(raw_wv, 2), second_stage_pieces(raw_wv, 3),
            k_rope_pieces(0), k_rope_pieces(1),
        ]
        WK_COLUMNS, WV_COLUMNS, K_ROPE_COLUMNS = (0, 1, 4, 5), (2, 3, 6, 7), (8, 9)
        pieces = [(c, g) for c in range(len(columns)) for g in range(len(columns[c]))]
        codes_of = {}
        grouped_of = {}
        regrouped = []
        quantised = []

        def regroup_half(h, engine="scalar"):
            j = len(regrouped)
            c, g = pieces[j]
            if h == 0:
                grouped_of[j] = stage.tile([P, UNIT * PACK], BF16, align_bytes=64, tag="grouped", name="grouped")
            width = UNIT // 2
            regroup(
                nc, engine, grouped_of[j][:, h * width * PACK : (h + 1) * width * PACK],
                columns[c][g][:, :, h * width : (h + 1) * width],
            )
            if h == 1:
                regrouped.append(j)

        def regroup_next(engine="scalar"):
            j = len(regrouped)
            c, g = pieces[j]
            grouped_of[j] = stage.tile([P, UNIT * PACK], BF16, align_bytes=64, tag="grouped", name="grouped")
            regroup(nc, engine, grouped_of[j][:], columns[c][g])
            regrouped.append(j)

        def quantise_next():
            j = len(quantised)
            if j < len(pieces):
                c, g = pieces[j]
                if g == 0:
                    count = len(columns[c])
                    pool, tag = (a_pool, "a") if count == PASSES else (w_pool, "w")
                    codes_of[c] = (
                        pool.tile([P, count, UNIT], U32, align_bytes=64, tag=tag + "_codes", name="codes"),
                        pool.tile([P, count, UNIT], U8, align_bytes=64, tag=tag + "_scales", name="scales"),
                    )
                quantise(nc, grouped_of[j][:], codes_of[c][0][:, g, :], codes_of[c][1][:, g, :])
                quantised.append(j)

        def wide_unit(column_pair, bias_row, flat, i, half, rotated):
            return {
                "columns": column_pair,
                "bias_row": bias_row + 2 * i,
                "tiles": slice(2 * half, 2 * half + 2),
                "first_block": (2 - 16 * i) % 3 if rotated else None,
                "dest": flat[:, 2 * i * UNIT : 2 * (i + 1) * UNIT],
            }

        def k_rope_unit(i):
            return {
                "columns": K_ROPE_COLUMNS[i : i + 1],
                "bias_row": ROW_ROPE_BIAS + i,
                "tiles": slice(0, TOKEN_TILES),
                "first_block": (2 - 32 - 8 * i) % 3,
                "dest": k_flat[:, NOPE_COLS + i * UNIT : NOPE_COLS + (i + 1) * UNIT],
            }

        def wk_unit(i, half):
            return wide_unit(WK_COLUMNS[2 * i : 2 * i + 2], ROW_WK_BIAS, k_flat, i, half, True)

        def wv_unit(i, half):
            return wide_unit(WV_COLUMNS[2 * i : 2 * i + 2], ROW_WV_BIAS, v_flat, i, half, False)

        units = [wk_unit(0, 0), wk_unit(0, 1), wv_unit(0, 0), wv_unit(0, 1), wk_unit(1, 0), wv_unit(1, 0), wk_unit(1, 1), wv_unit(1, 1), k_rope_unit(0), k_rope_unit(1)]

        def add_latent_bias(tt):
            nc.vector.scalar_tensor_tensor(
                out=c_all[:, tt, :], in0=latent_sums[tt][:], scalar=1.0, in1=spread[:, ROW_LATENT_BIAS, :],
                op0=ALU.mult, op1=ALU.add, accum_out=c_sum[:, tt : tt + 1],
            )

        def negate_mean(tt):
            one_tile = slice(tt, tt + 1)
            nc.scalar.mul(out=minus_mean[:, one_tile], in_=c_sum[:, one_tile], mul=-1.0 / RANK)

        def sum_squares(tt):
            one_tile = slice(tt, tt + 1)
            squares = norm.tile([P, RANK], BF16, tag="squares", name="squares")
            nc.scalar.activation(
                out=squares[:], in_=c_all[:, tt, :], func=ACT.Square, bias=minus_mean[:, one_tile], scale=1.0,
                accum_out=square_sum[:, one_tile],
            )

        def invert_std(tt):
            one_tile = slice(tt, tt + 1)
            nc.scalar.activation(
                out=inv_std[:, one_tile], in_=square_sum[:, one_tile], func=ACT.Abs_reciprocal_sqrt, bias=eps[:],
                scale=1.0 / RANK,
            )

        normed_of = {}

        def normalise(tt):
            normed_of[tt] = norm.tile([P, RANK], F32, tag="normed", name="normed")
            nc.vector.tensor_scalar(
                out=normed_of[tt][:], in0=c_all[:, tt, :], scalar1=minus_mean[:, tt : tt + 1],
                scalar2=inv_std[:, tt : tt + 1], op0=ALU.add, op1=ALU.mult,
            )

        turned_of = {}
        cn_of = {}
        cn_grouped_of = {}

        def turn_cn(tt):
            turned_of[tt] = banks.tile([P, PACK, P], F32, tag="bank", name="normed_turned")
            for t in range(PACK):
                nc.tensor.transpose(turned_of[tt][:, t, :], normed_of[tt][:, t * P : (t + 1) * P], ident_f32[:])

        def scale_cn(tt):
            cn_of[tt] = norm.tile([P, PACK, P], BF16, tag="cn", name="cn")
            for t in range(PACK):
                nc.scalar.activation(
                    out=cn_of[tt][:, t, :], in_=turned_of[tt][:, t, :], func=ACT.Identity,
                    bias=norm_cols[:, ROW_SHIFT, t : t + 1], scale=norm_cols[:, ROW_GAIN, t : t + 1],
                )

        def regroup_cn(tt, engine):
            cn_grouped_of[tt] = norm.tile([P, P * PACK], BF16, align_bytes=64, tag="cn_grouped", name="cn_grouped")
            regroup(nc, engine, cn_grouped_of[tt][:], cn_of[tt][:])

        def quantise_cn(tt):
            tokens = slice(tt * P, (tt + 1) * P)
            quantise(nc, cn_grouped_of[tt][:], cn_codes[:, tokens], cn_scales[:, tokens])

        def pieces_of(n):
            return sum(len(columns[c]) for c in range(max(units[n]["columns"]) + 1))

        def one_pass(n, i, g, last):
            unit = units[n]
            halves = len(unit["columns"])
            c = unit["columns"][i % halves]
            tt = unit["tiles"].start + i // halves
            if len(columns[c]) == PASSES:
                tokens = slice(g * P, (g + 1) * P)
                lhs_codes, lhs_scales = x_codes[:, tt, tokens], x_scales[:, tt, tokens]
            else:
                tokens = slice(tt * P, (tt + 1) * P)
                lhs_codes, lhs_scales = cn_codes[:, tokens], cn_scales[:, tokens]
            nc.tensor.matmul_mx(
                out=unit["sums"][i][:],
                lhsT=lhs_codes.bitcast(FP8X4),
                lhsT_scale=lhs_scales,
                rhs=codes_of[c][0][:, g, :].bitcast(FP8X4),
                rhs_scale=codes_of[c][1][:, g, :],
                start=g == 0,
                stop=last,
            )

        def multiply_unit(n):
            unit = units[n]
            if "sums" not in unit:
                unit["sums"] = [None] * 4
                for i in range(4):
                    unit["sums"][i] = banks.tile([P, UNIT], F32, tag="bank", name="unit_sum")
            count = len(columns[unit["columns"][0]])
            ready = max(0, min(count, count - (pieces_of(n) - len(quantised))))
            for g in range(unit.get("passes", 0), ready):
                for i in range(4):
                    one_pass(n, i, g, g == count - 1)
            unit["passes"] = ready

        def store(unit, tiles):
            first_tile = unit["tiles"].start
            nc.sync.dma_start(
                out=unit["dest"].rearrange("(t p) c -> p t c", p=P)[:, first_tile + tiles.start : first_tile + tiles.stop, :],
                in_=unit["out"][:, tiles, :],
            )

        def drain(n, parts=range(4), groups=None):
            unit = units[n]
            halves = len(unit["columns"])
            count = 4 // halves
            if parts[0] == 0:
                unit["out"] = outs.tile([P, count, halves * UNIT], F32, tag="unit_out", name="unit_out")
            for i in parts:
                tile_, half = i // halves, i % halves
                nc.vector.tensor_tensor(
                    out=unit["out"][:, tile_, half * UNIT : (half + 1) * UNIT], in0=unit["sums"][i][:],
                    in1=spread[:, unit["bias_row"] + half, :], op=ALU.add,
                )
                if half == halves - 1:
                    if unit["first_block"] is None:
                        store(unit, slice(tile_, tile_ + 1))
                    else:
                        for first_tile, end_tile in ((0, count),) if groups is None else groups:
                            if tile_ + 1 == end_tile:
                                rotate(nc.gpsimd, n, slice(first_tile, end_tile))

        def rotate(engine, n, tiles):
            unit = units[n]
            first_tile = unit["tiles"].start
            of_tokens = slice(first_tile + tiles.start, first_tile + tiles.stop)
            unit.setdefault("adds", []).append(
                rotate_products(
                    engine, scratch, unit["out"][:, tiles, :], unit["first_block"], cos_pair[:, of_tokens, :],
                    sin_minus[:, of_tokens, :], sin_plus[:, of_tokens, :],
                ) + (tiles,)
            )

        def finish(n, parts=None):
            adds = units[n]["adds"]
            for i in range(len(adds)) if parts is None else parts:
                pairs, straight, crossed, tiles = adds[i]
                nc.vector.tensor_tensor(out=pairs, in0=straight, in1=crossed, op=ALU.add)
                store(units[n], tiles)

        def regroup_upto(count, engine="scalar"):
            while len(regrouped) < count:
                regroup_next(engine)

        def quantise_upto(count):
            while len(quantised) < min(count, len(pieces)):
                if len(regrouped) <= len(quantised):
                    regroup_next()
                quantise_next()

        add_latent_bias(0)
        quantise_x(2)
        open_latent(2)
        multiply_latent(2, (0, 1, 2, 3))
        negate_mean(0)
        sum_squares(0)
        invert_std(0)
        add_latent_bias(1)
        quantise_x(3)
        open_latent(3)
        multiply_latent(3, (0, 1, 2, 3))
        negate_mean(1)
        sum_squares(1)
        invert_std(1)
        normalise(0)
        turn_cn(0)
        add_latent_bias(2)
        negate_mean(2)
        sum_squares(2)
        normalise(1)
        turn_cn(1)
        keep_warm(2, raw_wk[:, 0, :UNIT])
        add_latent_bias(3)
        regroup_half(0, "vector")
        scale_cn(0)
        invert_std(2)
        negate_mean(3)
        sum_squares(3)
        normalise(2)
        turn_cn(2)
        keep_warm(2, raw_wk[:, 1, :UNIT])
        regroup_half(1, "vector")
        scale_cn(1)
        invert_std(3)
        regroup_cn(0, "vector")
        scale_cn(2)
        quantise_next()
        quantise_cn(0)
        normalise(3)
        turn_cn(3)
        keep_warm(2, raw_wk[:, 2, :UNIT])
        regroup_cn(1, "vector")
        scale_cn(3)
        regroup_next("vector")
        quantise_cn(1)
        regroup_cn(2, "vector")
        quantise_next()
        quantise_cn(2)
        regroup_cn(3, "vector")
        regroup_next("scalar")
        quantise_cn(3)
        quantise_upto(2)
        multiply_unit(0)
        multiply_unit(1)
        drain(0)
        quantise_upto(4)
        multiply_unit(2)
        drain(1)
        multiply_unit(3)
        drain(2)
        drain(3)
        finish(0)
        finish(1)
        quantise_upto(8)
        multiply_unit(4)
        multiply_unit(5)
        drain(4)
        quantise_upto(10)
        multiply_unit(6)
        drain(5)
        multiply_unit(7)
        drain(6)
        finish(4)
        quantise_upto(13)
        multiply_unit(8)
        drain(7)
        multiply_unit(9)
        drain(8, groups=())
        finish(6)
        quantise_upto(15)
        multiply_unit(9)
        quantise_upto(16)
        multiply_unit(9)
        rotate(nc.vector, 8, slice(0, 4))
        finish(8)
        quantise_upto(16)
        multiply_unit(9)
        drain(9, groups=())
        rotate(nc.vector, 9, slice(0, 1))
        rotate(nc.vector, 9, slice(1, 2))
        finish(9, (0, 1))
        rotate(nc.vector, 9, slice(2, 3))
        rotate(nc.vector, 9, slice(3, 4))
        finish(9, (2, 3))
